import numpy as np
import ml_dtypes


def mxq(x, axis, fmt="e4m3"):
    dtype, down = {"e4m3": (ml_dtypes.float8_e4m3fn, 7), "e5m2": (ml_dtypes.float8_e5m2, 14)}[fmt]
    v = np.moveaxis(np.asarray(x, np.float32).astype(ml_dtypes.bfloat16).astype(np.float64), axis, -1)
    blocks = v.reshape(v.shape[:-1] + (-1, 32))
    amax = np.abs(blocks).max(-1, keepdims=True)
    byte = np.maximum(np.where(amax > 0, np.frexp(amax)[1] - 1 + 127, 0) - down, 1)
    scale = np.exp2(byte - 127.0)
    codes = (blocks / scale).astype(np.float32).astype(dtype).astype(np.float64)
    return np.moveaxis((codes * scale).reshape(v.shape), -1, axis)


WIDE = False


def mx_kscale(k):
    if not WIDE:
        return np.ones(k)
    levels = np.array([10, -10, 5, -5, 0])
    a = np.random.permutation(np.resize(levels, k // 512 * 4)).reshape(k // 512, 4)
    idx = np.arange(k)
    return np.exp2(a[idx // 512, idx % 128 // 32])


BF16 = ml_dtypes.bfloat16


def bf(x):
    return np.asarray(x, np.float32).astype(BF16)


def f64(x):
    return np.asarray(x).astype(np.float64)


B, C, CP, H, W, KW = 1, 512, 19, 96, 96, 7
PAD = KW // 2
BN_EPS = 1e-5


def pad_hw(v):
    return np.pad(v, ((0, 0), (0, 0), (PAD, PAD), (PAD, PAD)))


def setup_inputs():
    s, t = mx_kscale(C), mx_kscale(C)
    return {
        "x": bf(np.random.standard_normal((B, C, H, W))),
        "coarse_probs": bf(np.random.random((B, CP, H, W))),
        "sigma": bf(1.5 + 0.1 * np.random.standard_normal(1)),
        "w_feat": bf(np.random.standard_normal((C, C)) * 2.0 / np.sqrt(C) * t[:, None] / s[None, :]),
        "w_fuse": bf(np.random.standard_normal((C, C)) * 2.5 / np.sqrt(C) / t[None, :]),
        "bn_gamma": bf((1.0 + 0.1 * np.random.standard_normal(C)) * s),
        "bn_beta": bf(0.1 * np.random.standard_normal(C) * s),
        "bn_mean": bf(0.1 * np.random.standard_normal(C)),
        "bn_var": bf(np.random.random(C) + 0.5),
    }


def reference(x, coarse_probs, sigma, w_feat, w_fuse, bn_gamma, bn_beta, bn_mean, bn_var):
    x, p = f64(x), f64(coarse_probs)
    inv = 1.0 / np.sqrt(f64(bn_var) + BN_EPS)
    xn = (x - f64(bn_mean)[None, :, None, None]) * (inv * f64(bn_gamma))[None, :, None, None] + f64(bn_beta)[None, :, None, None]

    pp = pad_hw(p)
    dist_sq = np.stack([((pp[:, :, i:i + H, j:j + W] - p) ** 2).sum(axis=1) for i in range(KW) for j in range(KW)], axis=1)
    denom = 2.0 * np.maximum(f64(sigma)[0], 0.0) ** 2 + 1e-8
    a = np.exp(-dist_sq / denom)
    e = np.exp(a - a.max(axis=1, keepdims=True))
    affinity = e / e.sum(axis=1, keepdims=True)

    xq = mxq(xn, 1, "e4m3")
    messages = (mxq(f64(w_feat), 1, "e4m3") @ xq.reshape(B, C, H * W)).reshape(B, C, H, W)

    mp = pad_hw(messages)
    agg = np.zeros((B, C, H, W))
    for i in range(KW):
        for j in range(KW):
            agg = agg + mp[:, :, i:i + H, j:j + W] * affinity[:, i * KW + j][:, None]

    aq = mxq(agg, 1, "e4m3")
    refined = (mxq(f64(w_fuse), 1, "e4m3") @ aq.reshape(B, C, H * W)).reshape(B, C, H, W)
    return x + refined

@@ -1,0 +1,333 @@
+from contextlib import ExitStack
+
+import concourse.mybir as mybir
+from concourse.masks import make_identity
+
+F32 = mybir.dt.float32
+BF16 = mybir.dt.bfloat16
+I32 = mybir.dt.int32
+U32 = mybir.dt.uint32
+U8 = mybir.dt.uint8
+FP8X4 = mybir.dt.float8_e4m3fn_x4
+ALU = mybir.AluOpType
+ACT = mybir.ActivationFunctionType
+AX = mybir.AxisListType
+
+P = 128
+C = 512
+CP = 19
+H = 96
+W = 96
+KW = 7
+PAD = 3
+NOFF = KW * KW
+RB = 12
+CB = 6
+BH = H // RB
+BW = W // CB
+HR = RB + 2 * PAD
+HC = CB + 2 * PAD
+NPOS = RB * CB
+T = 4
+XLEN = PAD + BH * W + PAD
+XPITCH = 784
+ZP = W + 2 * PAD
+VECTOR = 0
+GPSIMD = 1
+ACC_ROWS = 8
+
+FLOPS = 2 * 2 * C * C * H * W + 2 * NOFF * C * H * W
+
+
+def tile_dcblock_t_kernel(
+    tc, x, coarse_probs, sigma, w_feat, w_fuse, bn_gamma, bn_beta, bn_mean, bn_var, out
+):
+    nc = tc.nc
+    with ExitStack() as ctx:
+        const = ctx.enter_context(tc.tile_pool(name="const", bufs=1))
+
+        ident_b = const.tile([P, P], BF16, name="ident_b")
+        make_identity(nc, ident_b[:])
+        ident_f = const.tile([P, P], F32, name="ident_f")
+        make_identity(nc, ident_f[:])
+
+        aff = const.tile([P, NOFF, NPOS], F32, name="aff")
+        w1q = const.tile([P, C], U32, name="w1q", align_bytes=64)
+        w1s = const.tile([P, C], U8, name="w1s", align_bytes=64)
+        w2q = const.tile([P, C], U32, name="w2q", align_bytes=64)
+        w2s = const.tile([P, C], U8, name="w2s", align_bytes=64)
+        bsc = const.tile([P, T], F32, name="bsc")
+        bbi = const.tile([P, T], F32, name="bbi")
+        neginv = const.tile([P, 1], F32, name="neginv")
+        negone = const.tile([P, 1], F32, name="negone")
+        sel = const.tile([P, CB], F32, name="sel")
+        valid = const.tile([P, HR, HC], F32, name="valid")
+        xr_tiles = [const.tile([P, T, XPITCH], BF16, name="xr%d" % k) for k in range(2)]
+        for k in range(2):
+            nc.vector.memset(xr_tiles[k][:], 0.0)
+        nc.vector.memset(negone[:], -1.0)
+
+        with tc.tile_pool(name="prep", bufs=1) as prep, tc.psum_pool(name="psw", bufs=1) as psw:
+            prm = prep.tile([P, P], BF16, name="prm")
+            nc.vector.memset(prm[:], 0.0)
+            for k, vec in enumerate((bn_gamma, bn_beta, bn_mean, bn_var)):
+                nc.sync.dma_start(out=prm[T * k : T * k + T, :], in_=vec.rearrange("(t p) -> t p", p=P))
+            prm_t = psw.tile([P, P], BF16, name="prm_t")
+            nc.tensor.transpose(prm_t[:], prm[:], ident_b[:])
+            pf = prep.tile([P, 4 * T], F32, name="pf")
+            nc.vector.tensor_copy(out=pf[:], in_=prm_t[:, 0 : 4 * T])
+            sd = prep.tile([P, T], F32, name="sd")
+            nc.vector.tensor_scalar(out=sd[:], in0=pf[:, 3 * T : 4 * T], scalar1=1e-5, scalar2=None, op0=ALU.add)
+            nc.scalar.activation(out=sd[:], in_=sd[:], func=ACT.Sqrt)
+            nc.vector.reciprocal(out=sd[:], in_=sd[:])
+            nc.vector.tensor_tensor(out=bsc[:], in0=sd[:], in1=pf[:, 0:T], op=ALU.mult)
+            ms = prep.tile([P, T], F32, name="ms")
+            nc.vector.tensor_tensor(out=ms[:], in0=pf[:, 2 * T : 3 * T], in1=bsc[:], op=ALU.mult)
+            nc.vector.tensor_tensor(out=bbi[:], in0=pf[:, T : 2 * T], in1=ms[:], op=ALU.subtract)
+
+            sg = prep.tile([P, 1], BF16, name="sg")
+            nc.sync.dma_start(out=sg[:], in_=sigma.partition_broadcast(P))
+            sf = prep.tile([P, 1], F32, name="sf")
+            nc.vector.tensor_scalar(out=sf[:], in0=sg[:], scalar1=0.0, scalar2=None, op0=ALU.max)
+            nc.vector.tensor_tensor(out=sf[:], in0=sf[:], in1=sf[:], op=ALU.mult)
+            nc.vector.tensor_scalar(out=sf[:], in0=sf[:], scalar1=2.0, scalar2=1e-8, op0=ALU.mult, op1=ALU.add)
+            nc.vector.reciprocal(out=sf[:], in_=sf[:])
+            nc.vector.tensor_scalar(out=neginv[:], in0=sf[:], scalar1=-1.0, scalar2=None, op0=ALU.mult)
+
+            for wi, (w_dram, wq, wsc) in enumerate(((w_feat, w1q, w1s), (w_fuse, w2q, w2s))):
+                w_sb = prep.tile([P, T, C], BF16, name="w_sb%d" % wi)
+                nc.sync.dma_start(out=w_sb[:], in_=w_dram.rearrange("(a p) c -> p a c", p=P))
+                w_gr = prep.tile([P, C, T], BF16, name="w_gr%d" % wi, align_bytes=64)
+                for a in range(T):
+                    w_t = psw.tile([P, T, P], BF16, name="w_t", bufs=2)
+                    for t in range(T):
+                        nc.tensor.transpose(w_t[:, t, :], w_sb[:, a, t * P : (t + 1) * P], ident_b[:])
+                    nc.vector.tensor_copy(
+                        out=w_gr[:, a * P : (a + 1) * P, :], in_=w_t[:].rearrange("p t o -> p o t")
+                    )
+                nc.vector.quantize_mx(
+                    out=wq[:].bitcast(FP8X4), scales=wsc[:], in_=w_gr[:].rearrange("p o t -> p (o t)")
+                )
+
+            pidx = prep.tile([P, 1], I32, name="pidx")
+            nc.gpsimd.iota(pidx[:], pattern=[[0, 1]], base=0, channel_multiplier=1)
+            bhi = prep.tile([P, 1], I32, name="bhi")
+            nc.vector.tensor_scalar(out=bhi[:], in0=pidx[:], scalar1=4, scalar2=None, op0=ALU.arith_shift_right)
+            bwi = prep.tile([P, 1], I32, name="bwi")
+            nc.vector.tensor_scalar(out=bwi[:], in0=pidx[:], scalar1=15, scalar2=None, op0=ALU.bitwise_and)
+            rowb = prep.tile([P, 1], F32, name="rowb")
+            nc.vector.tensor_copy(out=rowb[:], in_=bhi[:])
+            nc.vector.tensor_scalar(
+                out=rowb[:], in0=rowb[:], scalar1=float(RB), scalar2=float(-PAD), op0=ALU.mult, op1=ALU.add
+            )
+            colb = prep.tile([P, 1], F32, name="colb")
+            nc.vector.tensor_copy(out=colb[:], in_=bwi[:])
+            nc.vector.tensor_scalar(
+                out=colb[:], in0=colb[:], scalar1=float(CB), scalar2=float(-PAD), op0=ALU.mult, op1=ALU.add
+            )
+            cnt_i = prep.tile([P, HR], I32, name="cnt_i")
+            nc.gpsimd.iota(cnt_i[:], pattern=[[1, HR]], base=0, channel_multiplier=0)
+            cnt = prep.tile([P, HR], F32, name="cnt")
+            nc.vector.tensor_copy(out=cnt[:], in_=cnt_i[:])
+            vh = prep.tile([P, HR], F32, name="vh")
+            vh2 = prep.tile([P, HR], F32, name="vh2")
+            nc.vector.tensor_scalar(
+                out=vh[:], in0=cnt[:], scalar1=rowb[:, 0:1], scalar2=0.0, op0=ALU.add, op1=ALU.is_ge
+            )
+            nc.vector.tensor_scalar(
+                out=vh2[:], in0=cnt[:], scalar1=rowb[:, 0:1], scalar2=float(H - 1), op0=ALU.add, op1=ALU.is_le
+            )
+            nc.vector.tensor_tensor(out=vh[:], in0=vh[:], in1=vh2[:], op=ALU.mult)
+            vw = prep.tile([P, HC], F32, name="vw")
+            vw2 = prep.tile([P, HC], F32, name="vw2")
+            nc.vector.tensor_scalar(
+                out=vw[:], in0=cnt[:, 0:HC], scalar1=colb[:, 0:1], scalar2=0.0, op0=ALU.add, op1=ALU.is_ge
+            )
+            nc.vector.tensor_scalar(
+                out=vw2[:], in0=cnt[:, 0:HC], scalar1=colb[:, 0:1], scalar2=float(W - 1), op0=ALU.add, op1=ALU.is_le
+            )
+            nc.vector.tensor_tensor(out=vw[:], in0=vw[:], in1=vw2[:], op=ALU.mult)
+            nc.vector.tensor_tensor(
+                out=valid[:],
+                in0=vh[:].unsqueeze(2).to_broadcast([P, HR, HC]),
+                in1=vw[:].unsqueeze(1).to_broadcast([P, HR, HC]),
+                op=ALU.mult,
+            )
+            sel_i = prep.tile([P, CB], I32, name="sel_i")
+            nc.gpsimd.iota(sel_i[:], pattern=[[-CP, CB]], base=0, channel_multiplier=1)
+            sel_f = prep.tile([P, CB], F32, name="sel_f")
+            nc.vector.tensor_copy(out=sel_f[:], in_=sel_i[:])
+            sel2 = prep.tile([P, CB], F32, name="sel2")
+            nc.vector.tensor_scalar(out=sel[:], in0=sel_f[:], scalar1=0.0, scalar2=None, op0=ALU.is_ge)
+            nc.vector.tensor_scalar(out=sel2[:], in0=sel_f[:], scalar1=float(CP - 1), scalar2=None, op0=ALU.is_le)
+            nc.vector.tensor_tensor(out=sel[:], in0=sel[:], in1=sel2[:], op=ALU.mult)
+
+        with tc.tile_pool(name="affp", bufs=1) as affp, tc.psum_pool(name="psa", bufs=1) as psa:
+            nat = affp.tile([P, ZP, ZP], BF16, name="nat")
+            nc.vector.memset(nat[:], 0.0)
+            probs = coarse_probs[0]
+            for j in range(CB):
+                w0 = max(0, j - PAD)
+                z0 = w0 - j + PAD
+                for c0, c1 in ((0, 16), (16, CP)):
+                    nc.sync.dma_start(
+                        out=nat[CP * j + c0 : CP * j + c1, PAD : PAD + H, z0 : z0 + W - w0], in_=probs[c0:c1, :, w0:W]
+                    )
+            centre = nat[:, PAD : PAD + H, PAD : PAD + W : CB].rearrange("p (a i) b -> p i a b", i=RB)
+            e1 = affp.tile([P, NOFF, NPOS], F32, name="e1")
+            e2 = affp.tile([P, NOFF, NPOS], F32, name="e2")
+            for dhi in range(KW):
+                d2 = psa.tile([P, KW, RB, CB], F32, name="d2_%d" % dhi)
+                for dwi in range(KW):
+                    shifted = nat[:, dhi : dhi + H, dwi : dwi + W : CB].rearrange("p (a i) b -> p i a b", i=RB)
+                    diff = affp.tile([P, RB, BH, BW], F32, name="diff", bufs=2)
+                    nc.vector.tensor_tensor(out=diff[:], in0=shifted, in1=centre, op=ALU.subtract)
+                    sq = affp.tile([P, RB * P], F32, name="sq", bufs=2)
+                    nc.scalar.activation(out=sq[:], in_=diff[:].rearrange("p i a b -> p (i a b)"), func=ACT.Square)
+                    for i in range(RB):
+                        nc.tensor.matmul(
+                            out=d2[:, dwi, i, :], lhsT=sq[:, i * P : (i + 1) * P], rhs=sel[:], start=True, stop=True
+                        )
+                offs = slice(dhi * KW, (dhi + 1) * KW)
+                nc.scalar.activation(
+                    out=e1[:, offs, :], in_=d2[:].rearrange("p a i j -> p a (i j)"), func=ACT.Exp, scale=neginv[:, 0:1]
+                )
+                nc.scalar.activation(out=e2[:, offs, :], in_=e1[:, offs, :], func=ACT.Exp, bias=negone[:, 0:1])
+            ssum = affp.tile([P, NPOS], F32, name="ssum")
+            nc.vector.tensor_reduce(out=ssum[:], in_=e2[:].rearrange("p o q -> p q o"), axis=AX.X, op=ALU.add)
+            nc.vector.reciprocal(out=ssum[:], in_=ssum[:])
+            for dhi in range(KW):
+                for dwi in range(KW):
+                    o = dhi * KW + dwi
+                    nc.vector.tensor_tensor(
+                        out=e1[:, o, :].rearrange("p (i j) -> p i j", j=CB),
+                        in0=e2[:, o, :].rearrange("p (i j) -> p i j", j=CB),
+                        in1=valid[:, dhi : dhi + RB, dwi : dwi + CB],
+                        op=ALU.mult,
+                    )
+            nc.vector.tensor_tensor(
+                out=aff[:], in0=e1[:], in1=ssum[:].unsqueeze(1).to_broadcast([P, NOFF, NPOS]), op=ALU.mult
+            )
+
+        xs = ctx.enter_context(tc.tile_pool(name="xs", bufs=2))
+        accp = ctx.enter_context(tc.tile_pool(name="accp", bufs=ACC_ROWS * CB))
+        st2 = ctx.enter_context(tc.tile_pool(name="st2", bufs=2))
+        ps_v = ctx.enter_context(tc.psum_pool(name="ps_v", bufs=2))
+        ps_g = ctx.enter_context(tc.psum_pool(name="ps_g", bufs=2))
+        ps_t = ctx.enter_context(tc.psum_pool(name="ps_t", bufs=2))
+        ps_o = ctx.enter_context(tc.psum_pool(name="ps_o", bufs=2))
+
+        x_v = x[0].rearrange("(t p) (a r) w -> t p r a w", p=P, r=RB)
+        out_v = out[0].rearrange("(m p) (a r) w -> m p r a w", p=P, r=RB)
+        acc = {}
+
+        def second_conv(i):
+            x_res = st2.tile([P, T, BH * W], BF16, name="x_res", bufs=1)
+            for t in range(T):
+                nc.sync.dma_start(
+                    out=x_res[:, t, :].rearrange("p (a w) -> p a w", w=W), in_=x_v[t, :, i, :, :]
+                )
+            grp = st2.tile([P, BH * W, T], BF16, name="grp", align_bytes=64)
+            grp_v = grp[:].rearrange("p (k b) t -> p b k t", b=CB)
+            for j in range(CB):
+                a_t = ps_t.tile([P, T, P], F32, name="a_t")
+                for t in range(T):
+                    nc.tensor.transpose(a_t[:, t, :], acc[(i, j)][:, t * P : (t + 1) * P], ident_f[:])
+                nc.scalar.copy(out=grp_v[:, j], in_=a_t[:].rearrange("p t k -> p k t"))
+            aq = st2.tile([P, BH * W], U32, name="aq", align_bytes=64)
+            asc = st2.tile([P, BH * W], U8, name="asc", align_bytes=64)
+            grp_f = grp[:].rearrange("p k t -> p (k t)")
+            for c0, c1 in ((0, 512), (512, 768)):
+                nc.vector.quantize_mx(
+                    out=aq[:, c0:c1].bitcast(FP8X4), scales=asc[:, c0:c1], in_=grp_f[:, T * c0 : T * c1]
+                )
+            for m in range(T):
+                o_sb = st2.tile([P, BH * W], F32, name="o_sb")
+                for c0, c1 in ((0, 512), (512, 768)):
+                    o_ps = ps_o.tile([P, 512], F32, name="o_ps")
+                    nc.tensor.matmul_mx(
+                        out=o_ps[:, 0 : c1 - c0],
+                        lhsT=w2q[:, m * P : (m + 1) * P].bitcast(FP8X4),
+                        lhsT_scale=w2s[:, m * P : (m + 1) * P],
+                        rhs=aq[:, c0:c1].bitcast(FP8X4),
+                        rhs_scale=asc[:, c0:c1],
+                        start=True,
+                        stop=True,
+                    )
+                    nc.vector.tensor_tensor(
+                        out=o_sb[:, c0:c1], in0=o_ps[:, 0 : c1 - c0], in1=x_res[:, m, c0:c1], op=ALU.add
+                    )
+                nc.sync.dma_start(out=out_v[m, :, i, :, :], in_=o_sb[:].rearrange("p (a w) -> p a w", w=W))
+
+        for ip in range(HR):
+            hrow = ip - PAD
+            r = hrow % RB
+            shift = (hrow - r) // RB
+            a_lo = max(0, -shift)
+            a_hi = min(BH, BH - shift)
+            xr = xr_tiles[ip % 2]
+            for t in range(T):
+                nc.sync.dma_start(
+                    out=xr[:, t, PAD + a_lo * W : PAD + a_hi * W].rearrange("p (a w) -> p a w", w=W),
+                    in_=x_v[t, :, r, a_lo + shift : a_hi + shift, :],
+                )
+            xn = xs.tile([P, T, XLEN], BF16, name="xn")
+            for t in range(T):
+                nc.scalar.activation(
+                    out=xn[:, t, :], in_=xr[:, t, 0:XLEN], func=ACT.Identity, scale=bsc[:, t : t + 1], bias=bbi[:, t : t + 1]
+                )
+            halves = [xn[:, :, CB * a : CB * a + P * CB].rearrange("p t (k b) -> p b k t", b=CB) for a in range(2)]
+            for q in range(HC // 4):
+                xg = xs.tile([P, 4, P, T], BF16, name="xg", bufs=3, align_bytes=64)
+                for a in range(2):
+                    lo = max(4 * q, CB * a)
+                    hi = min(4 * q + 4, CB * a + CB)
+                    if lo < hi:
+                        nc.scalar.copy(out=xg[:, lo - 4 * q : hi - 4 * q], in_=halves[a][:, lo - CB * a : hi - CB * a])
+                xq = xs.tile([P, 4 * P], U32, name="xq", bufs=3, align_bytes=64)
+                xsc = xs.tile([P, 4 * P], U8, name="xsc", bufs=3, align_bytes=64)
+                nc.vector.quantize_mx(
+                    out=xq[:].bitcast(FP8X4), scales=xsc[:], in_=xg[:].rearrange("p b k t -> p (b k t)")
+                )
+                for jl in range(4):
+                    jp = 4 * q + jl
+                    rows = range(max(0, ip - 2 * PAD), min(RB - 1, ip) + 1)
+                    cols = range(max(0, jp - 2 * PAD), min(CB - 1, jp) + 1)
+                    for owner, pool in ((VECTOR, ps_v), (GPSIMD, ps_g)):
+                        mine = [(i, j) for i in rows for j in cols if ((i + j) % 3 == 2) == (owner == GPSIMD)]
+                        if not mine:
+                            continue
+                        msg = pool.tile([P, C], F32, name="msg")
+                        nc.tensor.matmul_mx(
+                            out=msg[:],
+                            lhsT=xq[:, jl * P : (jl + 1) * P].bitcast(FP8X4),
+                            lhsT_scale=xsc[:, jl * P : (jl + 1) * P],
+                            rhs=w1q[:].bitcast(FP8X4),
+                            rhs_scale=w1s[:],
+                            start=True,
+                            stop=True,
+                        )
+                        for i, j in mine:
+                            o = (ip - i) * KW + (jp - j)
+                            wgt = aff[:, o, i * CB + j : i * CB + j + 1]
+                            first = ip == i and jp == j
+                            if first:
+                                acc[(i, j)] = accp.tile([P, C], F32, name="acc")
+                            dst = acc[(i, j)]
+                            if owner == VECTOR:
+                                if first:
+                                    nc.vector.tensor_scalar(
+                                        out=dst[:], in0=msg[:], scalar1=wgt, scalar2=None, op0=ALU.mult
+                                    )
+                                else:
+                                    nc.vector.scalar_tensor_tensor(
+                                        out=dst[:], in0=msg[:], scalar=wgt, in1=dst[:], op0=ALU.mult, op1=ALU.add
+                                    )
+                            elif first:
+                                nc.scalar.activation(out=dst[:], in_=msg[:], func=ACT.Copy, scale=wgt)
+                            else:
+                                prod = xs.tile([P, C], F32, name="prod", bufs=4)
+                                nc.scalar.activation(out=prod[:], in_=msg[:], func=ACT.Copy, scale=wgt)
+                                nc.gpsimd.tensor_tensor(out=dst[:], in0=dst[:], in1=prod[:], op=ALU.add)
+            if ip >= 2 * PAD:
+                second_conv(ip - 2 * PAD)

@@ -1,4 +1,5 @@
 from contextlib import ExitStack
+from functools import partial
 
 import concourse.mybir as mybir
 from concourse.masks import make_identity
@@ -20,23 +21,26 @@ H = 96
 W = 96
 KW = 7
 PAD = 3
-NOFF = KW * KW
-RB = 12
-CB = 6
+RB = 24
+CB = 3
 BH = H // RB
 BW = W // CB
 HR = RB + 2 * PAD
 HC = CB + 2 * PAD
-NPOS = RB * CB
 T = 4
-XLEN = PAD + BH * W + PAD
-XPITCH = 784
+ROWPX = BH * W
+XLEN = PAD + ROWPX + PAD
+XPITCH = 400
+NROWS = 120
 ZP = W + 2 * PAD
-VECTOR = 0
-GPSIMD = 1
-ACC_ROWS = 8
+NPAIR = RB // 2
+AFFW = KW * 2 * KW * CB
+VCOL = 1
+PE_COLS = (0, 2)
+COST_S = 0.47
+COST_G = 0.62
 
-FLOPS = 2 * 2 * C * C * H * W + 2 * NOFF * C * H * W
+FLOPS = 2 * 2 * C * C * H * W + 2 * KW * KW * C * H * W
 
 
 def tile_dcblock_t_kernel(
@@ -51,7 +55,7 @@ def tile_dcblock_t_kernel(
         ident_f = const.tile([P, P], F32, name="ident_f")
         make_identity(nc, ident_f[:])
 
-        aff = const.tile([P, NOFF, NPOS], F32, name="aff")
+        aff = const.tile([P, NPAIR, KW, KW, 2, CB], F32, name="aff")
         w1q = const.tile([P, C], U32, name="w1q", align_bytes=64)
         w1s = const.tile([P, C], U8, name="w1s", align_bytes=64)
         w2q = const.tile([P, C], U32, name="w2q", align_bytes=64)
@@ -60,12 +64,24 @@ def tile_dcblock_t_kernel(
         bbi = const.tile([P, T], F32, name="bbi")
         neginv = const.tile([P, 1], F32, name="neginv")
         negone = const.tile([P, 1], F32, name="negone")
-        sel = const.tile([P, CB], F32, name="sel")
-        valid = const.tile([P, HR, HC], F32, name="valid")
+        sel = const.tile([P, 2 * CB], F32, name="sel")
+        vhh = const.tile([P, NPAIR, KW, 2], F32, name="vhh")
+        vww = const.tile([P, KW, 2, CB], F32, name="vww")
+        nat = const.tile([P, NROWS, ZP], BF16, name="nat")
         xr_tiles = [const.tile([P, T, XPITCH], BF16, name="xr%d" % k) for k in range(2)]
+        nc.vector.memset(nat[:], 0.0)
         for k in range(2):
             nc.vector.memset(xr_tiles[k][:], 0.0)
         nc.vector.memset(negone[:], -1.0)
+        probs = coarse_probs[0]
+        for s in range(2):
+            for j in range(CB):
+                g = s * CB + j
+                for c0, c1 in ((0, 16), (16, CP)):
+                    nc.sync.dma_start(
+                        out=nat[CP * g + c0 : CP * g + c1, PAD - s : PAD - s + H, PAD - j : PAD - j + W],
+                        in_=probs[c0:c1, :, :],
+                    )
 
         with tc.tile_pool(name="prep", bufs=1) as prep, tc.psum_pool(name="psw", bufs=1) as psw:
             prm = prep.tile([P, P], BF16, name="prm")
@@ -94,27 +110,12 @@ def tile_dcblock_t_kernel(
             nc.vector.reciprocal(out=sf[:], in_=sf[:])
             nc.vector.tensor_scalar(out=neginv[:], in0=sf[:], scalar1=-1.0, scalar2=None, op0=ALU.mult)
 
-            for wi, (w_dram, wq, wsc) in enumerate(((w_feat, w1q, w1s), (w_fuse, w2q, w2s))):
-                w_sb = prep.tile([P, T, C], BF16, name="w_sb%d" % wi)
-                nc.sync.dma_start(out=w_sb[:], in_=w_dram.rearrange("(a p) c -> p a c", p=P))
-                w_gr = prep.tile([P, C, T], BF16, name="w_gr%d" % wi, align_bytes=64)
-                for a in range(T):
-                    w_t = psw.tile([P, T, P], BF16, name="w_t", bufs=2)
-                    for t in range(T):
-                        nc.tensor.transpose(w_t[:, t, :], w_sb[:, a, t * P : (t + 1) * P], ident_b[:])
-                    nc.vector.tensor_copy(
-                        out=w_gr[:, a * P : (a + 1) * P, :], in_=w_t[:].rearrange("p t o -> p o t")
-                    )
-                nc.vector.quantize_mx(
-                    out=wq[:].bitcast(FP8X4), scales=wsc[:], in_=w_gr[:].rearrange("p o t -> p (o t)")
-                )
-
             pidx = prep.tile([P, 1], I32, name="pidx")
             nc.gpsimd.iota(pidx[:], pattern=[[0, 1]], base=0, channel_multiplier=1)
             bhi = prep.tile([P, 1], I32, name="bhi")
-            nc.vector.tensor_scalar(out=bhi[:], in0=pidx[:], scalar1=4, scalar2=None, op0=ALU.arith_shift_right)
+            nc.vector.tensor_scalar(out=bhi[:], in0=pidx[:], scalar1=5, scalar2=None, op0=ALU.arith_shift_right)
             bwi = prep.tile([P, 1], I32, name="bwi")
-            nc.vector.tensor_scalar(out=bwi[:], in0=pidx[:], scalar1=15, scalar2=None, op0=ALU.bitwise_and)
+            nc.vector.tensor_scalar(out=bwi[:], in0=pidx[:], scalar1=BW - 1, scalar2=None, op0=ALU.bitwise_and)
             rowb = prep.tile([P, 1], F32, name="rowb")
             nc.vector.tensor_copy(out=rowb[:], in_=bhi[:])
             nc.vector.tensor_scalar(
@@ -147,119 +148,113 @@ def tile_dcblock_t_kernel(
                 out=vw2[:], in0=cnt[:, 0:HC], scalar1=colb[:, 0:1], scalar2=float(W - 1), op0=ALU.add, op1=ALU.is_le
             )
             nc.vector.tensor_tensor(out=vw[:], in0=vw[:], in1=vw2[:], op=ALU.mult)
-            nc.vector.tensor_tensor(
-                out=valid[:],
-                in0=vh[:].unsqueeze(2).to_broadcast([P, HR, HC]),
-                in1=vw[:].unsqueeze(1).to_broadcast([P, HR, HC]),
-                op=ALU.mult,
-            )
-            sel_i = prep.tile([P, CB], I32, name="sel_i")
-            nc.gpsimd.iota(sel_i[:], pattern=[[-CP, CB]], base=0, channel_multiplier=1)
-            sel_f = prep.tile([P, CB], F32, name="sel_f")
+            for dhi in range(KW):
+                for s in range(2):
+                    nc.vector.tensor_copy(out=vhh[:, :, dhi, s], in_=vh[:, dhi + s : dhi + s + RB - 1 : 2])
+            for dwi in range(KW):
+                for s in range(2):
+                    nc.vector.tensor_copy(out=vww[:, dwi, s, :], in_=vw[:, dwi : dwi + CB])
+            sel_i = prep.tile([P, 2 * CB], I32, name="sel_i")
+            nc.gpsimd.iota(sel_i[:], pattern=[[-CP, 2 * CB]], base=0, channel_multiplier=1)
+            sel_f = prep.tile([P, 2 * CB], F32, name="sel_f")
             nc.vector.tensor_copy(out=sel_f[:], in_=sel_i[:])
-            sel2 = prep.tile([P, CB], F32, name="sel2")
+            sel2 = prep.tile([P, 2 * CB], F32, name="sel2")
             nc.vector.tensor_scalar(out=sel[:], in0=sel_f[:], scalar1=0.0, scalar2=None, op0=ALU.is_ge)
             nc.vector.tensor_scalar(out=sel2[:], in0=sel_f[:], scalar1=float(CP - 1), scalar2=None, op0=ALU.is_le)
             nc.vector.tensor_tensor(out=sel[:], in0=sel[:], in1=sel2[:], op=ALU.mult)
 
-        with tc.tile_pool(name="affp", bufs=1) as affp, tc.psum_pool(name="psa", bufs=1) as psa:
-            nat = affp.tile([P, ZP, ZP], BF16, name="nat")
-            nc.vector.memset(nat[:], 0.0)
-            probs = coarse_probs[0]
-            for j in range(CB):
-                w0 = max(0, j - PAD)
-                z0 = w0 - j + PAD
-                for c0, c1 in ((0, 16), (16, CP)):
-                    nc.sync.dma_start(
-                        out=nat[CP * j + c0 : CP * j + c1, PAD : PAD + H, z0 : z0 + W - w0], in_=probs[c0:c1, :, w0:W]
+            for wi, (w_dram, wq, wsc) in enumerate(((w_feat, w1q, w1s), (w_fuse, w2q, w2s))):
+                w_sb = prep.tile([P, T, C], BF16, name="w_sb%d" % wi)
+                nc.sync.dma_start(out=w_sb[:], in_=w_dram.rearrange("(a p) c -> p a c", p=P))
+                w_gr = prep.tile([P, C, T], BF16, name="w_gr%d" % wi, align_bytes=64)
+                for a in range(T):
+                    w_t = psw.tile([P, T, P], BF16, name="w_t", bufs=2)
+                    for t in range(T):
+                        nc.tensor.transpose(w_t[:, t, :], w_sb[:, a, t * P : (t + 1) * P], ident_b[:])
+                    nc.vector.tensor_copy(
+                        out=w_gr[:, a * P : (a + 1) * P, :], in_=w_t[:].rearrange("p t o -> p o t")
                     )
-            centre = nat[:, PAD : PAD + H, PAD : PAD + W : CB].rearrange("p (a i) b -> p i a b", i=RB)
-            e1 = affp.tile([P, NOFF, NPOS], F32, name="e1")
-            e2 = affp.tile([P, NOFF, NPOS], F32, name="e2")
-            for dhi in range(KW):
-                d2 = psa.tile([P, KW, RB, CB], F32, name="d2_%d" % dhi)
-                for dwi in range(KW):
-                    shifted = nat[:, dhi : dhi + H, dwi : dwi + W : CB].rearrange("p (a i) b -> p i a b", i=RB)
-                    diff = affp.tile([P, RB, BH, BW], F32, name="diff", bufs=2)
-                    nc.vector.tensor_tensor(out=diff[:], in0=shifted, in1=centre, op=ALU.subtract)
-                    sq = affp.tile([P, RB * P], F32, name="sq", bufs=2)
-                    nc.scalar.activation(out=sq[:], in_=diff[:].rearrange("p i a b -> p (i a b)"), func=ACT.Square)
-                    for i in range(RB):
-                        nc.tensor.matmul(
-                            out=d2[:, dwi, i, :], lhsT=sq[:, i * P : (i + 1) * P], rhs=sel[:], start=True, stop=True
-                        )
-                offs = slice(dhi * KW, (dhi + 1) * KW)
-                nc.scalar.activation(
-                    out=e1[:, offs, :], in_=d2[:].rearrange("p a i j -> p a (i j)"), func=ACT.Exp, scale=neginv[:, 0:1]
+                nc.vector.quantize_mx(
+                    out=wq[:].bitcast(FP8X4), scales=wsc[:], in_=w_gr[:].rearrange("p o t -> p (o t)")
                 )
-                nc.scalar.activation(out=e2[:, offs, :], in_=e1[:, offs, :], func=ACT.Exp, bias=negone[:, 0:1])
-            ssum = affp.tile([P, NPOS], F32, name="ssum")
-            nc.vector.tensor_reduce(out=ssum[:], in_=e2[:].rearrange("p o q -> p q o"), axis=AX.X, op=ALU.add)
-            nc.vector.reciprocal(out=ssum[:], in_=ssum[:])
-            for dhi in range(KW):
-                for dwi in range(KW):
-                    o = dhi * KW + dwi
-                    nc.vector.tensor_tensor(
-                        out=e1[:, o, :].rearrange("p (i j) -> p i j", j=CB),
-                        in0=e2[:, o, :].rearrange("p (i j) -> p i j", j=CB),
-                        in1=valid[:, dhi : dhi + RB, dwi : dwi + CB],
-                        op=ALU.mult,
-                    )
-            nc.vector.tensor_tensor(
-                out=aff[:], in0=e1[:], in1=ssum[:].unsqueeze(1).to_broadcast([P, NOFF, NPOS]), op=ALU.mult
-            )
 
+        affp = ctx.enter_context(tc.tile_pool(name="affp", bufs=2))
         xs = ctx.enter_context(tc.tile_pool(name="xs", bufs=2))
-        accp = ctx.enter_context(tc.tile_pool(name="accp", bufs=ACC_ROWS * CB))
+        msgp = ctx.enter_context(tc.tile_pool(name="msgp", bufs=14))
+        prodp = ctx.enter_context(tc.tile_pool(name="prodp", bufs=3))
+        accp = ctx.enter_context(tc.tile_pool(name="accp", bufs=8 * CB))
         st2 = ctx.enter_context(tc.tile_pool(name="st2", bufs=2))
         ps_v = ctx.enter_context(tc.psum_pool(name="ps_v", bufs=2))
-        ps_g = ctx.enter_context(tc.psum_pool(name="ps_g", bufs=2))
-        ps_t = ctx.enter_context(tc.psum_pool(name="ps_t", bufs=2))
-        ps_o = ctx.enter_context(tc.psum_pool(name="ps_o", bufs=2))
+        ps_s = ctx.enter_context(tc.psum_pool(name="ps_s", bufs=2))
+        ps_a = ctx.enter_context(tc.psum_pool(name="ps_a", bufs=2))
+        ps_m = ctx.enter_context(tc.psum_pool(name="ps_m", bufs=2))
 
         x_v = x[0].rearrange("(t p) (a r) w -> t p r a w", p=P, r=RB)
         out_v = out[0].rearrange("(m p) (a r) w -> m p r a w", p=P, r=RB)
         acc = {}
+        xq_of = {}
+        msgs = {}
+        e_of = {}
+        clock = {"s": 0.0, "g": 0.0}
 
-        def second_conv(i):
-            x_res = st2.tile([P, T, BH * W], BF16, name="x_res", bufs=1)
-            for t in range(T):
-                nc.sync.dma_start(
-                    out=x_res[:, t, :].rearrange("p (a w) -> p a w", w=W), in_=x_v[t, :, i, :, :]
+        def aff_diff(k, dwi):
+            if dwi == 0:
+                e_of[k] = ps_m.tile([P, KW, KW, 2 * CB], F32, name="d2", tag="misc")
+            d2 = e_of[k]
+            shifted = nat[:, 2 * k : 2 * k + H, dwi : dwi + W : CB].rearrange("p (a r) b -> p r a b", r=RB)[:, 0:KW]
+            centre = nat[:, 2 * k + PAD : 2 * k + PAD + (BH - 1) * RB + 1 : RB, PAD : PAD + W : CB]
+            diff = affp.tile([P, KW, BH, BW], F32, name="diff")
+            nc.vector.tensor_tensor(
+                out=diff[:], in0=shifted, in1=centre.unsqueeze(1).to_broadcast([P, KW, BH, BW]), op=ALU.subtract
+            )
+            sq = affp.tile([P, KW * P], F32, name="sq")
+            nc.scalar.activation(out=sq[:], in_=diff[:].rearrange("p r a b -> p (r a b)"), func=ACT.Square)
+            clock["s"] += 0.8
+            for dhi in range(KW):
+                nc.tensor.matmul(
+                    out=d2[:, dhi, dwi, :], lhsT=sq[:, dhi * P : (dhi + 1) * P], rhs=sel[:], start=True, stop=True
                 )
-            grp = st2.tile([P, BH * W, T], BF16, name="grp", align_bytes=64)
-            grp_v = grp[:].rearrange("p (k b) t -> p b k t", b=CB)
-            for j in range(CB):
-                a_t = ps_t.tile([P, T, P], F32, name="a_t")
-                for t in range(T):
-                    nc.tensor.transpose(a_t[:, t, :], acc[(i, j)][:, t * P : (t + 1) * P], ident_f[:])
-                nc.scalar.copy(out=grp_v[:, j], in_=a_t[:].rearrange("p t k -> p k t"))
-            aq = st2.tile([P, BH * W], U32, name="aq", align_bytes=64)
-            asc = st2.tile([P, BH * W], U8, name="asc", align_bytes=64)
-            grp_f = grp[:].rearrange("p k t -> p (k t)")
-            for c0, c1 in ((0, 512), (512, 768)):
-                nc.vector.quantize_mx(
-                    out=aq[:, c0:c1].bitcast(FP8X4), scales=asc[:, c0:c1], in_=grp_f[:, T * c0 : T * c1]
-                )
-            for m in range(T):
-                o_sb = st2.tile([P, BH * W], F32, name="o_sb")
-                for c0, c1 in ((0, 512), (512, 768)):
-                    o_ps = ps_o.tile([P, 512], F32, name="o_ps")
-                    nc.tensor.matmul_mx(
-                        out=o_ps[:, 0 : c1 - c0],
-                        lhsT=w2q[:, m * P : (m + 1) * P].bitcast(FP8X4),
-                        lhsT_scale=w2s[:, m * P : (m + 1) * P],
-                        rhs=aq[:, c0:c1].bitcast(FP8X4),
-                        rhs_scale=asc[:, c0:c1],
-                        start=True,
-                        stop=True,
-                    )
-                    nc.vector.tensor_tensor(
-                        out=o_sb[:, c0:c1], in0=o_ps[:, 0 : c1 - c0], in1=x_res[:, m, c0:c1], op=ALU.add
-                    )
-                nc.sync.dma_start(out=out_v[m, :, i, :, :], in_=o_sb[:].rearrange("p (a w) -> p a w", w=W))
 
-        for ip in range(HR):
+        def aff_exp(k):
+            d2 = e_of[k]
+            e1 = affp.tile([P, AFFW], F32, name="e1")
+            nc.scalar.activation(
+                out=e1[:], in_=d2[:].rearrange("p h w g -> p (h w g)"), func=ACT.Exp, scale=neginv[:, 0:1]
+            )
+            e2 = affp.tile([P, KW, KW, 2, CB], F32, name="e2")
+            nc.scalar.activation(
+                out=e2[:].rearrange("p h w s j -> p (h w s j)"), in_=e1[:], func=ACT.Exp, bias=negone[:, 0:1]
+            )
+            clock["s"] += 0.6
+            e_of[k] = e2
+
+        def aff_norm(k):
+            e2 = e_of[k]
+            ssum = affp.tile([P, 2, CB], F32, name="ssum")
+            nc.vector.tensor_reduce(out=ssum[:], in_=e2[:].rearrange("p h w s j -> p s j (h w)"), axis=AX.X, op=ALU.add)
+            nc.vector.reciprocal(out=ssum[:], in_=ssum[:])
+            em = affp.tile([P, KW, KW, 2, CB], F32, name="em")
+            nc.vector.tensor_tensor(
+                out=em[:].rearrange("p h w s j -> p h (w s j)"),
+                in0=e2[:].rearrange("p h w s j -> p h (w s j)"),
+                in1=vww[:].rearrange("p w s j -> p (w s j)").unsqueeze(1).to_broadcast([P, KW, KW * 2 * CB]),
+                op=ALU.mult,
+            )
+            for s in range(2):
+                for j in range(CB):
+                    nc.vector.scalar_tensor_tensor(
+                        out=aff[:, k, :, :, s, j],
+                        in0=em[:, :, :, s, j],
+                        scalar=ssum[:, s, j : j + 1],
+                        in1=vhh[:, k, :, s].unsqueeze(2).to_broadcast([P, KW, KW]),
+                        op0=ALU.mult,
+                        op1=ALU.mult,
+                    )
+
+        def aff_head(k):
+            return [partial(aff_diff, k, dwi) for dwi in range(KW)] + [partial(aff_exp, k)]
+
+        def x_load(ip):
             hrow = ip - PAD
             r = hrow % RB
             shift = (hrow - r) // RB
@@ -271,63 +266,193 @@ def tile_dcblock_t_kernel(
                     out=xr[:, t, PAD + a_lo * W : PAD + a_hi * W].rearrange("p (a w) -> p a w", w=W),
                     in_=x_v[t, :, r, a_lo + shift : a_hi + shift, :],
                 )
+
+        def x_norm(ip):
+            xr = xr_tiles[ip % 2]
             xn = xs.tile([P, T, XLEN], BF16, name="xn")
             for t in range(T):
                 nc.scalar.activation(
-                    out=xn[:, t, :], in_=xr[:, t, 0:XLEN], func=ACT.Identity, scale=bsc[:, t : t + 1], bias=bbi[:, t : t + 1]
+                    out=xn[:, t, :],
+                    in_=xr[:, t, 0:XLEN],
+                    func=ACT.Identity,
+                    scale=bsc[:, t : t + 1],
+                    bias=bbi[:, t : t + 1],
                 )
-            halves = [xn[:, :, CB * a : CB * a + P * CB].rearrange("p t (k b) -> p b k t", b=CB) for a in range(2)]
-            for q in range(HC // 4):
-                xg = xs.tile([P, 4, P, T], BF16, name="xg", bufs=3, align_bytes=64)
-                for a in range(2):
-                    lo = max(4 * q, CB * a)
-                    hi = min(4 * q + 4, CB * a + CB)
-                    if lo < hi:
-                        nc.scalar.copy(out=xg[:, lo - 4 * q : hi - 4 * q], in_=halves[a][:, lo - CB * a : hi - CB * a])
-                xq = xs.tile([P, 4 * P], U32, name="xq", bufs=3, align_bytes=64)
-                xsc = xs.tile([P, 4 * P], U8, name="xsc", bufs=3, align_bytes=64)
+            clock["s"] += 1.6
+            xq_of[ip] = xn
+
+        def x_group(ip):
+            xn = xq_of[ip]
+            xg = xs.tile([P, HC, P, T], BF16, name="xg", align_bytes=64)
+            for u in range(HC // CB):
+                nc.scalar.copy(
+                    out=xg[:, CB * u : CB * u + CB],
+                    in_=xn[:, :, CB * u : CB * u + ROWPX].rearrange("p t (k b) -> p b k t", b=CB),
+                )
+            clock["s"] += 4.5
+            xq_of[ip] = xg
+
+        def x_quant(ip):
+            xg = xq_of[ip][:].rearrange("p b k t -> p (b k t)")
+            xq = xs.tile([P, HC * P], U32, name="xq", align_bytes=64)
+            xsc = xs.tile([P, HC * P], U8, name="xsc", align_bytes=64)
+            for c0, c1 in ((0, 8 * P), (8 * P, 9 * P)):
+                nc.vector.quantize_mx(out=xq[:, c0:c1].bitcast(FP8X4), scales=xsc[:, c0:c1], in_=xg[:, T * c0 : T * c1])
+            xq_of[ip] = (xq, xsc)
+
+        def first_conv(ip, jp, pool):
+            xq, xsc = xq_of[ip]
+            msg = pool.tile([P, C], F32, name="msg")
+            nc.tensor.matmul_mx(
+                out=msg[:],
+                lhsT=xq[:, jp * P : (jp + 1) * P].bitcast(FP8X4),
+                lhsT_scale=xsc[:, jp * P : (jp + 1) * P],
+                rhs=w1q[:].bitcast(FP8X4),
+                rhs_scale=w1s[:],
+                start=True,
+                stop=True,
+            )
+            return msg
+
+        def msg_copy(ip, jp):
+            msg = first_conv(ip, jp, ps_s)
+            m_sb = msgp.tile([P, C], F32, name="m_sb")
+            nc.scalar.copy(out=m_sb[:], in_=msg[:])
+            clock["s"] += 0.45
+            msgs[(ip, jp)] = m_sb
+
+        def x_chores(ip):
+            return [partial(f, ip) for f in (x_load, x_norm, x_group, x_quant)] + [
+                partial(msg_copy, ip, jp) for jp in range(HC)
+            ]
+
+        def weight(ip, jp, i, j):
+            return aff[:, i // 2, ip - i, jp - j, i % 2, j : j + 1]
+
+        def vector_job(ip, jp, rows):
+            msg = first_conv(ip, jp, ps_v)
+            for i in rows:
+                wgt = weight(ip, jp, i, VCOL)
+                if ip == i and jp == VCOL:
+                    acc[(i, VCOL)] = accp.tile([P, C], F32, name="acc")
+                    nc.vector.tensor_scalar(out=acc[(i, VCOL)][:], in0=msg[:], scalar1=wgt, scalar2=None, op0=ALU.mult)
+                else:
+                    dst = acc[(i, VCOL)]
+                    nc.vector.scalar_tensor_tensor(
+                        out=dst[:], in0=msg[:], scalar=wgt, in1=dst[:], op0=ALU.mult, op1=ALU.add
+                    )
+
+        def group(ip, i, j):
+            part = ps_a.tile([P, T, P], F32, name="part")
+            for dwi in range(KW):
+                src = msgs[(ip, j + dwi)]
+                wgt = weight(ip, j + dwi, i, j)
+                if clock["s"] + COST_S <= clock["g"] + COST_G:
+                    prod = prodp.tile([P, C], F32, name="prod_s")
+                    nc.scalar.activation(out=prod[:], in_=src[:], func=ACT.Copy, scale=wgt)
+                    clock["s"] += COST_S
+                else:
+                    prod = prodp.tile([P, C], F32, name="prod_g")
+                    nc.gpsimd.tensor_scalar(
+                        out=prod[:], in0=src[:], scalar1=wgt, scalar2=0.0, op0=ALU.mult, op1=ALU.add
+                    )
+                    clock["g"] += COST_G
+                for t in range(T):
+                    nc.tensor.matmul(
+                        out=part[:, t, :],
+                        lhsT=prod[:, t * P : (t + 1) * P],
+                        rhs=ident_f[:],
+                        is_transpose=True,
+                        start=(dwi == 0 and t == 0),
+                        stop=(dwi == KW - 1 and t == T - 1),
+                    )
+            return part
+
+        def join(ip, i, j, part):
+            flat = part[:].rearrange("p t k -> p (t k)")
+            if ip == i:
+                acc[(i, j)] = accp.tile([P, C], F32, name="acc")
+                nc.vector.tensor_copy(out=acc[(i, j)][:], in_=flat)
+            else:
+                dst = acc[(i, j)]
+                nc.vector.tensor_tensor(out=dst[:], in0=flat, in1=dst[:], op=ALU.add)
+
+        st = {}
+
+        def conv2_gather(i):
+            x_res = st2.tile([P, T, ROWPX], BF16, name="x_res")
+            for t in range(T):
+                nc.sync.dma_start(out=x_res[:, t, :].rearrange("p (a w) -> p a w", w=W), in_=x_v[t, :, i, :, :])
+            grp = st2.tile([P, ROWPX, T], BF16, name="grp", align_bytes=64)
+            grp_v = grp[:].rearrange("p (k b) t -> p b k t", b=CB)
+            for j in range(CB):
+                if j == VCOL:
+                    a_t = ps_m.tile([P, T, P], F32, name="a_t", tag="misc")
+                    for t in range(T):
+                        nc.tensor.transpose(a_t[:, t, :], acc[(i, j)][:, t * P : (t + 1) * P], ident_f[:])
+                    src = a_t[:]
+                else:
+                    src = acc[(i, j)][:].rearrange("p (t k) -> p t k", t=T)
+                nc.scalar.copy(out=grp_v[:, j], in_=src.rearrange("p t k -> p k t"))
+                clock["s"] += 0.65
+            st["x_res"] = x_res
+            st["grp"] = grp
+
+        def conv2_quant(i):
+            aq = st2.tile([P, ROWPX], U32, name="aq", align_bytes=64)
+            asc = st2.tile([P, ROWPX], U8, name="asc", align_bytes=64)
+            grp_f = st["grp"][:].rearrange("p k t -> p (k t)")
+            for c0, c1 in ((0, 256), (256, 384)):
                 nc.vector.quantize_mx(
-                    out=xq[:].bitcast(FP8X4), scales=xsc[:], in_=xg[:].rearrange("p b k t -> p (b k t)")
+                    out=aq[:, c0:c1].bitcast(FP8X4), scales=asc[:, c0:c1], in_=grp_f[:, T * c0 : T * c1]
                 )
-                for jl in range(4):
-                    jp = 4 * q + jl
-                    rows = range(max(0, ip - 2 * PAD), min(RB - 1, ip) + 1)
-                    cols = range(max(0, jp - 2 * PAD), min(CB - 1, jp) + 1)
-                    for owner, pool in ((VECTOR, ps_v), (GPSIMD, ps_g)):
-                        mine = [(i, j) for i in rows for j in cols if ((i + j) % 3 == 2) == (owner == GPSIMD)]
-                        if not mine:
-                            continue
-                        msg = pool.tile([P, C], F32, name="msg")
-                        nc.tensor.matmul_mx(
-                            out=msg[:],
-                            lhsT=xq[:, jl * P : (jl + 1) * P].bitcast(FP8X4),
-                            lhsT_scale=xsc[:, jl * P : (jl + 1) * P],
-                            rhs=w1q[:].bitcast(FP8X4),
-                            rhs_scale=w1s[:],
-                            start=True,
-                            stop=True,
-                        )
-                        for i, j in mine:
-                            o = (ip - i) * KW + (jp - j)
-                            wgt = aff[:, o, i * CB + j : i * CB + j + 1]
-                            first = ip == i and jp == j
-                            if first:
-                                acc[(i, j)] = accp.tile([P, C], F32, name="acc")
-                            dst = acc[(i, j)]
-                            if owner == VECTOR:
-                                if first:
-                                    nc.vector.tensor_scalar(
-                                        out=dst[:], in0=msg[:], scalar1=wgt, scalar2=None, op0=ALU.mult
-                                    )
-                                else:
-                                    nc.vector.scalar_tensor_tensor(
-                                        out=dst[:], in0=msg[:], scalar=wgt, in1=dst[:], op0=ALU.mult, op1=ALU.add
-                                    )
-                            elif first:
-                                nc.scalar.activation(out=dst[:], in_=msg[:], func=ACT.Copy, scale=wgt)
-                            else:
-                                prod = xs.tile([P, C], F32, name="prod", bufs=4)
-                                nc.scalar.activation(out=prod[:], in_=msg[:], func=ACT.Copy, scale=wgt)
-                                nc.gpsimd.tensor_tensor(out=dst[:], in0=dst[:], in1=prod[:], op=ALU.add)
-            if ip >= 2 * PAD:
-                second_conv(ip - 2 * PAD)
+            st["aq"] = aq
+            st["asc"] = asc
+
+        def conv2_out(i, m):
+            o_ps = ps_m.tile([P, ROWPX], F32, name="o_ps", tag="misc")
+            for c0, c1 in ((0, 256), (256, 384)):
+                nc.tensor.matmul_mx(
+                    out=o_ps[:, c0:c1],
+                    lhsT=w2q[:, m * P : (m + 1) * P].bitcast(FP8X4),
+                    lhsT_scale=w2s[:, m * P : (m + 1) * P],
+                    rhs=st["aq"][:, c0:c1].bitcast(FP8X4),
+                    rhs_scale=st["asc"][:, c0:c1],
+                    start=True,
+                    stop=True,
+                )
+            o_sb = st2.tile([P, ROWPX], F32, name="o_sb", bufs=3)
+            nc.vector.tensor_tensor(out=o_sb[:], in0=o_ps[:], in1=st["x_res"][:, m, :], op=ALU.add)
+            nc.sync.dma_start(out=out_v[m, :, i, :, :], in_=o_sb[:].rearrange("p (a w) -> p a w", w=W))
+
+        def conv2_chores(i):
+            return [partial(conv2_gather, i), partial(conv2_quant, i)] + [partial(conv2_out, i, m) for m in range(T)]
+
+        for f in aff_head(0) + [partial(aff_norm, 0)] + x_chores(0):
+            f()
+        for ip in range(HR):
+            rows = list(range(max(0, ip - 2 * PAD), min(RB - 1, ip) + 1))
+            chores = []
+            if ip + 1 < HR:
+                chores += x_chores(ip + 1)
+            k_next = ip // 2 + 1
+            if k_next < NPAIR:
+                chores += aff_head(k_next) if ip % 2 == 0 else [partial(aff_norm, k_next)]
+            if ip - 2 * PAD - 1 >= 0:
+                chores += conv2_chores(ip - 2 * PAD - 1)
+            slots = [(i, j) for j in PE_COLS for i in rows]
+            jobs = [partial(vector_job, ip, jp, rows) for jp in range(VCOL, VCOL + KW)]
+            n = len(slots)
+            waiting = None
+            for k, (i, j) in enumerate(slots):
+                part = group(ip, i, j)
+                for f in jobs[k * len(jobs) // n : (k + 1) * len(jobs) // n]:
+                    f()
+                if waiting is not None:
+                    join(*waiting)
+                waiting = (ip, i, j, part)
+                for f in chores[k * len(chores) // n : (k + 1) * len(chores) // n]:
+                    f()
+            join(*waiting)
+        for f in conv2_chores(RB - 1):
+            f()

@@ -35,10 +35,7 @@ NROWS = 120
 ZP = W + 2 * PAD
 NPAIR = RB // 2
 AFFW = KW * 2 * KW * CB
-VCOL = 1
-PE_COLS = (0, 2)
-COST_S = 0.47
-COST_G = 0.62
+OWNER = ("VTV", "TVG", "VTV", "TVT", "VGV", "TVT", "VTV", "GVT")
 
 FLOPS = 2 * 2 * C * C * H * W + 2 * KW * KW * C * H * W
 
@@ -179,14 +176,13 @@ def tile_dcblock_t_kernel(
                 )
 
         affp = ctx.enter_context(tc.tile_pool(name="affp", bufs=2))
-        xs = ctx.enter_context(tc.tile_pool(name="xs", bufs=2))
-        msgp = ctx.enter_context(tc.tile_pool(name="msgp", bufs=14))
-        prodp = ctx.enter_context(tc.tile_pool(name="prodp", bufs=3))
-        accp = ctx.enter_context(tc.tile_pool(name="accp", bufs=8 * CB))
+        xs = ctx.enter_context(tc.tile_pool(name="xs", bufs=1))
+        msgp = ctx.enter_context(tc.tile_pool(name="msgp", bufs=2 * HC))
+        prodp = ctx.enter_context(tc.tile_pool(name="prodp", bufs=4))
+        accp = ctx.enter_context(tc.tile_pool(name="accp", bufs=9 * CB))
         st2 = ctx.enter_context(tc.tile_pool(name="st2", bufs=2))
-        ps_v = ctx.enter_context(tc.psum_pool(name="ps_v", bufs=2))
-        ps_s = ctx.enter_context(tc.psum_pool(name="ps_s", bufs=2))
-        ps_a = ctx.enter_context(tc.psum_pool(name="ps_a", bufs=2))
+        ps_v = ctx.enter_context(tc.psum_pool(name="ps_v", bufs=3))
+        ps_a = ctx.enter_context(tc.psum_pool(name="ps_a", bufs=3))
         ps_m = ctx.enter_context(tc.psum_pool(name="ps_m", bufs=2))
 
         x_v = x[0].rearrange("(t p) (a r) w -> t p r a w", p=P, r=RB)
@@ -195,7 +191,6 @@ def tile_dcblock_t_kernel(
         xq_of = {}
         msgs = {}
         e_of = {}
-        clock = {"s": 0.0, "g": 0.0}
 
         def aff_diff(k, dwi):
             if dwi == 0:
@@ -204,12 +199,11 @@ def tile_dcblock_t_kernel(
             shifted = nat[:, 2 * k : 2 * k + H, dwi : dwi + W : CB].rearrange("p (a r) b -> p r a b", r=RB)[:, 0:KW]
             centre = nat[:, 2 * k + PAD : 2 * k + PAD + (BH - 1) * RB + 1 : RB, PAD : PAD + W : CB]
             diff = affp.tile([P, KW, BH, BW], F32, name="diff")
-            nc.vector.tensor_tensor(
+            nc.gpsimd.tensor_tensor(
                 out=diff[:], in0=shifted, in1=centre.unsqueeze(1).to_broadcast([P, KW, BH, BW]), op=ALU.subtract
             )
             sq = affp.tile([P, KW * P], F32, name="sq")
             nc.scalar.activation(out=sq[:], in_=diff[:].rearrange("p r a b -> p (r a b)"), func=ACT.Square)
-            clock["s"] += 0.8
             for dhi in range(KW):
                 nc.tensor.matmul(
                     out=d2[:, dhi, dwi, :], lhsT=sq[:, dhi * P : (dhi + 1) * P], rhs=sel[:], start=True, stop=True
@@ -225,7 +219,6 @@ def tile_dcblock_t_kernel(
             nc.scalar.activation(
                 out=e2[:].rearrange("p h w s j -> p (h w s j)"), in_=e1[:], func=ACT.Exp, bias=negone[:, 0:1]
             )
-            clock["s"] += 0.6
             e_of[k] = e2
 
         def aff_norm(k):
@@ -278,7 +271,6 @@ def tile_dcblock_t_kernel(
                     scale=bsc[:, t : t + 1],
                     bias=bbi[:, t : t + 1],
                 )
-            clock["s"] += 1.6
             xq_of[ip] = xn
 
         def x_group(ip):
@@ -289,20 +281,31 @@ def tile_dcblock_t_kernel(
                     out=xg[:, CB * u : CB * u + CB],
                     in_=xn[:, :, CB * u : CB * u + ROWPX].rearrange("p t (k b) -> p b k t", b=CB),
                 )
-            clock["s"] += 4.5
             xq_of[ip] = xg
 
         def x_quant(ip):
             xg = xq_of[ip][:].rearrange("p b k t -> p (b k t)")
-            xq = xs.tile([P, HC * P], U32, name="xq", align_bytes=64)
-            xsc = xs.tile([P, HC * P], U8, name="xsc", align_bytes=64)
+            xq = xs.tile([P, HC * P], U32, name="xq", bufs=2, align_bytes=64)
+            xsc = xs.tile([P, HC * P], U8, name="xsc", bufs=2, align_bytes=64)
             for c0, c1 in ((0, 8 * P), (8 * P, 9 * P)):
                 nc.vector.quantize_mx(out=xq[:, c0:c1].bitcast(FP8X4), scales=xsc[:, c0:c1], in_=xg[:, T * c0 : T * c1])
             xq_of[ip] = (xq, xsc)
 
-        def first_conv(ip, jp, pool):
+        def x_chores(ip):
+            return [partial(f, ip) for f in (x_load, x_norm, x_group, x_quant)]
+
+        def weight(ip, jp, i, j):
+            return aff[:, i // 2, ip - i, jp - j, i % 2, j : j + 1]
+
+        def owner(i, j):
+            return OWNER[i % 8][j]
+
+        def rows_of(ip):
+            return range(max(0, ip - 2 * PAD), min(RB - 1, ip) + 1)
+
+        def position_job(ip, jp):
             xq, xsc = xq_of[ip]
-            msg = pool.tile([P, C], F32, name="msg")
+            msg = ps_v.tile([P, C], F32, name="msg")
             nc.tensor.matmul_mx(
                 out=msg[:],
                 lhsT=xq[:, jp * P : (jp + 1) * P].bitcast(FP8X4),
@@ -312,51 +315,32 @@ def tile_dcblock_t_kernel(
                 start=True,
                 stop=True,
             )
-            return msg
-
-        def msg_copy(ip, jp):
-            msg = first_conv(ip, jp, ps_s)
             m_sb = msgp.tile([P, C], F32, name="m_sb")
             nc.scalar.copy(out=m_sb[:], in_=msg[:])
-            clock["s"] += 0.45
             msgs[(ip, jp)] = m_sb
+            src = m_sb
+            for i in rows_of(ip):
+                for j in range(max(0, jp - 2 * PAD), min(CB - 1, jp) + 1):
+                    if owner(i, j) != "V":
+                        continue
+                    wgt = weight(ip, jp, i, j)
+                    if ip == i and jp == j:
+                        acc[(i, j)] = accp.tile([P, C], F32, name="acc")
+                        nc.vector.tensor_scalar(out=acc[(i, j)][:], in0=src[:], scalar1=wgt, scalar2=None, op0=ALU.mult)
+                    else:
+                        dst = acc[(i, j)]
+                        nc.vector.scalar_tensor_tensor(
+                            out=dst[:], in0=src[:], scalar=wgt, in1=dst[:], op0=ALU.mult, op1=ALU.add
+                        )
+                    src = msg
 
-        def x_chores(ip):
-            return [partial(f, ip) for f in (x_load, x_norm, x_group, x_quant)] + [
-                partial(msg_copy, ip, jp) for jp in range(HC)
-            ]
-
-        def weight(ip, jp, i, j):
-            return aff[:, i // 2, ip - i, jp - j, i % 2, j : j + 1]
-
-        def vector_job(ip, jp, rows):
-            msg = first_conv(ip, jp, ps_v)
-            for i in rows:
-                wgt = weight(ip, jp, i, VCOL)
-                if ip == i and jp == VCOL:
-                    acc[(i, VCOL)] = accp.tile([P, C], F32, name="acc")
-                    nc.vector.tensor_scalar(out=acc[(i, VCOL)][:], in0=msg[:], scalar1=wgt, scalar2=None, op0=ALU.mult)
-                else:
-                    dst = acc[(i, VCOL)]
-                    nc.vector.scalar_tensor_tensor(
-                        out=dst[:], in0=msg[:], scalar=wgt, in1=dst[:], op0=ALU.mult, op1=ALU.add
-                    )
-
-        def group(ip, i, j):
+        def tensor_group(ip, i, j):
             part = ps_a.tile([P, T, P], F32, name="part")
             for dwi in range(KW):
-                src = msgs[(ip, j + dwi)]
-                wgt = weight(ip, j + dwi, i, j)
-                if clock["s"] + COST_S <= clock["g"] + COST_G:
-                    prod = prodp.tile([P, C], F32, name="prod_s")
-                    nc.scalar.activation(out=prod[:], in_=src[:], func=ACT.Copy, scale=wgt)
-                    clock["s"] += COST_S
-                else:
-                    prod = prodp.tile([P, C], F32, name="prod_g")
-                    nc.gpsimd.tensor_scalar(
-                        out=prod[:], in0=src[:], scalar1=wgt, scalar2=0.0, op0=ALU.mult, op1=ALU.add
-                    )
-                    clock["g"] += COST_G
+                prod = prodp.tile([P, C], F32, name="prod_s")
+                nc.scalar.activation(
+                    out=prod[:], in_=msgs[(ip, j + dwi)][:], func=ACT.Copy, scale=weight(ip, j + dwi, i, j)
+                )
                 for t in range(T):
                     nc.tensor.matmul(
                         out=part[:, t, :],
@@ -377,6 +361,20 @@ def tile_dcblock_t_kernel(
                 dst = acc[(i, j)]
                 nc.vector.tensor_tensor(out=dst[:], in0=flat, in1=dst[:], op=ALU.add)
 
+        def gpsimd_group(ip, i, j):
+            for dwi in range(KW):
+                src = msgs[(ip, j + dwi)]
+                wgt = weight(ip, j + dwi, i, j)
+                if ip == i and dwi == 0:
+                    acc[(i, j)] = accp.tile([P, C], F32, name="acc")
+                    prod = acc[(i, j)]
+                else:
+                    prod = prodp.tile([P, C], F32, name="prod_g", bufs=2)
+                nc.gpsimd.tensor_scalar(out=prod[:], in0=src[:], scalar1=wgt, scalar2=0.0, op0=ALU.mult, op1=ALU.add)
+                if not (ip == i and dwi == 0):
+                    dst = acc[(i, j)]
+                    nc.gpsimd.tensor_tensor(out=dst[:], in0=dst[:], in1=prod[:], op=ALU.add)
+
         st = {}
 
         def conv2_gather(i):
@@ -386,7 +384,7 @@ def tile_dcblock_t_kernel(
             grp = st2.tile([P, ROWPX, T], BF16, name="grp", align_bytes=64)
             grp_v = grp[:].rearrange("p (k b) t -> p b k t", b=CB)
             for j in range(CB):
-                if j == VCOL:
+                if owner(i, j) != "T":
                     a_t = ps_m.tile([P, T, P], F32, name="a_t", tag="misc")
                     for t in range(T):
                         nc.tensor.transpose(a_t[:, t, :], acc[(i, j)][:, t * P : (t + 1) * P], ident_f[:])
@@ -394,7 +392,6 @@ def tile_dcblock_t_kernel(
                 else:
                     src = acc[(i, j)][:].rearrange("p (t k) -> p t k", t=T)
                 nc.scalar.copy(out=grp_v[:, j], in_=src.rearrange("p t k -> p k t"))
-                clock["s"] += 0.65
             st["x_res"] = x_res
             st["grp"] = grp
 
@@ -430,29 +427,34 @@ def tile_dcblock_t_kernel(
 
         for f in aff_head(0) + [partial(aff_norm, 0)] + x_chores(0):
             f()
-        for ip in range(HR):
-            rows = list(range(max(0, ip - 2 * PAD), min(RB - 1, ip) + 1))
+        for r in range(HR + 1):
+            jobs = [partial(position_job, r, jp) for jp in range(HC)] if r < HR else []
             chores = []
-            if ip + 1 < HR:
-                chores += x_chores(ip + 1)
-            k_next = ip // 2 + 1
+            if r + 1 < HR:
+                chores += x_chores(r + 1)
+            k_next = r // 2 + 1
             if k_next < NPAIR:
-                chores += aff_head(k_next) if ip % 2 == 0 else [partial(aff_norm, k_next)]
-            if ip - 2 * PAD - 1 >= 0:
-                chores += conv2_chores(ip - 2 * PAD - 1)
-            slots = [(i, j) for j in PE_COLS for i in rows]
-            jobs = [partial(vector_job, ip, jp, rows) for jp in range(VCOL, VCOL + KW)]
-            n = len(slots)
+                chores += aff_head(k_next) if r % 2 == 0 else [partial(aff_norm, k_next)]
+            if r - 2 * PAD - 2 >= 0:
+                chores += conv2_chores(r - 2 * PAD - 2)
+            slots = [(i, j) for j in range(CB) for i in rows_of(r - 1) if owner(i, j) != "V"] if r > 0 else []
+            n = max(1, len(slots))
             waiting = None
-            for k, (i, j) in enumerate(slots):
-                part = group(ip, i, j)
+            for k in range(n):
                 for f in jobs[k * len(jobs) // n : (k + 1) * len(jobs) // n]:
                     f()
-                if waiting is not None:
-                    join(*waiting)
-                waiting = (ip, i, j, part)
+                if k < len(slots):
+                    i, j = slots[k]
+                    if owner(i, j) == "G":
+                        gpsimd_group(r - 1, i, j)
+                    else:
+                        part = tensor_group(r - 1, i, j)
+                        if waiting is not None:
+                            join(*waiting)
+                        waiting = (r - 1, i, j, part)
                 for f in chores[k * len(chores) // n : (k + 1) * len(chores) // n]:
                     f()
-            join(*waiting)
+            if waiting is not None:
+                join(*waiting)
         for f in conv2_chores(RB - 1):
             f()

@@ -35,6 +35,7 @@ NROWS = 120
 ZP = W + 2 * PAD
 NPAIR = RB // 2
 AFFW = KW * 2 * KW * CB
+JOIN_LAG = 1
 OWNER = ("VTV", "TVG", "VTV", "TVT", "VGV", "TVT", "VTV", "GVT")
 
 FLOPS = 2 * 2 * C * C * H * W + 2 * KW * KW * C * H * W
@@ -178,11 +179,11 @@ def tile_dcblock_t_kernel(
         affp = ctx.enter_context(tc.tile_pool(name="affp", bufs=2))
         xs = ctx.enter_context(tc.tile_pool(name="xs", bufs=1))
         msgp = ctx.enter_context(tc.tile_pool(name="msgp", bufs=2 * HC))
-        prodp = ctx.enter_context(tc.tile_pool(name="prodp", bufs=4))
+        prodp = ctx.enter_context(tc.tile_pool(name="prodp", bufs=8))
         accp = ctx.enter_context(tc.tile_pool(name="accp", bufs=9 * CB))
         st2 = ctx.enter_context(tc.tile_pool(name="st2", bufs=2))
         ps_v = ctx.enter_context(tc.psum_pool(name="ps_v", bufs=3))
-        ps_a = ctx.enter_context(tc.psum_pool(name="ps_a", bufs=3))
+        ps_a = ctx.enter_context(tc.psum_pool(name="ps_a", bufs=2))
         ps_m = ctx.enter_context(tc.psum_pool(name="ps_m", bufs=2))
 
         x_v = x[0].rearrange("(t p) (a r) w -> t p r a w", p=P, r=RB)
@@ -190,20 +191,30 @@ def tile_dcblock_t_kernel(
         acc = {}
         xq_of = {}
         msgs = {}
+        banks = {}
         e_of = {}
 
         def aff_diff(k, dwi):
             if dwi == 0:
-                e_of[k] = ps_m.tile([P, KW, KW, 2 * CB], F32, name="d2", tag="misc")
-            d2 = e_of[k]
+                e_of[k] = ps_m.tile([P, KW, KW, 2 * CB], F32, name="d2", bufs=1)
             shifted = nat[:, 2 * k : 2 * k + H, dwi : dwi + W : CB].rearrange("p (a r) b -> p r a b", r=RB)[:, 0:KW]
             centre = nat[:, 2 * k + PAD : 2 * k + PAD + (BH - 1) * RB + 1 : RB, PAD : PAD + W : CB]
             diff = affp.tile([P, KW, BH, BW], F32, name="diff")
             nc.gpsimd.tensor_tensor(
                 out=diff[:], in0=shifted, in1=centre.unsqueeze(1).to_broadcast([P, KW, BH, BW]), op=ALU.subtract
             )
+            e_of[(k, dwi)] = diff
+
+        def aff_square(k, dwi):
             sq = affp.tile([P, KW * P], F32, name="sq")
-            nc.scalar.activation(out=sq[:], in_=diff[:].rearrange("p r a b -> p (r a b)"), func=ACT.Square)
+            nc.scalar.activation(
+                out=sq[:], in_=e_of[(k, dwi)][:].rearrange("p r a b -> p (r a b)"), func=ACT.Square
+            )
+            e_of[(k, dwi)] = sq
+
+        def aff_sum(k, dwi):
+            d2 = e_of[k]
+            sq = e_of[(k, dwi)]
             for dhi in range(KW):
                 nc.tensor.matmul(
                     out=d2[:, dhi, dwi, :], lhsT=sq[:, dhi * P : (dhi + 1) * P], rhs=sel[:], start=True, stop=True
@@ -245,7 +256,12 @@ def tile_dcblock_t_kernel(
                     )
 
         def aff_head(k):
-            return [partial(aff_diff, k, dwi) for dwi in range(KW)] + [partial(aff_exp, k)]
+            order = []
+            for n in range(KW + 2):
+                for f, dwi in ((aff_diff, n), (aff_square, n - 1), (aff_sum, n - 2)):
+                    if 0 <= dwi < KW:
+                        order.append(partial(f, k, dwi))
+            return order + [partial(aff_exp, k)]
 
         def x_load(ip):
             hrow = ip - PAD
@@ -303,7 +319,7 @@ def tile_dcblock_t_kernel(
         def rows_of(ip):
             return range(max(0, ip - 2 * PAD), min(RB - 1, ip) + 1)
 
-        def position_job(ip, jp):
+        def position_pass(ip, jp):
             xq, xsc = xq_of[ip]
             msg = ps_v.tile([P, C], F32, name="msg")
             nc.tensor.matmul_mx(
@@ -315,10 +331,16 @@ def tile_dcblock_t_kernel(
                 start=True,
                 stop=True,
             )
+            banks[(ip, jp)] = msg
+
+        def position_copy(ip, jp):
             m_sb = msgp.tile([P, C], F32, name="m_sb")
-            nc.scalar.copy(out=m_sb[:], in_=msg[:])
+            nc.scalar.copy(out=m_sb[:], in_=banks[(ip, jp)][:])
             msgs[(ip, jp)] = m_sb
-            src = m_sb
+
+        def position_use(ip, jp):
+            msg = banks[(ip, jp)]
+            src = msgs[(ip, jp)]
             for i in rows_of(ip):
                 for j in range(max(0, jp - 2 * PAD), min(CB - 1, jp) + 1):
                     if owner(i, j) != "V":
@@ -377,23 +399,25 @@ def tile_dcblock_t_kernel(
 
         st = {}
 
-        def conv2_gather(i):
+        def conv2_load(i):
             x_res = st2.tile([P, T, ROWPX], BF16, name="x_res")
             for t in range(T):
                 nc.sync.dma_start(out=x_res[:, t, :].rearrange("p (a w) -> p a w", w=W), in_=x_v[t, :, i, :, :])
-            grp = st2.tile([P, ROWPX, T], BF16, name="grp", align_bytes=64)
-            grp_v = grp[:].rearrange("p (k b) t -> p b k t", b=CB)
-            for j in range(CB):
-                if owner(i, j) != "T":
-                    a_t = ps_m.tile([P, T, P], F32, name="a_t", tag="misc")
-                    for t in range(T):
-                        nc.tensor.transpose(a_t[:, t, :], acc[(i, j)][:, t * P : (t + 1) * P], ident_f[:])
-                    src = a_t[:]
-                else:
-                    src = acc[(i, j)][:].rearrange("p (t k) -> p t k", t=T)
-                nc.scalar.copy(out=grp_v[:, j], in_=src.rearrange("p t k -> p k t"))
             st["x_res"] = x_res
-            st["grp"] = grp
+            st["grp"] = st2.tile([P, ROWPX, T], BF16, name="grp", align_bytes=64)
+
+        def conv2_turn(i, j):
+            if owner(i, j) != "T":
+                a_t = ps_m.tile([P, T, P], F32, name="a_t", tag="misc")
+                for t in range(T):
+                    nc.tensor.transpose(a_t[:, t, :], acc[(i, j)][:, t * P : (t + 1) * P], ident_f[:])
+                st[j] = a_t[:]
+            else:
+                st[j] = acc[(i, j)][:].rearrange("p (t k) -> p t k", t=T)
+
+        def conv2_round(i, j):
+            grp_v = st["grp"][:].rearrange("p (k b) t -> p b k t", b=CB)
+            nc.scalar.copy(out=grp_v[:, j], in_=st[j].rearrange("p t k -> p k t"))
 
         def conv2_quant(i):
             aq = st2.tile([P, ROWPX], U32, name="aq", align_bytes=64)
@@ -406,7 +430,7 @@ def tile_dcblock_t_kernel(
             st["aq"] = aq
             st["asc"] = asc
 
-        def conv2_out(i, m):
+        def conv2_pass(i, m):
             o_ps = ps_m.tile([P, ROWPX], F32, name="o_ps", tag="misc")
             for c0, c1 in ((0, 256), (256, 384)):
                 nc.tensor.matmul_mx(
@@ -418,43 +442,67 @@ def tile_dcblock_t_kernel(
                     start=True,
                     stop=True,
                 )
+            st[("o", m)] = o_ps
+
+        def conv2_out(i, m):
             o_sb = st2.tile([P, ROWPX], F32, name="o_sb", bufs=3)
-            nc.vector.tensor_tensor(out=o_sb[:], in0=o_ps[:], in1=st["x_res"][:, m, :], op=ALU.add)
+            nc.vector.tensor_tensor(out=o_sb[:], in0=st[("o", m)][:], in1=st["x_res"][:, m, :], op=ALU.add)
             nc.sync.dma_start(out=out_v[m, :, i, :, :], in_=o_sb[:].rearrange("p (a w) -> p a w", w=W))
 
         def conv2_chores(i):
-            return [partial(conv2_gather, i), partial(conv2_quant, i)] + [partial(conv2_out, i, m) for m in range(T)]
+            order = [partial(conv2_load, i), partial(conv2_turn, i, 0)]
+            for j in range(1, CB):
+                order += [partial(conv2_turn, i, j), partial(conv2_round, i, j - 1)]
+            order += [partial(conv2_round, i, CB - 1), None, partial(conv2_quant, i), None, partial(conv2_pass, i, 0)]
+            for m in range(1, T):
+                order += [partial(conv2_pass, i, m), partial(conv2_out, i, m - 1)]
+            return order + [partial(conv2_out, i, T - 1)]
 
-        for f in aff_head(0) + [partial(aff_norm, 0)] + x_chores(0):
+        ctx.enter_context(tc.manual_schedule())
+        for f in x_chores(0) + aff_head(0) + [partial(aff_norm, 0)]:
             f()
+        position_pass(0, 0)
+        position_copy(0, 0)
+        position_pass(0, 1)
+
+        def position_job(ip, jp):
+            q = ip * HC + jp
+            if q + 1 < HR * HC:
+                position_copy((q + 1) // HC, (q + 1) % HC)
+            if q + 2 < HR * HC:
+                position_pass((q + 2) // HC, (q + 2) % HC)
+            position_use(ip, jp)
+
+        def spread(items, lo, hi):
+            return [(lo + (hi - lo) * (k + 0.5) / len(items), f) for k, f in enumerate(items)]
+
+        pending = []
+
+        def tensor_slot(ip, i, j):
+            pending.append((ip, i, j, tensor_group(ip, i, j)))
+            if len(pending) > JOIN_LAG:
+                join(*pending.pop(0))
+
         for r in range(HR + 1):
-            jobs = [partial(position_job, r, jp) for jp in range(HC)] if r < HR else []
-            chores = []
+            plan = []
+            if r < HR:
+                plan += spread([partial(position_job, r, jp) for jp in range(HC)], 0.0, 1.0)
             if r + 1 < HR:
-                chores += x_chores(r + 1)
+                plan += spread(x_chores(r + 1), 0.0, 0.6)
             k_next = r // 2 + 1
             if k_next < NPAIR:
-                chores += aff_head(k_next) if r % 2 == 0 else [partial(aff_norm, k_next)]
+                plan += spread(aff_head(k_next) if r % 2 == 0 else [partial(aff_norm, k_next)], 0.0, 1.0)
             if r - 2 * PAD - 2 >= 0:
-                chores += conv2_chores(r - 2 * PAD - 2)
-            slots = [(i, j) for j in range(CB) for i in rows_of(r - 1) if owner(i, j) != "V"] if r > 0 else []
-            n = max(1, len(slots))
-            waiting = None
-            for k in range(n):
-                for f in jobs[k * len(jobs) // n : (k + 1) * len(jobs) // n]:
+                plan += spread(conv2_chores(r - 2 * PAD - 2), 0.0, 1.0)
+            if r > 0:
+                mine = [(i, j) for j in range(CB) for i in rows_of(r - 1)]
+                plan += spread([partial(tensor_slot, r - 1, i, j) for i, j in mine if owner(i, j) == "T"], 0.0, 1.0)
+                plan += spread([partial(gpsimd_group, r - 1, i, j) for i, j in mine if owner(i, j) == "G"], 0.0, 1.0)
+            for place, f in sorted(plan, key=lambda item: item[0]):
+                if f is not None:
                     f()
-                if k < len(slots):
-                    i, j = slots[k]
-                    if owner(i, j) == "G":
-                        gpsimd_group(r - 1, i, j)
-                    else:
-                        part = tensor_group(r - 1, i, j)
-                        if waiting is not None:
-                            join(*waiting)
-                        waiting = (r - 1, i, j, part)
-                for f in chores[k * len(chores) // n : (k + 1) * len(chores) // n]:
-                    f()
-            if waiting is not None:
-                join(*waiting)
+            for n in range(len(pending)):
+                join(*pending.pop(0))
         for f in conv2_chores(RB - 1):
-            f()
+            if f is not None:
+                f()

@@ -21,21 +21,29 @@ H = 96
 W = 96
 KW = 7
 PAD = 3
-RB = 24
+RB = 20
 CB = 3
-BH = H // RB
+BH = 4
 BW = W // CB
+HA = BH * RB
 HR = RB + 2 * PAD
 HC = CB + 2 * PAD
 T = 4
 ROWPX = BH * W
 XLEN = PAD + ROWPX + PAD
 XPITCH = 400
-NROWS = 120
+NROWS = H + 2 * PAD
 ZP = W + 2 * PAD
 NPAIR = RB // 2
 AFFW = KW * 2 * KW * CB
-JOIN_LAG = 1
+PR = 8
+PC = 16
+HY = PR + 2 * PAD
+HZ = PC + 2 * PAD
+NU = HY * HZ
+KT = 3
+BROWS = H - HA + PAD
+BY = H - HA + 2 * PAD
 OWNER = ("VTV", "TVG", "VTV", "TVT", "VGV", "TVT", "VTV", "GVT")
 
 FLOPS = 2 * 2 * C * C * H * W + 2 * KW * KW * C * H * W
@@ -72,6 +80,8 @@ def tile_dcblock_t_kernel(
             nc.vector.memset(xr_tiles[k][:], 0.0)
         nc.vector.memset(negone[:], -1.0)
         probs = coarse_probs[0]
+        x_v = x[0].rearrange("(t p) h w -> t p h w", p=P)
+        out_v = out[0].rearrange("(m p) h w -> m p h w", p=P)
         for s in range(2):
             for j in range(CB):
                 g = s * CB + j
@@ -176,45 +186,225 @@ def tile_dcblock_t_kernel(
                     out=wq[:].bitcast(FP8X4), scales=wsc[:], in_=w_gr[:].rearrange("p o t -> p (o t)")
                 )
 
+        with tc.tile_pool(name="pb", bufs=1) as pb, tc.tile_pool(name="pbw", bufs=2) as pbw, tc.psum_pool(
+            name="psb", bufs=1
+        ) as psb:
+            u_i = pb.tile([P, KT], I32, name="u_i")
+            nc.gpsimd.iota(u_i[:], pattern=[[P, KT]], base=0, channel_multiplier=1)
+            u_f = pb.tile([P, KT], F32, name="u_f")
+            nc.vector.tensor_copy(out=u_f[:], in_=u_i[:])
+            y_f = pb.tile([P, KT], F32, name="y_f")
+            nc.vector.memset(y_f[:], 0.0)
+            for m in range(1, KT * P // HZ + 1):
+                nc.vector.scalar_tensor_tensor(
+                    out=y_f[:], in0=u_f[:], scalar=float(HZ * m), in1=y_f[:], op0=ALU.is_ge, op1=ALU.add
+                )
+            z_f = pb.tile([P, KT], F32, name="z_f")
+            nc.vector.scalar_tensor_tensor(
+                out=z_f[:], in0=y_f[:], scalar=float(-HZ), in1=u_f[:], op0=ALU.mult, op1=ALU.add
+            )
+            yo_i = pb.tile([P, P], I32, name="yo_i")
+            nc.gpsimd.iota(yo_i[:], pattern=[[1, PR], [0, PC]], base=0, channel_multiplier=0)
+            zo_i = pb.tile([P, P], I32, name="zo_i")
+            nc.gpsimd.iota(zo_i[:], pattern=[[0, PR], [1, PC]], base=0, channel_multiplier=0)
+            yo = pb.tile([P, P], F32, name="yo")
+            nc.vector.tensor_copy(out=yo[:], in_=yo_i[:])
+            zo = pb.tile([P, P], F32, name="zo")
+            nc.vector.tensor_copy(out=zo[:], in_=zo_i[:])
+            band = pb.tile([P, KT, P], F32, name="band")
+            side = pb.tile([P, P], F32, name="side")
+            for k in range(KT):
+                first = True
+                for grid, mine in ((yo, y_f), (zo, z_f)):
+                    for bound, op in ((float(-2 * PAD), ALU.is_ge), (0.0, ALU.is_le)):
+                        dst = band[:, k, :] if first else side[:]
+                        nc.vector.tensor_scalar(
+                            out=dst, in0=grid[:], scalar1=mine[:, k : k + 1], scalar2=bound, op0=ALU.subtract, op1=op
+                        )
+                        if not first:
+                            nc.vector.tensor_tensor(out=band[:, k, :], in0=band[:, k, :], in1=side[:], op=ALU.mult)
+                        first = False
+            ones2 = pb.tile([P, 2], F32, name="ones2")
+            nc.vector.memset(ones2[:], 1.0)
+
+            pr_raw = pb.tile([P, BROWS * W], BF16, name="pr_raw")
+            for c0, c1 in ((0, 16), (16, CP)):
+                nc.sync.dma_start(
+                    out=pr_raw[c0:c1, :].rearrange("c (y w) -> c y w", w=W), in_=probs[c0:c1, HA - PAD : H, :]
+                )
+            pv = pb.tile([P, BY, ZP], F32, name="pv")
+            nc.vector.memset(pv[:], 0.0)
+            nc.vector.tensor_copy(
+                out=pv[0:CP, 0:BROWS, PAD : PAD + W], in_=pr_raw[0:CP, :].rearrange("c (y w) -> c y w", w=W)
+            )
+            pa = pb.tile([P, BY, ZP], F32, name="pa")
+            nc.vector.tensor_scalar(out=pa[:], in0=pv[:], scalar1=-2.0, scalar2=None, op0=ALU.mult)
+            sqp = pb.tile([P, BY * ZP], F32, name="sqp")
+            nc.scalar.activation(out=sqp[:], in_=pv[:].rearrange("p y z -> p (y z)"), func=ACT.Square)
+            w_n = pb.tile([P, P], F32, name="w_n")
+            nc.vector.memset(w_n[:], 0.0)
+            nc.vector.memset(w_n[0:32, 32:33], 1.0)
+            nc.vector.memset(w_n[0:32, 64:65], 1.0)
+            pa_f = pa[:].rearrange("p y z -> p (y z)")
+            pv_f = pv[:].rearrange("p y z -> p (y z)")
+            for c0 in range(0, BY * ZP, 512):
+                c1 = min(c0 + 512, BY * ZP)
+                n_ps = psb.tile([P, 512], F32, name="n_ps", tag="g_ps")
+                nc.tensor.matmul(out=n_ps[:, 0 : c1 - c0], lhsT=w_n[:], rhs=sqp[:, c0:c1], start=True, stop=True)
+                nc.vector.tensor_copy(out=pa_f[32:64, c0:c1], in_=n_ps[32:64, 0 : c1 - c0])
+                nc.vector.tensor_copy(out=pv_f[64:96, c0:c1], in_=n_ps[64:96, 0 : c1 - c0])
+            nc.vector.memset(pa[64:96], 1.0)
+            nc.vector.memset(pv[32:64], 1.0)
+
+            xrb = pb.tile([P, T, BROWS * W], BF16, name="xrb")
+            for t in range(T):
+                nc.sync.dma_start(
+                    out=xrb[:, t, :].rearrange("p (y w) -> p y w", w=W), in_=x_v[t, :, HA - PAD : H, :]
+                )
+            xrb_v = xrb[:].rearrange("p t (y w) -> p t y w", w=W)
+            xnb = pb.tile([P, T, BY, ZP], BF16, name="xnb")
+            nc.vector.memset(xnb[:], 0.0)
+            for t in range(T):
+                nc.scalar.activation(
+                    out=xnb[:, t, 0:BROWS, PAD : PAD + W],
+                    in_=xrb_v[:, t],
+                    func=ACT.Identity,
+                    scale=bsc[:, t : t + 1],
+                    bias=bbi[:, t : t + 1],
+                )
+
+            for y0 in range(0, H - HA, PR):
+                for z0 in range(0, W, PC):
+                    xgp = pbw.tile([P, KT * P, T], BF16, name="xgp", align_bytes=64)
+                    nc.vector.memset(xgp[:, NU:, :], 0.0)
+                    nc.vector.tensor_copy(
+                        out=xgp[:, 0:NU, :].rearrange("p (y z) t -> p y z t", z=HZ),
+                        in_=xnb[:, :, y0 : y0 + HY, z0 : z0 + HZ].rearrange("p t y z -> p y z t"),
+                    )
+                    xqp = pbw.tile([P, KT * P], U32, name="xqp", align_bytes=64)
+                    xsp = pbw.tile([P, KT * P], U8, name="xsp", align_bytes=64)
+                    xgp_f = xgp[:].rearrange("p u t -> p (u t)")
+                    for c0, c1 in ((0, 256), (256, 384)):
+                        nc.vector.quantize_mx(
+                            out=xqp[:, c0:c1].bitcast(FP8X4), scales=xsp[:, c0:c1], in_=xgp_f[:, T * c0 : T * c1]
+                        )
+                    m_sb = []
+                    for k in range(KT):
+                        msg = psb.tile([P, C], F32, name="msg", bufs=2)
+                        nc.tensor.matmul_mx(
+                            out=msg[:],
+                            lhsT=xqp[:, k * P : (k + 1) * P].bitcast(FP8X4),
+                            lhsT_scale=xsp[:, k * P : (k + 1) * P],
+                            rhs=w1q[:].bitcast(FP8X4),
+                            rhs_scale=w1s[:],
+                            start=True,
+                            stop=True,
+                        )
+                        m_sb.append(pbw.tile([P, C], F32, name="m_sb%d" % k))
+                        if k == 1:
+                            nc.scalar.copy(out=m_sb[k][:], in_=msg[:])
+                        else:
+                            nc.vector.tensor_copy(out=m_sb[k][:], in_=msg[:])
+                    au = pbw.tile([P, KT * P], F32, name="au")
+                    nc.gpsimd.memset(au[:, NU:], 0.0)
+                    nc.gpsimd.tensor_copy(
+                        out=au[:, 0:NU].rearrange("p (y z) -> p y z", z=HZ), in_=pa[:, y0 : y0 + HY, z0 : z0 + HZ]
+                    )
+                    bv = pbw.tile([P, P], F32, name="bv")
+                    nc.gpsimd.tensor_copy(
+                        out=bv[:].rearrange("p (y z) -> p y z", z=PC),
+                        in_=pv[:, y0 + PAD : y0 + PAD + PR, z0 + PAD : z0 + PAD + PC],
+                    )
+                    d2p = psb.tile([P, KT, P], F32, name="d2p")
+                    for k in range(KT):
+                        nc.tensor.matmul(
+                            out=d2p[:, k, :], lhsT=au[:, k * P : (k + 1) * P], rhs=bv[:], start=True, stop=True
+                        )
+                    e1p = pbw.tile([P, KT * P], F32, name="e1p")
+                    nc.scalar.activation(
+                        out=e1p[:], in_=d2p[:].rearrange("p k v -> p (k v)"), func=ACT.Exp, scale=neginv[:, 0:1]
+                    )
+                    e2p = pbw.tile([P, KT * P], F32, name="e2p")
+                    nc.scalar.activation(out=e2p[:], in_=e1p[:], func=ACT.Exp, bias=negone[:, 0:1])
+                    emp = pbw.tile([P, KT, P], F32, name="emp")
+                    nc.vector.tensor_tensor(
+                        out=emp[:].rearrange("p k v -> p (k v)"),
+                        in0=e2p[:],
+                        in1=band[:].rearrange("p k v -> p (k v)"),
+                        op=ALU.mult,
+                    )
+                    s_ps = psb.tile([P, 2], F32, name="s_ps")
+                    for k in range(KT):
+                        nc.tensor.matmul(
+                            out=s_ps[:], lhsT=emp[:, k, :], rhs=ones2[:], start=(k == 0), stop=(k == KT - 1)
+                        )
+                    g_ps = psb.tile([P, C], F32, name="g_ps")
+                    for k in range(KT):
+                        nc.tensor.matmul(
+                            out=g_ps[:], lhsT=emp[:, k, :], rhs=m_sb[k][:], start=(k == 0), stop=(k == KT - 1)
+                        )
+                    rs = pbw.tile([P, 1], F32, name="rs")
+                    nc.vector.reciprocal(out=rs[:], in_=s_ps[:, 0:1])
+                    agg = pbw.tile([P, C], F32, name="agg")
+                    nc.scalar.activation(out=agg[:], in_=g_ps[:], func=ACT.Copy, scale=rs[:, 0:1])
+                    a_t = psb.tile([P, T, P], F32, name="a_t")
+                    for t in range(T):
+                        nc.tensor.transpose(a_t[:, t, :], agg[:, t * P : (t + 1) * P], ident_f[:])
+                    grp = pbw.tile([P, P, T], BF16, name="grp", align_bytes=64)
+                    nc.vector.tensor_copy(out=grp[:], in_=a_t[:].rearrange("p t v -> p v t"))
+                    aqp = pbw.tile([P, P], U32, name="aqp", align_bytes=64)
+                    asp = pbw.tile([P, P], U8, name="asp", align_bytes=64)
+                    nc.vector.quantize_mx(
+                        out=aqp[:].bitcast(FP8X4), scales=asp[:], in_=grp[:].rearrange("p v t -> p (v t)")
+                    )
+                    o_ps = psb.tile([P, T, P], F32, name="o_ps")
+                    for m in range(T):
+                        nc.tensor.matmul_mx(
+                            out=o_ps[:, m, :],
+                            lhsT=w2q[:, m * P : (m + 1) * P].bitcast(FP8X4),
+                            lhsT_scale=w2s[:, m * P : (m + 1) * P],
+                            rhs=aqp[:].bitcast(FP8X4),
+                            rhs_scale=asp[:],
+                            start=True,
+                            stop=True,
+                        )
+                    o_sb = pbw.tile([P, T, PR, PC], F32, name="o_sb")
+                    nc.vector.tensor_tensor(
+                        out=o_sb[:],
+                        in0=o_ps[:].rearrange("p m (y z) -> p m y z", z=PC),
+                        in1=xrb_v[:, :, PAD + y0 : PAD + y0 + PR, z0 : z0 + PC],
+                        op=ALU.add,
+                    )
+                    for m in range(T):
+                        nc.sync.dma_start(out=out_v[m, :, HA + y0 : HA + y0 + PR, z0 : z0 + PC], in_=o_sb[:, m])
+
         affp = ctx.enter_context(tc.tile_pool(name="affp", bufs=2))
         xs = ctx.enter_context(tc.tile_pool(name="xs", bufs=1))
         msgp = ctx.enter_context(tc.tile_pool(name="msgp", bufs=2 * HC))
-        prodp = ctx.enter_context(tc.tile_pool(name="prodp", bufs=8))
+        prodp = ctx.enter_context(tc.tile_pool(name="prodp", bufs=4))
         accp = ctx.enter_context(tc.tile_pool(name="accp", bufs=9 * CB))
         st2 = ctx.enter_context(tc.tile_pool(name="st2", bufs=2))
         ps_v = ctx.enter_context(tc.psum_pool(name="ps_v", bufs=3))
-        ps_a = ctx.enter_context(tc.psum_pool(name="ps_a", bufs=2))
+        ps_a = ctx.enter_context(tc.psum_pool(name="ps_a", bufs=3))
         ps_m = ctx.enter_context(tc.psum_pool(name="ps_m", bufs=2))
 
-        x_v = x[0].rearrange("(t p) (a r) w -> t p r a w", p=P, r=RB)
-        out_v = out[0].rearrange("(m p) (a r) w -> m p r a w", p=P, r=RB)
         acc = {}
         xq_of = {}
         msgs = {}
-        banks = {}
         e_of = {}
 
         def aff_diff(k, dwi):
             if dwi == 0:
-                e_of[k] = ps_m.tile([P, KW, KW, 2 * CB], F32, name="d2", bufs=1)
-            shifted = nat[:, 2 * k : 2 * k + H, dwi : dwi + W : CB].rearrange("p (a r) b -> p r a b", r=RB)[:, 0:KW]
+                e_of[k] = ps_m.tile([P, KW, KW, 2 * CB], F32, name="d2", tag="misc")
+            d2 = e_of[k]
+            shifted = nat[:, 2 * k : 2 * k + HA, dwi : dwi + W : CB].rearrange("p (a r) b -> p r a b", r=RB)[:, 0:KW]
             centre = nat[:, 2 * k + PAD : 2 * k + PAD + (BH - 1) * RB + 1 : RB, PAD : PAD + W : CB]
             diff = affp.tile([P, KW, BH, BW], F32, name="diff")
             nc.gpsimd.tensor_tensor(
                 out=diff[:], in0=shifted, in1=centre.unsqueeze(1).to_broadcast([P, KW, BH, BW]), op=ALU.subtract
             )
-            e_of[(k, dwi)] = diff
-
-        def aff_square(k, dwi):
             sq = affp.tile([P, KW * P], F32, name="sq")
-            nc.scalar.activation(
-                out=sq[:], in_=e_of[(k, dwi)][:].rearrange("p r a b -> p (r a b)"), func=ACT.Square
-            )
-            e_of[(k, dwi)] = sq
-
-        def aff_sum(k, dwi):
-            d2 = e_of[k]
-            sq = e_of[(k, dwi)]
+            nc.scalar.activation(out=sq[:], in_=diff[:].rearrange("p r a b -> p (r a b)"), func=ACT.Square)
             for dhi in range(KW):
                 nc.tensor.matmul(
                     out=d2[:, dhi, dwi, :], lhsT=sq[:, dhi * P : (dhi + 1) * P], rhs=sel[:], start=True, stop=True
@@ -256,24 +446,16 @@ def tile_dcblock_t_kernel(
                     )
 
         def aff_head(k):
-            order = []
-            for n in range(KW + 2):
-                for f, dwi in ((aff_diff, n), (aff_square, n - 1), (aff_sum, n - 2)):
-                    if 0 <= dwi < KW:
-                        order.append(partial(f, k, dwi))
-            return order + [partial(aff_exp, k)]
+            return [partial(aff_diff, k, dwi) for dwi in range(KW)] + [partial(aff_exp, k)]
 
         def x_load(ip):
             hrow = ip - PAD
-            r = hrow % RB
-            shift = (hrow - r) // RB
-            a_lo = max(0, -shift)
-            a_hi = min(BH, BH - shift)
+            a_lo = 1 if hrow < 0 else 0
             xr = xr_tiles[ip % 2]
             for t in range(T):
                 nc.sync.dma_start(
-                    out=xr[:, t, PAD + a_lo * W : PAD + a_hi * W].rearrange("p (a w) -> p a w", w=W),
-                    in_=x_v[t, :, r, a_lo + shift : a_hi + shift, :],
+                    out=xr[:, t, PAD + a_lo * W : PAD + BH * W].rearrange("p (a w) -> p a w", w=W),
+                    in_=x_v[t, :, hrow + a_lo * RB : hrow + (BH - 1) * RB + 1 : RB, :],
                 )
 
         def x_norm(ip):
@@ -319,7 +501,7 @@ def tile_dcblock_t_kernel(
         def rows_of(ip):
             return range(max(0, ip - 2 * PAD), min(RB - 1, ip) + 1)
 
-        def position_pass(ip, jp):
+        def position_job(ip, jp):
             xq, xsc = xq_of[ip]
             msg = ps_v.tile([P, C], F32, name="msg")
             nc.tensor.matmul_mx(
@@ -331,16 +513,10 @@ def tile_dcblock_t_kernel(
                 start=True,
                 stop=True,
             )
-            banks[(ip, jp)] = msg
-
-        def position_copy(ip, jp):
             m_sb = msgp.tile([P, C], F32, name="m_sb")
-            nc.scalar.copy(out=m_sb[:], in_=banks[(ip, jp)][:])
+            nc.scalar.copy(out=m_sb[:], in_=msg[:])
             msgs[(ip, jp)] = m_sb
-
-        def position_use(ip, jp):
-            msg = banks[(ip, jp)]
-            src = msgs[(ip, jp)]
+            src = m_sb
             for i in rows_of(ip):
                 for j in range(max(0, jp - 2 * PAD), min(CB - 1, jp) + 1):
                     if owner(i, j) != "V":
@@ -399,25 +575,23 @@ def tile_dcblock_t_kernel(
 
         st = {}
 
-        def conv2_load(i):
+        def conv2_gather(i):
             x_res = st2.tile([P, T, ROWPX], BF16, name="x_res")
             for t in range(T):
-                nc.sync.dma_start(out=x_res[:, t, :].rearrange("p (a w) -> p a w", w=W), in_=x_v[t, :, i, :, :])
+                nc.sync.dma_start(out=x_res[:, t, :].rearrange("p (a w) -> p a w", w=W), in_=x_v[t, :, i : i + (BH - 1) * RB + 1 : RB, :])
+            grp = st2.tile([P, ROWPX, T], BF16, name="grp", align_bytes=64)
+            grp_v = grp[:].rearrange("p (k b) t -> p b k t", b=CB)
+            for j in range(CB):
+                if owner(i, j) != "T":
+                    a_t = ps_m.tile([P, T, P], F32, name="a_t", tag="misc")
+                    for t in range(T):
+                        nc.tensor.transpose(a_t[:, t, :], acc[(i, j)][:, t * P : (t + 1) * P], ident_f[:])
+                    src = a_t[:]
+                else:
+                    src = acc[(i, j)][:].rearrange("p (t k) -> p t k", t=T)
+                nc.scalar.copy(out=grp_v[:, j], in_=src.rearrange("p t k -> p k t"))
             st["x_res"] = x_res
-            st["grp"] = st2.tile([P, ROWPX, T], BF16, name="grp", align_bytes=64)
-
-        def conv2_turn(i, j):
-            if owner(i, j) != "T":
-                a_t = ps_m.tile([P, T, P], F32, name="a_t", tag="misc")
-                for t in range(T):
-                    nc.tensor.transpose(a_t[:, t, :], acc[(i, j)][:, t * P : (t + 1) * P], ident_f[:])
-                st[j] = a_t[:]
-            else:
-                st[j] = acc[(i, j)][:].rearrange("p (t k) -> p t k", t=T)
-
-        def conv2_round(i, j):
-            grp_v = st["grp"][:].rearrange("p (k b) t -> p b k t", b=CB)
-            nc.scalar.copy(out=grp_v[:, j], in_=st[j].rearrange("p t k -> p k t"))
+            st["grp"] = grp
 
         def conv2_quant(i):
             aq = st2.tile([P, ROWPX], U32, name="aq", align_bytes=64)
@@ -430,7 +604,7 @@ def tile_dcblock_t_kernel(
             st["aq"] = aq
             st["asc"] = asc
 
-        def conv2_pass(i, m):
+        def conv2_out(i, m):
             o_ps = ps_m.tile([P, ROWPX], F32, name="o_ps", tag="misc")
             for c0, c1 in ((0, 256), (256, 384)):
                 nc.tensor.matmul_mx(
@@ -442,67 +616,45 @@ def tile_dcblock_t_kernel(
                     start=True,
                     stop=True,
                 )
-            st[("o", m)] = o_ps
-
-        def conv2_out(i, m):
             o_sb = st2.tile([P, ROWPX], F32, name="o_sb", bufs=3)
-            nc.vector.tensor_tensor(out=o_sb[:], in0=st[("o", m)][:], in1=st["x_res"][:, m, :], op=ALU.add)
-            nc.sync.dma_start(out=out_v[m, :, i, :, :], in_=o_sb[:].rearrange("p (a w) -> p a w", w=W))
+            nc.vector.tensor_tensor(out=o_sb[:], in0=o_ps[:], in1=st["x_res"][:, m, :], op=ALU.add)
+            nc.sync.dma_start(
+                out=out_v[m, :, i : i + (BH - 1) * RB + 1 : RB, :], in_=o_sb[:].rearrange("p (a w) -> p a w", w=W)
+            )
 
         def conv2_chores(i):
-            order = [partial(conv2_load, i), partial(conv2_turn, i, 0)]
-            for j in range(1, CB):
-                order += [partial(conv2_turn, i, j), partial(conv2_round, i, j - 1)]
-            order += [partial(conv2_round, i, CB - 1), None, partial(conv2_quant, i), None, partial(conv2_pass, i, 0)]
-            for m in range(1, T):
-                order += [partial(conv2_pass, i, m), partial(conv2_out, i, m - 1)]
-            return order + [partial(conv2_out, i, T - 1)]
+            return [partial(conv2_gather, i), partial(conv2_quant, i)] + [partial(conv2_out, i, m) for m in range(T)]
 
-        ctx.enter_context(tc.manual_schedule())
-        for f in x_chores(0) + aff_head(0) + [partial(aff_norm, 0)]:
+        for f in aff_head(0) + [partial(aff_norm, 0)] + x_chores(0):
             f()
-        position_pass(0, 0)
-        position_copy(0, 0)
-        position_pass(0, 1)
-
-        def position_job(ip, jp):
-            q = ip * HC + jp
-            if q + 1 < HR * HC:
-                position_copy((q + 1) // HC, (q + 1) % HC)
-            if q + 2 < HR * HC:
-                position_pass((q + 2) // HC, (q + 2) % HC)
-            position_use(ip, jp)
-
-        def spread(items, lo, hi):
-            return [(lo + (hi - lo) * (k + 0.5) / len(items), f) for k, f in enumerate(items)]
-
-        pending = []
-
-        def tensor_slot(ip, i, j):
-            pending.append((ip, i, j, tensor_group(ip, i, j)))
-            if len(pending) > JOIN_LAG:
-                join(*pending.pop(0))
-
         for r in range(HR + 1):
-            plan = []
-            if r < HR:
-                plan += spread([partial(position_job, r, jp) for jp in range(HC)], 0.0, 1.0)
+            jobs = [partial(position_job, r, jp) for jp in range(HC)] if r < HR else []
+            chores = []
             if r + 1 < HR:
-                plan += spread(x_chores(r + 1), 0.0, 0.6)
+                chores += x_chores(r + 1)
             k_next = r // 2 + 1
             if k_next < NPAIR:
-                plan += spread(aff_head(k_next) if r % 2 == 0 else [partial(aff_norm, k_next)], 0.0, 1.0)
+                chores += aff_head(k_next) if r % 2 == 0 else [partial(aff_norm, k_next)]
             if r - 2 * PAD - 2 >= 0:
-                plan += spread(conv2_chores(r - 2 * PAD - 2), 0.0, 1.0)
-            if r > 0:
-                mine = [(i, j) for j in range(CB) for i in rows_of(r - 1)]
-                plan += spread([partial(tensor_slot, r - 1, i, j) for i, j in mine if owner(i, j) == "T"], 0.0, 1.0)
-                plan += spread([partial(gpsimd_group, r - 1, i, j) for i, j in mine if owner(i, j) == "G"], 0.0, 1.0)
-            for place, f in sorted(plan, key=lambda item: item[0]):
-                if f is not None:
+                chores += conv2_chores(r - 2 * PAD - 2)
+            slots = [(i, j) for j in range(CB) for i in rows_of(r - 1) if owner(i, j) != "V"] if r > 0 else []
+            n = max(1, len(slots))
+            waiting = None
+            for k in range(n):
+                for f in jobs[k * len(jobs) // n : (k + 1) * len(jobs) // n]:
                     f()
-            for n in range(len(pending)):
-                join(*pending.pop(0))
+                if k < len(slots):
+                    i, j = slots[k]
+                    if owner(i, j) == "G":
+                        gpsimd_group(r - 1, i, j)
+                    else:
+                        part = tensor_group(r - 1, i, j)
+                        if waiting is not None:
+                            join(*waiting)
+                        waiting = (r - 1, i, j, part)
+                for f in chores[k * len(chores) // n : (k + 1) * len(chores) // n]:
+                    f()
+            if waiting is not None:
+                join(*waiting)
         for f in conv2_chores(RB - 1):
-            if f is not None:
-                f()
+            f()

@@ -7,7 +7,6 @@ from concourse.masks import make_identity
 F32 = mybir.dt.float32
 BF16 = mybir.dt.bfloat16
 I32 = mybir.dt.int32
-U32 = mybir.dt.uint32
 U8 = mybir.dt.uint8
 FP8X4 = mybir.dt.float8_e4m3fn_x4
 ALU = mybir.AluOpType
@@ -21,32 +20,55 @@ H = 96
 W = 96
 KW = 7
 PAD = 3
-RB = 20
-CB = 3
-BH = 4
-BW = W // CB
-HA = BH * RB
-HR = RB + 2 * PAD
-HC = CB + 2 * PAD
 T = 4
-ROWPX = BH * W
-XLEN = PAD + ROWPX + PAD
-XPITCH = 400
-NROWS = H + 2 * PAD
-ZP = W + 2 * PAD
-NPAIR = RB // 2
-AFFW = KW * 2 * KW * CB
-PR = 8
-PC = 16
-HY = PR + 2 * PAD
-HZ = PC + 2 * PAD
-NU = HY * HZ
-KT = 3
-BROWS = H - HA + PAD
-BY = H - HA + 2 * PAD
-OWNER = ("VTV", "TVG", "VTV", "TVT", "VGV", "TVT", "VTV", "GVT")
+TH = 8
+TW = 16
+TR = 9
+TC = W // TW
+NT = TR * TC
+HE = TR * TH
+HALF = TH // 2
+NQ = HALF * TW
+LOW = 64
+VR = HALF + 2 * PAD
+VC = TW + 2 * PAD
+VX = 24
+BR = 6
+BC = 3
+BA = 4
+BW = W // BC
+ROWPX = BA * W
+IR = BR + 2 * PAD
+JC = BC + 2 * PAD
+NPOS = BR * BC
+PITCH = 104
+CH = 16
+CHPX = CH * PITCH
+F_ROW0 = HE - PAD
+V_ROWS = (11, 10, 9, 3, 2, 1, 0)
+COPY_ROWS = (8, 7, 6, 5, 4)
+HZP = W + 2 * PAD
+RING_A = 12
+RING_B = 16
+KB = 6
+LAG = 1
+R0 = 13
 
 FLOPS = 2 * 2 * C * C * H * W + 2 * KW * KW * C * H * W
+
+
+def spread(*lists):
+    order = []
+    for n, items in enumerate(lists):
+        for k, f in enumerate(items):
+            order.append(((k + 0.5) / len(items), n, k, f))
+    order.sort(key=lambda e: e[0:3])
+    return [e[3] for e in order]
+
+
+def run(items):
+    for f in items:
+        f()
 
 
 def tile_dcblock_t_kernel(
@@ -55,606 +77,721 @@ def tile_dcblock_t_kernel(
     nc = tc.nc
     with ExitStack() as ctx:
         const = ctx.enter_context(tc.tile_pool(name="const", bufs=1))
+        ps_msg = ctx.enter_context(tc.psum_pool(name="ps_msg", bufs=3))
+        ps_pos = ctx.enter_context(tc.psum_pool(name="ps_pos", bufs=2))
+        ps_misc = ctx.enter_context(tc.psum_pool(name="ps_misc", bufs=3))
 
         ident_b = const.tile([P, P], BF16, name="ident_b")
         make_identity(nc, ident_b[:])
         ident_f = const.tile([P, P], F32, name="ident_f")
         make_identity(nc, ident_f[:])
-
-        aff = const.tile([P, NPAIR, KW, KW, 2, CB], F32, name="aff")
-        w1q = const.tile([P, C], U32, name="w1q", align_bytes=64)
+        aff_f = const.tile([P, KW, KW, BR, BC], F32, name="aff_f")
+        aff_e = const.tile([P, KW, KW, HALF, TW], F32, name="aff_e")
+        w1q = const.tile([P, C], I32, name="w1q", align_bytes=64)
         w1s = const.tile([P, C], U8, name="w1s", align_bytes=64)
-        w2q = const.tile([P, C], U32, name="w2q", align_bytes=64)
+        w2q = const.tile([P, C], I32, name="w2q", align_bytes=64)
         w2s = const.tile([P, C], U8, name="w2s", align_bytes=64)
         bsc = const.tile([P, T], F32, name="bsc")
         bbi = const.tile([P, T], F32, name="bbi")
         neginv = const.tile([P, 1], F32, name="neginv")
         negone = const.tile([P, 1], F32, name="negone")
-        sel = const.tile([P, 2 * CB], F32, name="sel")
-        vhh = const.tile([P, NPAIR, KW, 2], F32, name="vhh")
-        vww = const.tile([P, KW, 2, CB], F32, name="vww")
-        nat = const.tile([P, NROWS, ZP], BF16, name="nat")
-        xr_tiles = [const.tile([P, T, XPITCH], BF16, name="xr%d" % k) for k in range(2)]
-        nc.vector.memset(nat[:], 0.0)
-        for k in range(2):
-            nc.vector.memset(xr_tiles[k][:], 0.0)
         nc.vector.memset(negone[:], -1.0)
+
         probs = coarse_probs[0]
-        x_v = x[0].rearrange("(t p) h w -> t p h w", p=P)
+        x_k = x[0].rearrange("(p t) h w -> p t h w", t=T)
+        x_r = x[0].rearrange("(t p) h w -> p t h w", p=P)
         out_v = out[0].rearrange("(m p) h w -> m p h w", p=P)
-        for s in range(2):
-            for j in range(CB):
-                g = s * CB + j
-                for c0, c1 in ((0, 16), (16, CP)):
-                    nc.sync.dma_start(
-                        out=nat[CP * g + c0 : CP * g + c1, PAD - s : PAD - s + H, PAD - j : PAD - j + W],
-                        in_=probs[c0:c1, :, :],
-                    )
+        out_s = out[0].rearrange("c h w -> c (h w)")[:, 0 : HE * W].rearrange(
+            "(e b v) (k f) -> e b v k f", e=2, b=2, f=256
+        )
 
-        with tc.tile_pool(name="prep", bufs=1) as prep, tc.psum_pool(name="psw", bufs=1) as psw:
-            prm = prep.tile([P, P], BF16, name="prm")
-            nc.vector.memset(prm[:], 0.0)
-            for k, vec in enumerate((bn_gamma, bn_beta, bn_mean, bn_var)):
-                nc.sync.dma_start(out=prm[T * k : T * k + T, :], in_=vec.rearrange("(t p) -> t p", p=P))
-            prm_t = psw.tile([P, P], BF16, name="prm_t")
-            nc.tensor.transpose(prm_t[:], prm[:], ident_b[:])
-            pf = prep.tile([P, 4 * T], F32, name="pf")
-            nc.vector.tensor_copy(out=pf[:], in_=prm_t[:, 0 : 4 * T])
-            sd = prep.tile([P, T], F32, name="sd")
-            nc.vector.tensor_scalar(out=sd[:], in0=pf[:, 3 * T : 4 * T], scalar1=1e-5, scalar2=None, op0=ALU.add)
-            nc.scalar.activation(out=sd[:], in_=sd[:], func=ACT.Sqrt)
-            nc.vector.reciprocal(out=sd[:], in_=sd[:])
-            nc.vector.tensor_tensor(out=bsc[:], in0=sd[:], in1=pf[:, 0:T], op=ALU.mult)
-            ms = prep.tile([P, T], F32, name="ms")
-            nc.vector.tensor_tensor(out=ms[:], in0=pf[:, 2 * T : 3 * T], in1=bsc[:], op=ALU.mult)
-            nc.vector.tensor_tensor(out=bbi[:], in0=pf[:, T : 2 * T], in1=ms[:], op=ALU.subtract)
-
-            sg = prep.tile([P, 1], BF16, name="sg")
-            nc.sync.dma_start(out=sg[:], in_=sigma.partition_broadcast(P))
-            sf = prep.tile([P, 1], F32, name="sf")
-            nc.vector.tensor_scalar(out=sf[:], in0=sg[:], scalar1=0.0, scalar2=None, op0=ALU.max)
-            nc.vector.tensor_tensor(out=sf[:], in0=sf[:], in1=sf[:], op=ALU.mult)
-            nc.vector.tensor_scalar(out=sf[:], in0=sf[:], scalar1=2.0, scalar2=1e-8, op0=ALU.mult, op1=ALU.add)
-            nc.vector.reciprocal(out=sf[:], in_=sf[:])
-            nc.vector.tensor_scalar(out=neginv[:], in0=sf[:], scalar1=-1.0, scalar2=None, op0=ALU.mult)
-
-            pidx = prep.tile([P, 1], I32, name="pidx")
-            nc.gpsimd.iota(pidx[:], pattern=[[0, 1]], base=0, channel_multiplier=1)
-            bhi = prep.tile([P, 1], I32, name="bhi")
-            nc.vector.tensor_scalar(out=bhi[:], in0=pidx[:], scalar1=5, scalar2=None, op0=ALU.arith_shift_right)
-            bwi = prep.tile([P, 1], I32, name="bwi")
-            nc.vector.tensor_scalar(out=bwi[:], in0=pidx[:], scalar1=BW - 1, scalar2=None, op0=ALU.bitwise_and)
-            rowb = prep.tile([P, 1], F32, name="rowb")
-            nc.vector.tensor_copy(out=rowb[:], in_=bhi[:])
-            nc.vector.tensor_scalar(
-                out=rowb[:], in0=rowb[:], scalar1=float(RB), scalar2=float(-PAD), op0=ALU.mult, op1=ALU.add
-            )
-            colb = prep.tile([P, 1], F32, name="colb")
-            nc.vector.tensor_copy(out=colb[:], in_=bwi[:])
-            nc.vector.tensor_scalar(
-                out=colb[:], in0=colb[:], scalar1=float(CB), scalar2=float(-PAD), op0=ALU.mult, op1=ALU.add
-            )
-            cnt_i = prep.tile([P, HR], I32, name="cnt_i")
-            nc.gpsimd.iota(cnt_i[:], pattern=[[1, HR]], base=0, channel_multiplier=0)
-            cnt = prep.tile([P, HR], F32, name="cnt")
-            nc.vector.tensor_copy(out=cnt[:], in_=cnt_i[:])
-            vh = prep.tile([P, HR], F32, name="vh")
-            vh2 = prep.tile([P, HR], F32, name="vh2")
-            nc.vector.tensor_scalar(
-                out=vh[:], in0=cnt[:], scalar1=rowb[:, 0:1], scalar2=0.0, op0=ALU.add, op1=ALU.is_ge
-            )
-            nc.vector.tensor_scalar(
-                out=vh2[:], in0=cnt[:], scalar1=rowb[:, 0:1], scalar2=float(H - 1), op0=ALU.add, op1=ALU.is_le
-            )
-            nc.vector.tensor_tensor(out=vh[:], in0=vh[:], in1=vh2[:], op=ALU.mult)
-            vw = prep.tile([P, HC], F32, name="vw")
-            vw2 = prep.tile([P, HC], F32, name="vw2")
-            nc.vector.tensor_scalar(
-                out=vw[:], in0=cnt[:, 0:HC], scalar1=colb[:, 0:1], scalar2=0.0, op0=ALU.add, op1=ALU.is_ge
-            )
-            nc.vector.tensor_scalar(
-                out=vw2[:], in0=cnt[:, 0:HC], scalar1=colb[:, 0:1], scalar2=float(W - 1), op0=ALU.add, op1=ALU.is_le
-            )
-            nc.vector.tensor_tensor(out=vw[:], in0=vw[:], in1=vw2[:], op=ALU.mult)
-            for dhi in range(KW):
-                for s in range(2):
-                    nc.vector.tensor_copy(out=vhh[:, :, dhi, s], in_=vh[:, dhi + s : dhi + s + RB - 1 : 2])
-            for dwi in range(KW):
-                for s in range(2):
-                    nc.vector.tensor_copy(out=vww[:, dwi, s, :], in_=vw[:, dwi : dwi + CB])
-            sel_i = prep.tile([P, 2 * CB], I32, name="sel_i")
-            nc.gpsimd.iota(sel_i[:], pattern=[[-CP, 2 * CB]], base=0, channel_multiplier=1)
-            sel_f = prep.tile([P, 2 * CB], F32, name="sel_f")
-            nc.vector.tensor_copy(out=sel_f[:], in_=sel_i[:])
-            sel2 = prep.tile([P, 2 * CB], F32, name="sel2")
-            nc.vector.tensor_scalar(out=sel[:], in0=sel_f[:], scalar1=0.0, scalar2=None, op0=ALU.is_ge)
-            nc.vector.tensor_scalar(out=sel2[:], in0=sel_f[:], scalar1=float(CP - 1), scalar2=None, op0=ALU.is_le)
-            nc.vector.tensor_tensor(out=sel[:], in0=sel[:], in1=sel2[:], op=ALU.mult)
-
-            for wi, (w_dram, wq, wsc) in enumerate(((w_feat, w1q, w1s), (w_fuse, w2q, w2s))):
-                w_sb = prep.tile([P, T, C], BF16, name="w_sb%d" % wi)
-                nc.sync.dma_start(out=w_sb[:], in_=w_dram.rearrange("(a p) c -> p a c", p=P))
-                w_gr = prep.tile([P, C, T], BF16, name="w_gr%d" % wi, align_bytes=64)
-                for a in range(T):
-                    w_t = psw.tile([P, T, P], BF16, name="w_t", bufs=2)
-                    for t in range(T):
-                        nc.tensor.transpose(w_t[:, t, :], w_sb[:, a, t * P : (t + 1) * P], ident_b[:])
-                    nc.vector.tensor_copy(
-                        out=w_gr[:, a * P : (a + 1) * P, :], in_=w_t[:].rearrange("p t o -> p o t")
-                    )
-                nc.vector.quantize_mx(
-                    out=wq[:].bitcast(FP8X4), scales=wsc[:], in_=w_gr[:].rearrange("p o t -> p (o t)")
-                )
-
-        with tc.tile_pool(name="pb", bufs=1) as pb, tc.tile_pool(name="pbw", bufs=2) as pbw, tc.psum_pool(
-            name="psb", bufs=1
-        ) as psb:
-            u_i = pb.tile([P, KT], I32, name="u_i")
-            nc.gpsimd.iota(u_i[:], pattern=[[P, KT]], base=0, channel_multiplier=1)
-            u_f = pb.tile([P, KT], F32, name="u_f")
-            nc.vector.tensor_copy(out=u_f[:], in_=u_i[:])
-            y_f = pb.tile([P, KT], F32, name="y_f")
-            nc.vector.memset(y_f[:], 0.0)
-            for m in range(1, KT * P // HZ + 1):
-                nc.vector.scalar_tensor_tensor(
-                    out=y_f[:], in0=u_f[:], scalar=float(HZ * m), in1=y_f[:], op0=ALU.is_ge, op1=ALU.add
-                )
-            z_f = pb.tile([P, KT], F32, name="z_f")
-            nc.vector.scalar_tensor_tensor(
-                out=z_f[:], in0=y_f[:], scalar=float(-HZ), in1=u_f[:], op0=ALU.mult, op1=ALU.add
-            )
-            yo_i = pb.tile([P, P], I32, name="yo_i")
-            nc.gpsimd.iota(yo_i[:], pattern=[[1, PR], [0, PC]], base=0, channel_multiplier=0)
-            zo_i = pb.tile([P, P], I32, name="zo_i")
-            nc.gpsimd.iota(zo_i[:], pattern=[[0, PR], [1, PC]], base=0, channel_multiplier=0)
-            yo = pb.tile([P, P], F32, name="yo")
-            nc.vector.tensor_copy(out=yo[:], in_=yo_i[:])
-            zo = pb.tile([P, P], F32, name="zo")
-            nc.vector.tensor_copy(out=zo[:], in_=zo_i[:])
-            band = pb.tile([P, KT, P], F32, name="band")
-            side = pb.tile([P, P], F32, name="side")
-            for k in range(KT):
-                first = True
-                for grid, mine in ((yo, y_f), (zo, z_f)):
-                    for bound, op in ((float(-2 * PAD), ALU.is_ge), (0.0, ALU.is_le)):
-                        dst = band[:, k, :] if first else side[:]
-                        nc.vector.tensor_scalar(
-                            out=dst, in0=grid[:], scalar1=mine[:, k : k + 1], scalar2=bound, op0=ALU.subtract, op1=op
-                        )
-                        if not first:
-                            nc.vector.tensor_tensor(out=band[:, k, :], in0=band[:, k, :], in1=side[:], op=ALU.mult)
-                        first = False
-            ones2 = pb.tile([P, 2], F32, name="ones2")
-            nc.vector.memset(ones2[:], 1.0)
-
-            pr_raw = pb.tile([P, BROWS * W], BF16, name="pr_raw")
-            for c0, c1 in ((0, 16), (16, CP)):
-                nc.sync.dma_start(
-                    out=pr_raw[c0:c1, :].rearrange("c (y w) -> c y w", w=W), in_=probs[c0:c1, HA - PAD : H, :]
-                )
-            pv = pb.tile([P, BY, ZP], F32, name="pv")
-            nc.vector.memset(pv[:], 0.0)
-            nc.vector.tensor_copy(
-                out=pv[0:CP, 0:BROWS, PAD : PAD + W], in_=pr_raw[0:CP, :].rearrange("c (y w) -> c y w", w=W)
-            )
-            pa = pb.tile([P, BY, ZP], F32, name="pa")
-            nc.vector.tensor_scalar(out=pa[:], in0=pv[:], scalar1=-2.0, scalar2=None, op0=ALU.mult)
-            sqp = pb.tile([P, BY * ZP], F32, name="sqp")
-            nc.scalar.activation(out=sqp[:], in_=pv[:].rearrange("p y z -> p (y z)"), func=ACT.Square)
-            w_n = pb.tile([P, P], F32, name="w_n")
-            nc.vector.memset(w_n[:], 0.0)
-            nc.vector.memset(w_n[0:32, 32:33], 1.0)
-            nc.vector.memset(w_n[0:32, 64:65], 1.0)
-            pa_f = pa[:].rearrange("p y z -> p (y z)")
-            pv_f = pv[:].rearrange("p y z -> p (y z)")
-            for c0 in range(0, BY * ZP, 512):
-                c1 = min(c0 + 512, BY * ZP)
-                n_ps = psb.tile([P, 512], F32, name="n_ps", tag="g_ps")
-                nc.tensor.matmul(out=n_ps[:, 0 : c1 - c0], lhsT=w_n[:], rhs=sqp[:, c0:c1], start=True, stop=True)
-                nc.vector.tensor_copy(out=pa_f[32:64, c0:c1], in_=n_ps[32:64, 0 : c1 - c0])
-                nc.vector.tensor_copy(out=pv_f[64:96, c0:c1], in_=n_ps[64:96, 0 : c1 - c0])
-            nc.vector.memset(pa[64:96], 1.0)
-            nc.vector.memset(pv[32:64], 1.0)
-
-            xrb = pb.tile([P, T, BROWS * W], BF16, name="xrb")
-            for t in range(T):
-                nc.sync.dma_start(
-                    out=xrb[:, t, :].rearrange("p (y w) -> p y w", w=W), in_=x_v[t, :, HA - PAD : H, :]
-                )
-            xrb_v = xrb[:].rearrange("p t (y w) -> p t y w", w=W)
-            xnb = pb.tile([P, T, BY, ZP], BF16, name="xnb")
-            nc.vector.memset(xnb[:], 0.0)
-            for t in range(T):
-                nc.scalar.activation(
-                    out=xnb[:, t, 0:BROWS, PAD : PAD + W],
-                    in_=xrb_v[:, t],
-                    func=ACT.Identity,
-                    scale=bsc[:, t : t + 1],
-                    bias=bbi[:, t : t + 1],
-                )
-
-            for y0 in range(0, H - HA, PR):
-                for z0 in range(0, W, PC):
-                    xgp = pbw.tile([P, KT * P, T], BF16, name="xgp", align_bytes=64)
-                    nc.vector.memset(xgp[:, NU:, :], 0.0)
-                    nc.vector.tensor_copy(
-                        out=xgp[:, 0:NU, :].rearrange("p (y z) t -> p y z t", z=HZ),
-                        in_=xnb[:, :, y0 : y0 + HY, z0 : z0 + HZ].rearrange("p t y z -> p y z t"),
-                    )
-                    xqp = pbw.tile([P, KT * P], U32, name="xqp", align_bytes=64)
-                    xsp = pbw.tile([P, KT * P], U8, name="xsp", align_bytes=64)
-                    xgp_f = xgp[:].rearrange("p u t -> p (u t)")
-                    for c0, c1 in ((0, 256), (256, 384)):
-                        nc.vector.quantize_mx(
-                            out=xqp[:, c0:c1].bitcast(FP8X4), scales=xsp[:, c0:c1], in_=xgp_f[:, T * c0 : T * c1]
-                        )
-                    m_sb = []
-                    for k in range(KT):
-                        msg = psb.tile([P, C], F32, name="msg", bufs=2)
-                        nc.tensor.matmul_mx(
-                            out=msg[:],
-                            lhsT=xqp[:, k * P : (k + 1) * P].bitcast(FP8X4),
-                            lhsT_scale=xsp[:, k * P : (k + 1) * P],
-                            rhs=w1q[:].bitcast(FP8X4),
-                            rhs_scale=w1s[:],
-                            start=True,
-                            stop=True,
-                        )
-                        m_sb.append(pbw.tile([P, C], F32, name="m_sb%d" % k))
-                        if k == 1:
-                            nc.scalar.copy(out=m_sb[k][:], in_=msg[:])
-                        else:
-                            nc.vector.tensor_copy(out=m_sb[k][:], in_=msg[:])
-                    au = pbw.tile([P, KT * P], F32, name="au")
-                    nc.gpsimd.memset(au[:, NU:], 0.0)
-                    nc.gpsimd.tensor_copy(
-                        out=au[:, 0:NU].rearrange("p (y z) -> p y z", z=HZ), in_=pa[:, y0 : y0 + HY, z0 : z0 + HZ]
-                    )
-                    bv = pbw.tile([P, P], F32, name="bv")
-                    nc.gpsimd.tensor_copy(
-                        out=bv[:].rearrange("p (y z) -> p y z", z=PC),
-                        in_=pv[:, y0 + PAD : y0 + PAD + PR, z0 + PAD : z0 + PAD + PC],
-                    )
-                    d2p = psb.tile([P, KT, P], F32, name="d2p")
-                    for k in range(KT):
-                        nc.tensor.matmul(
-                            out=d2p[:, k, :], lhsT=au[:, k * P : (k + 1) * P], rhs=bv[:], start=True, stop=True
-                        )
-                    e1p = pbw.tile([P, KT * P], F32, name="e1p")
-                    nc.scalar.activation(
-                        out=e1p[:], in_=d2p[:].rearrange("p k v -> p (k v)"), func=ACT.Exp, scale=neginv[:, 0:1]
-                    )
-                    e2p = pbw.tile([P, KT * P], F32, name="e2p")
-                    nc.scalar.activation(out=e2p[:], in_=e1p[:], func=ACT.Exp, bias=negone[:, 0:1])
-                    emp = pbw.tile([P, KT, P], F32, name="emp")
-                    nc.vector.tensor_tensor(
-                        out=emp[:].rearrange("p k v -> p (k v)"),
-                        in0=e2p[:],
-                        in1=band[:].rearrange("p k v -> p (k v)"),
-                        op=ALU.mult,
-                    )
-                    s_ps = psb.tile([P, 2], F32, name="s_ps")
-                    for k in range(KT):
-                        nc.tensor.matmul(
-                            out=s_ps[:], lhsT=emp[:, k, :], rhs=ones2[:], start=(k == 0), stop=(k == KT - 1)
-                        )
-                    g_ps = psb.tile([P, C], F32, name="g_ps")
-                    for k in range(KT):
-                        nc.tensor.matmul(
-                            out=g_ps[:], lhsT=emp[:, k, :], rhs=m_sb[k][:], start=(k == 0), stop=(k == KT - 1)
-                        )
-                    rs = pbw.tile([P, 1], F32, name="rs")
-                    nc.vector.reciprocal(out=rs[:], in_=s_ps[:, 0:1])
-                    agg = pbw.tile([P, C], F32, name="agg")
-                    nc.scalar.activation(out=agg[:], in_=g_ps[:], func=ACT.Copy, scale=rs[:, 0:1])
-                    a_t = psb.tile([P, T, P], F32, name="a_t")
-                    for t in range(T):
-                        nc.tensor.transpose(a_t[:, t, :], agg[:, t * P : (t + 1) * P], ident_f[:])
-                    grp = pbw.tile([P, P, T], BF16, name="grp", align_bytes=64)
-                    nc.vector.tensor_copy(out=grp[:], in_=a_t[:].rearrange("p t v -> p v t"))
-                    aqp = pbw.tile([P, P], U32, name="aqp", align_bytes=64)
-                    asp = pbw.tile([P, P], U8, name="asp", align_bytes=64)
-                    nc.vector.quantize_mx(
-                        out=aqp[:].bitcast(FP8X4), scales=asp[:], in_=grp[:].rearrange("p v t -> p (v t)")
-                    )
-                    o_ps = psb.tile([P, T, P], F32, name="o_ps")
-                    for m in range(T):
-                        nc.tensor.matmul_mx(
-                            out=o_ps[:, m, :],
-                            lhsT=w2q[:, m * P : (m + 1) * P].bitcast(FP8X4),
-                            lhsT_scale=w2s[:, m * P : (m + 1) * P],
-                            rhs=aqp[:].bitcast(FP8X4),
-                            rhs_scale=asp[:],
-                            start=True,
-                            stop=True,
-                        )
-                    o_sb = pbw.tile([P, T, PR, PC], F32, name="o_sb")
-                    nc.vector.tensor_tensor(
-                        out=o_sb[:],
-                        in0=o_ps[:].rearrange("p m (y z) -> p m y z", z=PC),
-                        in1=xrb_v[:, :, PAD + y0 : PAD + y0 + PR, z0 : z0 + PC],
-                        op=ALU.add,
-                    )
-                    for m in range(T):
-                        nc.sync.dma_start(out=out_v[m, :, HA + y0 : HA + y0 + PR, z0 : z0 + PC], in_=o_sb[:, m])
-
-        affp = ctx.enter_context(tc.tile_pool(name="affp", bufs=2))
-        xs = ctx.enter_context(tc.tile_pool(name="xs", bufs=1))
-        msgp = ctx.enter_context(tc.tile_pool(name="msgp", bufs=2 * HC))
-        prodp = ctx.enter_context(tc.tile_pool(name="prodp", bufs=4))
-        accp = ctx.enter_context(tc.tile_pool(name="accp", bufs=9 * CB))
-        st2 = ctx.enter_context(tc.tile_pool(name="st2", bufs=2))
-        ps_v = ctx.enter_context(tc.psum_pool(name="ps_v", bufs=3))
-        ps_a = ctx.enter_context(tc.psum_pool(name="ps_a", bufs=3))
-        ps_m = ctx.enter_context(tc.psum_pool(name="ps_m", bufs=2))
-
-        acc = {}
-        xq_of = {}
-        msgs = {}
-        e_of = {}
-
-        def aff_diff(k, dwi):
-            if dwi == 0:
-                e_of[k] = ps_m.tile([P, KW, KW, 2 * CB], F32, name="d2", tag="misc")
-            d2 = e_of[k]
-            shifted = nat[:, 2 * k : 2 * k + HA, dwi : dwi + W : CB].rearrange("p (a r) b -> p r a b", r=RB)[:, 0:KW]
-            centre = nat[:, 2 * k + PAD : 2 * k + PAD + (BH - 1) * RB + 1 : RB, PAD : PAD + W : CB]
-            diff = affp.tile([P, KW, BH, BW], F32, name="diff")
-            nc.gpsimd.tensor_tensor(
-                out=diff[:], in0=shifted, in1=centre.unsqueeze(1).to_broadcast([P, KW, BH, BW]), op=ALU.subtract
-            )
-            sq = affp.tile([P, KW * P], F32, name="sq")
-            nc.scalar.activation(out=sq[:], in_=diff[:].rearrange("p r a b -> p (r a b)"), func=ACT.Square)
-            for dhi in range(KW):
-                nc.tensor.matmul(
-                    out=d2[:, dhi, dwi, :], lhsT=sq[:, dhi * P : (dhi + 1) * P], rhs=sel[:], start=True, stop=True
-                )
-
-        def aff_exp(k):
-            d2 = e_of[k]
-            e1 = affp.tile([P, AFFW], F32, name="e1")
-            nc.scalar.activation(
-                out=e1[:], in_=d2[:].rearrange("p h w g -> p (h w g)"), func=ACT.Exp, scale=neginv[:, 0:1]
-            )
-            e2 = affp.tile([P, KW, KW, 2, CB], F32, name="e2")
-            nc.scalar.activation(
-                out=e2[:].rearrange("p h w s j -> p (h w s j)"), in_=e1[:], func=ACT.Exp, bias=negone[:, 0:1]
-            )
-            e_of[k] = e2
-
-        def aff_norm(k):
-            e2 = e_of[k]
-            ssum = affp.tile([P, 2, CB], F32, name="ssum")
-            nc.vector.tensor_reduce(out=ssum[:], in_=e2[:].rearrange("p h w s j -> p s j (h w)"), axis=AX.X, op=ALU.add)
-            nc.vector.reciprocal(out=ssum[:], in_=ssum[:])
-            em = affp.tile([P, KW, KW, 2, CB], F32, name="em")
-            nc.vector.tensor_tensor(
-                out=em[:].rearrange("p h w s j -> p h (w s j)"),
-                in0=e2[:].rearrange("p h w s j -> p h (w s j)"),
-                in1=vww[:].rearrange("p w s j -> p (w s j)").unsqueeze(1).to_broadcast([P, KW, KW * 2 * CB]),
-                op=ALU.mult,
-            )
-            for s in range(2):
-                for j in range(CB):
-                    nc.vector.scalar_tensor_tensor(
-                        out=aff[:, k, :, :, s, j],
-                        in0=em[:, :, :, s, j],
-                        scalar=ssum[:, s, j : j + 1],
-                        in1=vhh[:, k, :, s].unsqueeze(2).to_broadcast([P, KW, KW]),
-                        op0=ALU.mult,
-                        op1=ALU.mult,
-                    )
-
-        def aff_head(k):
-            return [partial(aff_diff, k, dwi) for dwi in range(KW)] + [partial(aff_exp, k)]
-
-        def x_load(ip):
-            hrow = ip - PAD
-            a_lo = 1 if hrow < 0 else 0
-            xr = xr_tiles[ip % 2]
-            for t in range(T):
-                nc.sync.dma_start(
-                    out=xr[:, t, PAD + a_lo * W : PAD + BH * W].rearrange("p (a w) -> p a w", w=W),
-                    in_=x_v[t, :, hrow + a_lo * RB : hrow + (BH - 1) * RB + 1 : RB, :],
-                )
-
-        def x_norm(ip):
-            xr = xr_tiles[ip % 2]
-            xn = xs.tile([P, T, XLEN], BF16, name="xn")
-            for t in range(T):
-                nc.scalar.activation(
-                    out=xn[:, t, :],
-                    in_=xr[:, t, 0:XLEN],
-                    func=ACT.Identity,
-                    scale=bsc[:, t : t + 1],
-                    bias=bbi[:, t : t + 1],
-                )
-            xq_of[ip] = xn
-
-        def x_group(ip):
-            xn = xq_of[ip]
-            xg = xs.tile([P, HC, P, T], BF16, name="xg", align_bytes=64)
-            for u in range(HC // CB):
-                nc.scalar.copy(
-                    out=xg[:, CB * u : CB * u + CB],
-                    in_=xn[:, :, CB * u : CB * u + ROWPX].rearrange("p t (k b) -> p b k t", b=CB),
-                )
-            xq_of[ip] = xg
-
-        def x_quant(ip):
-            xg = xq_of[ip][:].rearrange("p b k t -> p (b k t)")
-            xq = xs.tile([P, HC * P], U32, name="xq", bufs=2, align_bytes=64)
-            xsc = xs.tile([P, HC * P], U8, name="xsc", bufs=2, align_bytes=64)
-            for c0, c1 in ((0, 8 * P), (8 * P, 9 * P)):
-                nc.vector.quantize_mx(out=xq[:, c0:c1].bitcast(FP8X4), scales=xsc[:, c0:c1], in_=xg[:, T * c0 : T * c1])
-            xq_of[ip] = (xq, xsc)
-
-        def x_chores(ip):
-            return [partial(f, ip) for f in (x_load, x_norm, x_group, x_quant)]
-
-        def weight(ip, jp, i, j):
-            return aff[:, i // 2, ip - i, jp - j, i % 2, j : j + 1]
-
-        def owner(i, j):
-            return OWNER[i % 8][j]
-
-        def rows_of(ip):
-            return range(max(0, ip - 2 * PAD), min(RB - 1, ip) + 1)
-
-        def position_job(ip, jp):
-            xq, xsc = xq_of[ip]
-            msg = ps_v.tile([P, C], F32, name="msg")
+        def mx_message(words, scales):
+            msg = ps_msg.tile([P, C], F32, name="msg")
             nc.tensor.matmul_mx(
                 out=msg[:],
-                lhsT=xq[:, jp * P : (jp + 1) * P].bitcast(FP8X4),
-                lhsT_scale=xsc[:, jp * P : (jp + 1) * P],
+                lhsT=words.bitcast(FP8X4),
+                lhsT_scale=scales,
                 rhs=w1q[:].bitcast(FP8X4),
                 rhs_scale=w1s[:],
                 start=True,
                 stop=True,
             )
-            m_sb = msgp.tile([P, C], F32, name="m_sb")
-            nc.scalar.copy(out=m_sb[:], in_=msg[:])
-            msgs[(ip, jp)] = m_sb
-            src = m_sb
-            for i in rows_of(ip):
-                for j in range(max(0, jp - 2 * PAD), min(CB - 1, jp) + 1):
-                    if owner(i, j) != "V":
-                        continue
-                    wgt = weight(ip, jp, i, j)
-                    if ip == i and jp == j:
-                        acc[(i, j)] = accp.tile([P, C], F32, name="acc")
-                        nc.vector.tensor_scalar(out=acc[(i, j)][:], in0=src[:], scalar1=wgt, scalar2=None, op0=ALU.mult)
-                    else:
-                        dst = acc[(i, j)]
-                        nc.vector.scalar_tensor_tensor(
-                            out=dst[:], in0=src[:], scalar=wgt, in1=dst[:], op0=ALU.mult, op1=ALU.add
-                        )
-                    src = msg
+            return msg
 
-        def tensor_group(ip, i, j):
-            part = ps_a.tile([P, T, P], F32, name="part")
-            for dwi in range(KW):
-                prod = prodp.tile([P, C], F32, name="prod_s")
-                nc.scalar.activation(
-                    out=prod[:], in_=msgs[(ip, j + dwi)][:], func=ACT.Copy, scale=weight(ip, j + dwi, i, j)
-                )
-                for t in range(T):
-                    nc.tensor.matmul(
-                        out=part[:, t, :],
-                        lhsT=prod[:, t * P : (t + 1) * P],
-                        rhs=ident_f[:],
-                        is_transpose=True,
-                        start=(dwi == 0 and t == 0),
-                        stop=(dwi == KW - 1 and t == T - 1),
-                    )
-            return part
-
-        def join(ip, i, j, part):
-            flat = part[:].rearrange("p t k -> p (t k)")
-            if ip == i:
-                acc[(i, j)] = accp.tile([P, C], F32, name="acc")
-                nc.vector.tensor_copy(out=acc[(i, j)][:], in_=flat)
-            else:
-                dst = acc[(i, j)]
-                nc.vector.tensor_tensor(out=dst[:], in0=flat, in1=dst[:], op=ALU.add)
-
-        def gpsimd_group(ip, i, j):
-            for dwi in range(KW):
-                src = msgs[(ip, j + dwi)]
-                wgt = weight(ip, j + dwi, i, j)
-                if ip == i and dwi == 0:
-                    acc[(i, j)] = accp.tile([P, C], F32, name="acc")
-                    prod = acc[(i, j)]
-                else:
-                    prod = prodp.tile([P, C], F32, name="prod_g", bufs=2)
-                nc.gpsimd.tensor_scalar(out=prod[:], in0=src[:], scalar1=wgt, scalar2=0.0, op0=ALU.mult, op1=ALU.add)
-                if not (ip == i and dwi == 0):
-                    dst = acc[(i, j)]
-                    nc.gpsimd.tensor_tensor(out=dst[:], in0=dst[:], in1=prod[:], op=ALU.add)
-
-        st = {}
-
-        def conv2_gather(i):
-            x_res = st2.tile([P, T, ROWPX], BF16, name="x_res")
+        def add_transposed(pos, src, first, last):
             for t in range(T):
-                nc.sync.dma_start(out=x_res[:, t, :].rearrange("p (a w) -> p a w", w=W), in_=x_v[t, :, i : i + (BH - 1) * RB + 1 : RB, :])
-            grp = st2.tile([P, ROWPX, T], BF16, name="grp", align_bytes=64)
-            grp_v = grp[:].rearrange("p (k b) t -> p b k t", b=CB)
-            for j in range(CB):
-                if owner(i, j) != "T":
-                    a_t = ps_m.tile([P, T, P], F32, name="a_t", tag="misc")
-                    for t in range(T):
-                        nc.tensor.transpose(a_t[:, t, :], acc[(i, j)][:, t * P : (t + 1) * P], ident_f[:])
-                    src = a_t[:]
+                nc.tensor.matmul(
+                    out=pos[:, t, :],
+                    lhsT=src[:, t * P : (t + 1) * P],
+                    rhs=ident_f[:],
+                    is_transpose=True,
+                    start=(first and t == 0),
+                    stop=(last and t == T - 1),
+                )
+
+        def vector_term(pool, accs, key, msg, wgt):
+            if key not in accs:
+                accs[key] = pool.tile([P, C], F32, name="acc")
+                nc.vector.tensor_scalar(out=accs[key][:], in0=msg[:], scalar1=wgt, scalar2=None, op0=ALU.mult)
+            else:
+                dst = accs[key]
+                nc.vector.scalar_tensor_tensor(
+                    out=dst[:], in0=msg[:], scalar=wgt, in1=dst[:], op0=ALU.mult, op1=ALU.add
+                )
+
+        count = [0]
+
+        def product(pool, src, wgt):
+            prod = pool.tile([P, C], F32, name="prod")
+            count[0] += 1
+            if count[0] % 5 in (2, 4):
+                nc.gpsimd.tensor_scalar(out=prod[:], in0=src[:], scalar1=wgt, scalar2=0.0, op0=ALU.mult, op1=ALU.add)
+            else:
+                nc.scalar.activation(out=prod[:], in_=src[:], func=ACT.Copy, scale=wgt)
+            return prod
+
+        def pack_steps(pool, stage, row0, xq, xs, base, r_hi):
+            v0 = max(0, row0)
+            v1 = min(r_hi, row0 + CH)
+            n = (v1 - v0) * W
+            st = {}
+
+            def load():
+                st["x"] = pool.tile([P, T, CH * W], BF16, name="x_in")
+                nc.sync.dma_start(
+                    out=st["x"][:, :, 0:n].rearrange("p t (h w) -> p t h w", w=W), in_=x_k[:, :, v0:v1, :]
+                )
+
+            def norm():
+                st["n"] = pool.tile([P, T, CH * W], BF16, name="x_n")
+                for t in range(T):
+                    nc.vector.tensor_scalar(
+                        out=st["n"][:, t, 0:n],
+                        in0=st["x"][:, t, 0:n],
+                        scalar1=bsc[:, t : t + 1],
+                        scalar2=bbi[:, t : t + 1],
+                        op0=ALU.mult,
+                        op1=ALU.add,
+                    )
+
+            def group(half):
+                rows = stage[:].rearrange("p (r z) t -> p r z t", z=PITCH)
+                a = (v1 - v0) // 2 * half
+                b = (v1 - v0) // 2 if half == 0 else v1 - v0
+                src = st["n"][:, :, a * W : b * W].rearrange("p t (r w) -> p r w t", w=W)
+                dst = rows[:, v0 - row0 + a : v0 - row0 + b, PAD : PAD + W, :]
+                if half == 0:
+                    nc.scalar.copy(out=dst, in_=src)
                 else:
-                    src = acc[(i, j)][:].rearrange("p (t k) -> p t k", t=T)
-                nc.scalar.copy(out=grp_v[:, j], in_=src.rearrange("p t k -> p k t"))
-            st["x_res"] = x_res
-            st["grp"] = grp
+                    nc.vector.tensor_copy(out=dst, in_=src)
 
-        def conv2_quant(i):
-            aq = st2.tile([P, ROWPX], U32, name="aq", align_bytes=64)
-            asc = st2.tile([P, ROWPX], U8, name="asc", align_bytes=64)
-            grp_f = st["grp"][:].rearrange("p k t -> p (k t)")
-            for c0, c1 in ((0, 256), (256, 384)):
-                nc.vector.quantize_mx(
-                    out=aq[:, c0:c1].bitcast(FP8X4), scales=asc[:, c0:c1], in_=grp_f[:, T * c0 : T * c1]
-                )
-            st["aq"] = aq
-            st["asc"] = asc
+            def quant():
+                flat = stage[:].rearrange("p u t -> p (u t)")
+                for c0, c1 in ((0, 1024), (1024, 1536), (1536, CHPX)):
+                    nc.vector.quantize_mx(
+                        out=xq[:, base + c0 : base + c1].bitcast(FP8X4),
+                        scales=xs[:, base + c0 : base + c1],
+                        in_=flat[:, T * c0 : T * c1],
+                    )
 
-        def conv2_out(i, m):
-            o_ps = ps_m.tile([P, ROWPX], F32, name="o_ps", tag="misc")
-            for c0, c1 in ((0, 256), (256, 384)):
-                nc.tensor.matmul_mx(
-                    out=o_ps[:, c0:c1],
-                    lhsT=w2q[:, m * P : (m + 1) * P].bitcast(FP8X4),
-                    lhsT_scale=w2s[:, m * P : (m + 1) * P],
-                    rhs=st["aq"][:, c0:c1].bitcast(FP8X4),
-                    rhs_scale=st["asc"][:, c0:c1],
-                    start=True,
-                    stop=True,
-                )
-            o_sb = st2.tile([P, ROWPX], F32, name="o_sb", bufs=3)
-            nc.vector.tensor_tensor(out=o_sb[:], in0=o_ps[:], in1=st["x_res"][:, m, :], op=ALU.add)
-            nc.sync.dma_start(
-                out=out_v[m, :, i : i + (BH - 1) * RB + 1 : RB, :], in_=o_sb[:].rearrange("p (a w) -> p a w", w=W)
+            return [load, norm, partial(group, 0), partial(group, 1), quant]
+
+        def finish_affinity(pool, aff, nq):
+            flat = aff[:].rearrange("p a b i j -> p (a b i j)")
+            nc.scalar.activation(out=flat, in_=flat, func=ACT.Exp, scale=neginv[:, 0:1])
+            nc.scalar.activation(out=flat, in_=flat, func=ACT.Exp, bias=negone[:, 0:1])
+            ssum = pool.tile([P, nq], F32, name="ssum")
+            nc.vector.tensor_reduce(
+                out=ssum[:], in_=aff[:].rearrange("p a b i j -> p (i j) (a b)"), axis=AX.X, op=ALU.add
+            )
+            nc.vector.reciprocal(out=ssum[:], in_=ssum[:])
+            by_off = aff[:].rearrange("p a b i j -> p (a b) (i j)")
+            nc.vector.tensor_tensor(
+                out=by_off, in0=by_off, in1=ssum[:].unsqueeze(1).to_broadcast([P, KW * KW, nq]), op=ALU.mult
             )
 
-        def conv2_chores(i):
-            return [partial(conv2_gather, i), partial(conv2_quant, i)] + [partial(conv2_out, i, m) for m in range(T)]
+        with ExitStack() as fpool:
+            xqp = fpool.enter_context(tc.tile_pool(name="xqp", bufs=1))
+            xqf = xqp.tile([P, 2 * CHPX], I32, name="xqf", align_bytes=64)
+            xsf = xqp.tile([P, 2 * CHPX], U8, name="xsf", align_bytes=64)
+            p_e = xqp.tile([P, VR, VX, CP], BF16, name="p_e")
 
-        for f in aff_head(0) + [partial(aff_norm, 0)] + x_chores(0):
-            f()
-        for r in range(HR + 1):
-            jobs = [partial(position_job, r, jp) for jp in range(HC)] if r < HR else []
-            chores = []
-            if r + 1 < HR:
-                chores += x_chores(r + 1)
-            k_next = r // 2 + 1
-            if k_next < NPAIR:
-                chores += aff_head(k_next) if r % 2 == 0 else [partial(aff_norm, k_next)]
-            if r - 2 * PAD - 2 >= 0:
-                chores += conv2_chores(r - 2 * PAD - 2)
-            slots = [(i, j) for j in range(CB) for i in rows_of(r - 1) if owner(i, j) != "V"] if r > 0 else []
-            n = max(1, len(slots))
-            waiting = None
-            for k in range(n):
-                for f in jobs[k * len(jobs) // n : (k + 1) * len(jobs) // n]:
-                    f()
-                if k < len(slots):
-                    i, j = slots[k]
-                    if owner(i, j) == "G":
-                        gpsimd_group(r - 1, i, j)
-                    else:
-                        part = tensor_group(r - 1, i, j)
-                        if waiting is not None:
-                            join(*waiting)
-                        waiting = (r - 1, i, j, part)
-                for f in chores[k * len(chores) // n : (k + 1) * len(chores) // n]:
-                    f()
-            if waiting is not None:
-                join(*waiting)
-        for f in conv2_chores(RB - 1):
-            f()
+            with tc.tile_pool(name="head", bufs=1) as head:
+                nat_f = head.tile([P, 30, HZP], BF16, name="nat_f")
+                nat_e = head.tile([P, 78, HZP], BF16, name="nat_e")
+                nc.vector.memset(nat_f[:], 0.0)
+                nc.gpsimd.memset(nat_e[:], 0.0)
+                for nat, lo, hi, y0 in ((nat_f, F_ROW0, H, 0), (nat_e, 0, HE + PAD, PAD)):
+                    for s in range(2):
+                        for j in range(BC):
+                            g = s * BC + j
+                            skip = max(0, s - y0)
+                            for c0, c1 in ((0, 16), (16, CP)):
+                                nc.sync.dma_start(
+                                    out=nat[
+                                        CP * g + c0 : CP * g + c1,
+                                        y0 - s + skip : y0 - s + hi - lo,
+                                        PAD - j : PAD - j + W,
+                                    ],
+                                    in_=probs[c0:c1, lo + skip : hi, :],
+                                )
+
+                prm = []
+                for k, vec in enumerate((bn_gamma, bn_beta, bn_mean, bn_var)):
+                    prm.append(head.tile([P, T], BF16, name="prm%d" % k))
+                    nc.sync.dma_start(out=prm[k][:], in_=vec.rearrange("(p t) -> p t", t=T))
+                sd = head.tile([P, T], F32, name="sd")
+                nc.vector.tensor_scalar(out=sd[:], in0=prm[3][:], scalar1=1e-5, scalar2=None, op0=ALU.add)
+                nc.scalar.activation(out=sd[:], in_=sd[:], func=ACT.Sqrt)
+                nc.vector.reciprocal(out=sd[:], in_=sd[:])
+                nc.vector.tensor_tensor(out=bsc[:], in0=prm[0][:], in1=sd[:], op=ALU.mult)
+                ms = head.tile([P, T], F32, name="ms")
+                nc.vector.tensor_tensor(out=ms[:], in0=prm[2][:], in1=bsc[:], op=ALU.mult)
+                nc.vector.tensor_tensor(out=bbi[:], in0=prm[1][:], in1=ms[:], op=ALU.subtract)
+
+                sg = head.tile([P, 1], BF16, name="sg")
+                nc.sync.dma_start(out=sg[:], in_=sigma.partition_broadcast(P))
+                sf = head.tile([P, 1], F32, name="sf")
+                nc.vector.tensor_scalar(out=sf[:], in0=sg[:], scalar1=0.0, scalar2=None, op0=ALU.max)
+                nc.vector.tensor_tensor(out=sf[:], in0=sf[:], in1=sf[:], op=ALU.mult)
+                nc.vector.tensor_scalar(out=sf[:], in0=sf[:], scalar1=2.0, scalar2=1e-8, op0=ALU.mult, op1=ALU.add)
+                nc.vector.reciprocal(out=sf[:], in_=sf[:])
+                nc.vector.tensor_scalar(out=neginv[:], in0=sf[:], scalar1=-1.0, scalar2=None, op0=ALU.mult)
+
+                p_f = head.tile([P, IR, JC, CP], BF16, name="p_f")
+                gat_f = head.tile([P, IR // 2, BC, P], BF16, name="gat_f")
+                for y2 in range(IR // 2):
+                    for x3 in range(BC):
+                        src = nat_f[:, 2 * y2 : 2 * y2 + BR * (BA - 1) + 1 : BR, BC * x3 : BC * x3 + BC * (BW - 1) + 1 : BC]
+                        dst = gat_f[:, y2, x3, :].rearrange("p (a w) -> p a w", a=BA)
+                        if (y2 + x3) % 2 == 0:
+                            nc.vector.tensor_copy(out=dst, in_=src)
+                        else:
+                            nc.scalar.copy(out=dst, in_=src)
+                for y2 in range(IR // 2):
+                    ps = ps_misc.tile([P, BC, P], BF16, name="ps_p", tag="misc")
+                    for x3 in range(BC):
+                        nc.tensor.transpose(ps[:, x3, :], gat_f[:, y2, x3, :], ident_b[:])
+                    nc.vector.tensor_copy(
+                        out=p_f[:, 2 * y2 : 2 * y2 + 2].rearrange("p s (x j) c -> p s x (j c)", j=BC),
+                        in_=ps[:, :, 0 : 6 * CP].rearrange("p x (s k) -> p s x k", s=2),
+                    )
+
+                stages = [head.tile([P, CHPX, T], BF16, name="stage%d" % k, align_bytes=64) for k in range(2)]
+                for k in range(2):
+                    nc.gpsimd.memset(stages[k][:], 0.0)
+                for k in range(2):
+                    run(pack_steps(head, stages[k], F_ROW0 + k * CH, xqf, xsf, k * CHPX, H))
+
+                for dh in range(KW):
+                    diff = head.tile([P, KW, NPOS * CP + 2], F32, name="diff", bufs=2)
+                    for dw in range(KW):
+                        eng = nc.gpsimd if dw in (1, 3, 5) else nc.vector
+                        eng.tensor_tensor(
+                            out=diff[:, dw, 0 : NPOS * CP].rearrange("p (i k) -> p i k", i=BR),
+                            in0=p_f[:, dh : dh + BR, dw : dw + BC, :].rearrange("p i j c -> p i (j c)"),
+                            in1=p_f[:, PAD : PAD + BR, PAD : PAD + BC, :].rearrange("p i j c -> p i (j c)"),
+                            op=ALU.subtract,
+                        )
+                    flat = diff[:, :, 0 : NPOS * CP]
+                    nc.scalar.activation(out=flat, in_=flat, func=ACT.Square)
+                    nc.vector.tensor_reduce(
+                        out=aff_f[:, dh].rearrange("p d i j -> p d (i j)"),
+                        in_=flat.rearrange("p d (q c) -> p d q c", c=CP),
+                        axis=AX.X,
+                        op=ALU.add,
+                    )
+                finish_affinity(head, aff_f, NPOS)
+
+                for wi, (rows, wq, wsc) in enumerate(
+                    (
+                        (w_feat.rearrange("(p a) c -> p a c", a=T), w1q, w1s),
+                        (w_fuse.rearrange("(a p) c -> p a c", a=T), w2q, w2s),
+                    )
+                ):
+                    w_sb = head.tile([P, T, C], BF16, name="w_sb", bufs=2)
+                    nc.sync.dma_start(out=w_sb[:], in_=rows)
+                    w_gr = head.tile([P, C, T], BF16, name="w_gr", bufs=2, align_bytes=64)
+                    for a in range(T):
+                        w_t = ps_misc.tile([P, T, P], BF16, name="w_t", tag="misc")
+                        for t in range(T):
+                            nc.tensor.transpose(w_t[:, t, :], w_sb[:, a, t : C : T], ident_b[:])
+                        nc.scalar.copy(out=w_gr[:, a * P : (a + 1) * P, :], in_=w_t[:].rearrange("p t o -> p o t"))
+                    nc.vector.quantize_mx(
+                        out=wq[:].bitcast(FP8X4), scales=wsc[:], in_=w_gr[:].rearrange("p o t -> p (o t)")
+                    )
+
+                gat_e = head.tile([P, VR // 2, 8, P], BF16, name="gat_e")
+                nc.gpsimd.memset(gat_e[:], 0.0)
+                for u in range(VR // 2):
+                    for x3 in range(8):
+                        for half in range(2):
+                            y0 = 2 * u + HALF * half
+                            src = nat_e[:, y0 : y0 + TH * (TR - 1) + 1 : TH, BC * x3 : BC * x3 + TW * (TC - 1) + 1 : TW]
+                            dst = gat_e[:, u, x3, LOW * half : LOW * half + NT].rearrange("p (r c) -> p r c", c=TC)
+                            nc.scalar.copy(out=dst, in_=src)
+                for u in range(VR // 2):
+                    for g in range(2):
+                        ps = ps_misc.tile([P, 4, P], BF16, name="ps_p", tag="misc")
+                        for k in range(4):
+                            nc.tensor.transpose(ps[:, k, :], gat_e[:, u, 4 * g + k, :], ident_b[:])
+                        cols = slice(12 * g, 12 * g + 12)
+                        nc.vector.tensor_copy(
+                            out=p_e[0:LOW, 2 * u : 2 * u + 2, cols, :].rearrange("p s (x j) c -> p s x (j c)", j=BC),
+                            in_=ps[0:LOW, :, 0 : 6 * CP].rearrange("p x (s k) -> p s x k", s=2),
+                        )
+                        for s in range(2):
+                            nc.scalar.copy(
+                                out=p_e[LOW:P, 2 * (4 - u) + 1 - s, cols, :].rearrange("p (x j) c -> p x (j c)", j=BC),
+                                in_=ps[LOW:P, :, 3 * CP * s : 3 * CP * (s + 1)],
+                            )
+
+            with ExitStack() as fx:
+                cpool = fx.enter_context(tc.tile_pool(name="cpool", bufs=1))
+                setp = fx.enter_context(tc.tile_pool(name="setp", bufs=3))
+                accp = fx.enter_context(tc.tile_pool(name="accp", bufs=13))
+                prodp = fx.enter_context(tc.tile_pool(name="prodp", bufs=6))
+                dpool = fx.enter_context(tc.tile_pool(name="dpool", bufs=2))
+                st2 = fx.enter_context(tc.tile_pool(name="st2", bufs=2))
+                sets = {}
+                accs = {}
+                copies = {}
+                xqf_v = xqf[:].rearrange("p (r z) -> p r z", z=PITCH)
+                xsf_v = xsf[:].rearrange("p (r z) -> p r z", z=PITCH)
+
+                def f_set(ip):
+                    words = setp.tile([P, JC * P], I32, name="words", align_bytes=64)
+                    scales = setp.tile([P, JC * P], U8, name="scales", align_bytes=64)
+                    for u in range(JC // BC):
+                        for dst, src in ((words, xqf_v), (scales, xsf_v)):
+                            nc.vector.tensor_copy(
+                                out=dst[:, BC * P * u : BC * P * (u + 1)].rearrange("p (b a w) -> p b a w", b=BC, a=BA),
+                                in_=src[:, ip : ip + BR * (BA - 1) + 1 : BR, BC * u : BC * u + W].rearrange(
+                                    "p a (w b) -> p b a w", b=BC
+                                ),
+                            )
+                    sets[ip] = (words, scales)
+
+                def f_message(ip, jp):
+                    words, scales = sets[ip]
+                    return mx_message(words[:, jp * P : (jp + 1) * P], scales[:, jp * P : (jp + 1) * P])
+
+                def f_weight(i, j, ip, jp):
+                    return aff_f[:, ip - i, jp - j, i, j : j + 1]
+
+                def f_vector(ip, jp):
+                    msg = f_message(ip, jp)
+                    for i in range(max(0, ip - 2 * PAD), min(BR - 1, ip) + 1):
+                        for j in range(max(0, jp - 2 * PAD), min(BC - 1, jp) + 1):
+                            vector_term(accp, accs, (i, j), msg, f_weight(i, j, ip, jp))
+
+                def f_copy(ip, jp):
+                    msg = f_message(ip, jp)
+                    copies[(ip, jp)] = cpool.tile([P, C], F32, name="cp%d_%d" % (ip, jp))
+                    nc.scalar.copy(out=copies[(ip, jp)][:], in_=msg[:])
+
+                def f_position(i, j):
+                    st = {}
+                    jobs = []
+                    terms = [(ip, j + dw) for ip in COPY_ROWS if i <= ip <= i + 2 * PAD for dw in range(KW)]
+
+                    def term(k, ip, jp):
+                        if k == 0:
+                            st["pos"] = ps_pos.tile([P, T, P], F32, name="pos")
+                        prod = product(prodp, copies[(ip, jp)], f_weight(i, j, ip, jp))
+                        add_transposed(st["pos"], prod, k == 0, False)
+
+                    def close():
+                        add_transposed(st["pos"], accs.pop((i, j)), False, True)
+                        if j == 0:
+                            grp[i] = st2.tile([P, ROWPX, T], BF16, name="grp", align_bytes=64)
+                        nc.scalar.copy(
+                            out=grp[i][:].rearrange("p (k b) t -> p b k t", b=BC)[:, j],
+                            in_=st["pos"][:].rearrange("p t k -> p k t"),
+                        )
+
+                    for k, (ip, jp) in enumerate(terms):
+                        jobs.append(partial(term, k, ip, jp))
+                    jobs.append(close)
+                    return jobs
+
+                grp = {}
+                f_st = {}
+
+                def f_conv_in(i):
+                    x_res = st2.tile([P, T, ROWPX], BF16, name="x_res")
+                    for t in range(T):
+                        nc.sync.dma_start(
+                            out=x_res[:, t, :].rearrange("p (a w) -> p a w", w=W),
+                            in_=x_r[:, t, HE + i : HE + i + BR * (BA - 1) + 1 : BR, :],
+                        )
+                    aq = st2.tile([P, ROWPX], I32, name="aq", align_bytes=64)
+                    asc = st2.tile([P, ROWPX], U8, name="asc", align_bytes=64)
+                    grp_f = grp.pop(i)[:].rearrange("p k t -> p (k t)")
+                    for c0, c1 in ((0, 256), (256, 384)):
+                        nc.vector.quantize_mx(
+                            out=aq[:, c0:c1].bitcast(FP8X4), scales=asc[:, c0:c1], in_=grp_f[:, T * c0 : T * c1]
+                        )
+                    f_st[i] = (x_res, aq, asc)
+
+                def f_conv_out(i, m):
+                    x_res, aq, asc = f_st[i]
+                    o_ps = ps_misc.tile([P, ROWPX], F32, name="o_ps", tag="misc")
+                    for c0, c1 in ((0, 256), (256, 384)):
+                        nc.tensor.matmul_mx(
+                            out=o_ps[:, c0:c1],
+                            lhsT=w2q[:, m * P : (m + 1) * P].bitcast(FP8X4),
+                            lhsT_scale=w2s[:, m * P : (m + 1) * P],
+                            rhs=aq[:, c0:c1].bitcast(FP8X4),
+                            rhs_scale=asc[:, c0:c1],
+                            start=True,
+                            stop=True,
+                        )
+                    o_sb = st2.tile([P, ROWPX], F32, name="o_sb")
+                    nc.vector.tensor_tensor(out=o_sb[:], in0=o_ps[:], in1=x_res[:, m, :], op=ALU.add)
+                    nc.sync.dma_start(
+                        out=out_v[m, :, HE + i : HE + i + BR * (BA - 1) + 1 : BR, :],
+                        in_=o_sb[:].rearrange("p (a w) -> p a w", w=W),
+                    )
+
+                def f_conv(i):
+                    return [partial(f_conv_in, i)] + [partial(f_conv_out, i, m) for m in range(T)]
+
+                def e_distance(dh, dw):
+                    diff = dpool.tile([P, NQ, CP], F32, name="diff")
+                    nc.gpsimd.tensor_tensor(
+                        out=diff[:].rearrange("p (y x) c -> p y (x c)", y=HALF),
+                        in0=p_e[:, dh : dh + HALF, dw : dw + TW, :].rearrange("p y x c -> p y (x c)"),
+                        in1=p_e[:, PAD : PAD + HALF, PAD : PAD + TW, :].rearrange("p y x c -> p y (x c)"),
+                        op=ALU.subtract,
+                    )
+                    flat = diff[:].rearrange("p q c -> p (q c)")
+                    nc.scalar.activation(out=flat, in_=flat, func=ACT.Square)
+                    nc.vector.tensor_reduce(
+                        out=aff_e[:, dh, dw].rearrange("p y x -> p (y x)"), in_=diff[:], axis=AX.X, op=ALU.add
+                    )
+
+                distances = [partial(e_distance, dh, dw) for dh in range(KW) for dw in range(KW)]
+
+                v_jobs = []
+                for ip in V_ROWS:
+                    v_jobs.append([partial(f_set, ip)] + [partial(f_vector, ip, jp) for jp in range(JC)])
+                c_jobs = []
+                for ip in COPY_ROWS:
+                    c_jobs += [partial(f_set, ip)] + [partial(f_copy, ip, jp) for jp in range(JC)]
+
+                def f_row(i):
+                    return sum([f_position(i, j) for j in range(BC)], [])
+
+                run(spread(sum(v_jobs[0:3], []), c_jobs, distances[0:20]))
+                run(spread(v_jobs[3], f_row(5) + f_row(4), distances[20:30]))
+                run(spread(v_jobs[4], f_row(3), f_conv(5) + f_conv(4), distances[30:37]))
+                run(spread(v_jobs[5], f_row(2), f_conv(3), distances[37:43]))
+                run(spread(v_jobs[6], f_row(1), f_conv(2), distances[43:49]))
+                run(spread(f_row(0), f_conv(1), [partial(finish_affinity, dpool, aff_e, NQ)]))
+                run(f_conv(0))
+
+        with ExitStack() as ex:
+            xep = ex.enter_context(tc.tile_pool(name="xep", bufs=1))
+            vset = ex.enter_context(tc.tile_pool(name="vset", bufs=4))
+            xqe = xep.tile([P, 5 * CHPX], I32, name="xqe", align_bytes=64)
+            xse = xep.tile([P, 5 * CHPX], U8, name="xse", align_bytes=64)
+            xqe_v = xqe[:].rearrange("p (r z) -> p r z", z=PITCH)
+            xse_v = xse[:].rearrange("p (r z) -> p r z", z=PITCH)
+            ring = []
+            free = []
+
+            def add_ring(pool, n):
+                for k in range(len(ring), len(ring) + n):
+                    ring.append(pool.tile([P, C], F32, name="ring%d" % k))
+                    nc.gpsimd.memset(ring[k][:], 0.0)
+                    free.append(k)
+
+            add_ring(xep, RING_A)
+            ready = []
+            e_acc = {}
+            e_dn = {}
+
+            def take():
+                return free.pop(0)
+
+            def e_set(r, k0, k1):
+                n = k1 - k0
+                words = vset.tile([P, KB, P], I32, name="words", align_bytes=64)
+                scales = vset.tile([P, KB, P], U8, name="scales", align_bytes=64)
+                base = 0 if k1 <= TW else 8
+                for dst, src in ((words, xqe_v), (scales, xse_v)):
+                    nc.vector.memset(dst[:, 0:n].rearrange("p k (h x) -> p k h x", h=2)[:, :, :, NT:LOW], 0)
+                    for half in range(2):
+                        s0 = r + PAD if half == 0 else TH - 1 - r + PAD
+                        nc.vector.tensor_copy(
+                            out=dst[:, 0:n, LOW * half : LOW * half + NT].rearrange("p k (r c) -> p k r c", c=TC),
+                            in_=src[:, s0 : s0 + TH * (TR - 1) + 1 : TH, base : base + W].rearrange(
+                                "p r (c x) -> p x r c", x=TW
+                            )[:, k0 - base : k1 - base],
+                        )
+                return [(words[:, k], scales[:, k]) for k in range(n)]
+
+            def e_weight(y, x, r, k):
+                return aff_e[:, r - y + PAD, k - x, y, x : x + 1]
+
+            def e_vector_term(y, x, r, k, msg):
+                wgt = e_weight(y, x, r, k)
+                if (y, x) not in e_acc and ready:
+                    load_own(y, x)
+                if (y, x) not in e_acc:
+                    e_acc[(y, x)] = take()
+                    dst = ring[e_acc[(y, x)]]
+                    nc.vector.tensor_scalar(out=dst[:], in0=msg[:], scalar1=wgt, scalar2=None, op0=ALU.mult)
+                else:
+                    dst = ring[e_acc[(y, x)]]
+                    nc.vector.scalar_tensor_tensor(
+                        out=dst[:], in0=msg[:], scalar=wgt, in1=dst[:], op0=ALU.mult, op1=ALU.add
+                    )
+
+            side_sets = {}
+
+            def side_set(r, k0):
+                side_sets[(r, k0)] = e_set(r, k0, k0 + PAD)
+
+            def side_message(r, k0, k):
+                msg = mx_message(*side_sets[(r, k0)][k - k0])
+                for y in range(max(0, r - PAD), min(HALF - 1, r + PAD) + 1):
+                    for x in range(max(0, k - 2 * PAD), min(TW - 1, k) + 1):
+                        e_vector_term(y, x, r, k, msg)
+
+            def side_jobs(k0):
+                jobs = []
+                for r in range(HALF + PAD):
+                    jobs.append(partial(side_set, r, k0))
+                    jobs += [partial(side_message, r, k0, k) for k in range(k0, k0 + PAD)]
+                return jobs
+
+            with tc.tile_pool(name="dense", bufs=1) as dense:
+                stages = [dense.tile([P, CHPX, T], BF16, name="stage%d" % k, align_bytes=64) for k in range(2)]
+                for k in range(2):
+                    nc.gpsimd.memset(stages[k][:], 0.0)
+                packs = []
+                for k in range(5):
+                    packs += pack_steps(dense, stages[k % 2], k * CH - PAD, xqe, xse, k * CHPX, HE + PAD)
+
+                aff_t = dense.tile([P, KW, KW, HALF, TW], F32, name="aff_t")
+                mat = dense.tile([P, NT, 2, NQ], F32, name="mat")
+
+                def mask_columns():
+                    nc.vector.tensor_copy(
+                        out=aff_t[:].rearrange("p a b y x -> p (a b y x)"),
+                        in_=aff_e[:].rearrange("p a b y x -> p (a b y x)"),
+                    )
+                    for dw in range(KW):
+                        if dw < PAD:
+                            nc.vector.memset(aff_t[:, :, dw, :, 0 : PAD - dw], 0.0)
+                        if dw > PAD:
+                            nc.vector.memset(aff_t[:, :, dw, :, TW + PAD - dw : TW], 0.0)
+
+                rows = {}
+
+                def spread_row(y):
+                    m = dense.tile([P, 64 + TW * P + 160], F32, name="rowmat", bufs=2)
+                    nc.gpsimd.memset(m[:], 0.0)
+                    for dh in range(PAD - y, KW):
+                        r = y + dh - PAD
+                        for half in range(2):
+                            lo, hi = LOW * half, LOW * half + LOW
+                            s = 64 + TW * (r if half == 0 else TH - 1 - r) - PAD
+                            dst = m[lo:hi, s : s + TW * (P + 1)].rearrange("p (x e) -> p x e", e=P + 1)[:, :, 0:KW]
+                            nc.vector.tensor_copy(out=dst, in_=aff_t[lo:hi, dh, :, y, :].rearrange("p d x -> p x d"))
+                    rows[y] = m
+
+                def turn(y, g):
+                    ps = ps_misc.tile([P, 4, P], F32, name="ps_m", tag="misc")
+                    for k in range(4):
+                        a = 64 + (4 * g + k) * P
+                        nc.tensor.transpose(ps[:, k, :], rows[y][:, a : a + P], ident_f[:])
+                    q0 = TW * y + 4 * g
+                    src = ps[:].rearrange("p q (h n) -> p h n q", h=2)
+                    for half in range(2):
+                        dst = mat[:, :, half, q0 : q0 + 4]
+                        if half == 0:
+                            nc.scalar.copy(out=dst, in_=src[:, half, 0:NT])
+                        else:
+                            nc.vector.tensor_copy(out=dst, in_=src[:, half, 0:NT])
+
+                own = {}
+
+                def own_set(tr):
+                    words = dense.tile([P, TC, P], I32, name="own_w", bufs=2, align_bytes=64)
+                    scales = dense.tile([P, TC, P], U8, name="own_s", bufs=2, align_bytes=64)
+                    for dst, src in ((words, xqe_v), (scales, xse_v)):
+                        nc.vector.tensor_copy(
+                            out=dst[:].rearrange("p c (r x) -> p c r x", x=TW),
+                            in_=src[:, TH * tr + PAD : TH * tr + PAD + TH, PAD : PAD + W].rearrange(
+                                "p r (c x) -> p c r x", x=TW
+                            ),
+                        )
+                    own[tr] = (words, scales)
+
+                def own_message(n):
+                    words, scales = own[n // TC]
+                    msg = mx_message(words[:, n % TC], scales[:, n % TC])
+                    own_m[n] = dense.tile([P, C], F32, name="own_m", bufs=3)
+                    nc.scalar.copy(out=own_m[n][:], in_=msg[:])
+
+                def own_sum(n):
+                    ps = ps_misc.tile([P, C], F32, name="own_ps", tag="misc")
+                    nc.tensor.matmul(
+                        out=ps[:],
+                        lhsT=mat[:, n].rearrange("p h q -> p (h q)"),
+                        rhs=own_m.pop(n)[:],
+                        start=True,
+                        stop=True,
+                    )
+                    res = dense.tile([P, C], F32, name="own_o", bufs=3)
+                    nc.scalar.copy(out=res[:], in_=ps[:])
+                    nc.sync.dma_start(
+                        out=out_s[:, n // 27, :, n % 27, :].rearrange("e v f -> v e f"),
+                        in_=res[:].rearrange("p (e f) -> p e f", e=2),
+                    )
+
+                own_m = {}
+                mats = [mask_columns]
+                for y in range(HALF):
+                    mats += [partial(spread_row, y)] + [partial(turn, y, g) for g in range(TW // 4)]
+                owns = []
+                for tr in range(TR):
+                    owns.append(partial(own_set, tr))
+                    for n in range(tr * TC, tr * TC + TC):
+                        owns.append(partial(own_message, n))
+                        if n > 0:
+                            owns.append(partial(own_sum, n - 1))
+                owns.append(partial(own_sum, NT - 1))
+                left = side_jobs(0)
+                run(spread(packs, mats))
+                run(spread(owns, left))
+
+            gpool = ex.enter_context(tc.tile_pool(name="gpool", bufs=1))
+            grp_e = gpool.tile([P, HE * W, T], BF16, name="grp_e", align_bytes=64)
+            add_ring(gpool, RING_B)
+            with ExitStack() as e2:
+                prodp = e2.enter_context(tc.tile_pool(name="prode", bufs=6))
+                cpe = e2.enter_context(tc.tile_pool(name="cpe", bufs=8))
+                row_sets = {}
+                copies = {}
+
+                ready.append(True)
+
+                def load_own(y, x):
+                    where = e_dn if (y, x) in e_acc else e_acc
+                    where[(y, x)] = take()
+                    dst = ring[where[(y, x)]]
+                    for half in range(2):
+                        v = NQ * half + TW * y + x
+                        for b in range(2):
+                            p0 = LOW * half + 27 * b
+                            nc.sync.dma_start(
+                                out=dst[p0 : p0 + 27, :].rearrange("p (e f) -> p e f", e=2),
+                                in_=out_s[:, b, v, :, :].rearrange("e k f -> k e f"),
+                            )
+
+                def row_set(r, k0):
+                    for k, ws in enumerate(e_set(r, k0, min(k0 + KB, VC))):
+                        row_sets[(r, k0 + k)] = ws
+
+                def far_message(k):
+                    msg = mx_message(*row_sets.pop((-3, k)))
+                    for x in range(max(0, k - 2 * PAD), min(TW - 1, k) + 1):
+                        e_vector_term(0, x, -3, k, msg)
+
+                def mid_message(k):
+                    msg = mx_message(*row_sets.pop((-2, k)))
+                    copies[(-2, k)] = cpe.tile([P, C], F32, name="cp_mid")
+                    nc.scalar.copy(out=copies[(-2, k)][:], in_=msg[:])
+                    for x in range(max(0, k - 2 * PAD), min(TW - 1, k) + 1):
+                        e_vector_term(1, x, -2, k, msg)
+
+                def near_message(k):
+                    msg = mx_message(*row_sets.pop((-1, k)))
+                    copies[(-1, k)] = cpe.tile([P, C], F32, name="cp_near")
+                    nc.scalar.copy(out=copies[(-1, k)][:], in_=msg[:])
+
+                def e_position(y, x):
+                    st = {}
+                    jobs = []
+                    terms = [(r, x + dw) for r in (-1, -2) if r >= y - PAD and not (y == 1 and r == -2) for dw in range(KW)]
+
+                    def term(n, r, k):
+                        if n == 0:
+                            st["pos"] = ps_pos.tile([P, T, P], F32, name="pos")
+                        prod = product(prodp, copies[(r, k)], e_weight(y, x, r, k))
+                        add_transposed(st["pos"], prod, n == 0, False)
+
+                    def close():
+                        if not terms:
+                            st["pos"] = ps_pos.tile([P, T, P], F32, name="pos")
+                        rest = [d.pop((y, x)) for d in (e_dn, e_acc) if (y, x) in d]
+                        for n, k in enumerate(rest):
+                            add_transposed(st["pos"], ring[k], not terms and n == 0, n == len(rest) - 1)
+                            free.append(k)
+                        for half in range(2):
+                            r = y if half == 0 else TH - 1 - y
+                            nc.scalar.copy(
+                                out=grp_e[:].rearrange("p (a r c x) t -> p a r c x t", r=TH, c=TC, x=TW)[:, :, r, :, x, :],
+                                in_=st["pos"][:, :, LOW * half : LOW * half + NT].rearrange("p t (a c) -> p a c t", c=TC),
+                            )
+
+                    for n, (r, k) in enumerate(terms):
+                        jobs.append(partial(term, n, r, k))
+                    jobs.append(close)
+                    return jobs
+
+                right = side_jobs(VC - PAD)
+                for k in range(VC + LAG):
+                    v_list = []
+                    if k < VC:
+                        if k % KB == 0:
+                            v_list += [partial(row_set, r, k) for r in (-3, -2, -1)]
+                        v_list += [partial(far_message, k), partial(mid_message, k), partial(near_message, k)]
+                    if R0 <= k < 19:
+                        v_list += right[len(right) * (k - R0) // (19 - R0) : len(right) * (k - R0 + 1) // (19 - R0)]
+                    x_pos = k - 2 * PAD - LAG
+                    p_list = []
+                    if 0 <= x_pos < TW:
+                        p_list = [partial(load_own, y, x_pos) for y in range(HALF) if x_pos < PAD or (y, x_pos) not in e_acc]
+                        for y in range(HALF):
+                            p_list += e_position(y, x_pos)
+                    lists = [a for a in (v_list, p_list) if a]
+                    run(spread(*lists))
+
+            with tc.tile_pool(name="tail", bufs=2) as tail:
+                npx = TH * W
+                for tr in range(TR):
+                    x_res = tail.tile([P, T, npx], BF16, name="x_res")
+                    nc.sync.dma_start(
+                        out=x_res[:].rearrange("p t (h w) -> p t h w", w=W), in_=x_r[:, :, TH * tr : TH * tr + TH, :]
+                    )
+                    aq = tail.tile([P, npx], I32, name="aq", align_bytes=64)
+                    asc = tail.tile([P, npx], U8, name="asc", align_bytes=64)
+                    flat = grp_e[:, tr * npx : (tr + 1) * npx, :].rearrange("p u t -> p (u t)")
+                    for c0, c1 in ((0, 512), (512, 768)):
+                        nc.vector.quantize_mx(
+                            out=aq[:, c0:c1].bitcast(FP8X4), scales=asc[:, c0:c1], in_=flat[:, T * c0 : T * c1]
+                        )
+                    for m in range(T):
+                        o_sb = tail.tile([P, npx], F32, name="o_sb")
+                        for c0, c1 in ((0, 512), (512, 768)):
+                            o_ps = ps_misc.tile([P, c1 - c0], F32, name="o_ps", tag="misc")
+                            nc.tensor.matmul_mx(
+                                out=o_ps[:],
+                                lhsT=w2q[:, m * P : (m + 1) * P].bitcast(FP8X4),
+                                lhsT_scale=w2s[:, m * P : (m + 1) * P],
+                                rhs=aq[:, c0:c1].bitcast(FP8X4),
+                                rhs_scale=asc[:, c0:c1],
+                                start=True,
+                                stop=True,
+                            )
+                            nc.vector.tensor_tensor(
+                                out=o_sb[:, c0:c1], in0=o_ps[:], in1=x_res[:, m, c0:c1], op=ALU.add
+                            )
+                        nc.sync.dma_start(
+                            out=out_v[m, :, TH * tr : TH * tr + TH, :], in_=o_sb[:].rearrange("p (h w) -> p h w", w=W)
+                        )

@@ -30,10 +30,13 @@ HE = TR * TH
 HALF = TH // 2
 NQ = HALF * TW
 LOW = 64
+NS = 3
+S_ROW = H - HALF
+NTS = NT + NS
 VR = HALF + 2 * PAD
 VC = TW + 2 * PAD
 VX = 24
-BR = 6
+BR = 5
 BC = 3
 BA = 4
 BW = W // BC
@@ -41,18 +44,26 @@ ROWPX = BA * W
 IR = BR + 2 * PAD
 JC = BC + 2 * PAD
 NPOS = BR * BC
+BI = BW + 2 * PAD // BC
 PITCH = 104
 CH = 16
 CHPX = CH * PITCH
 F_ROW0 = HE - PAD
-V_ROWS = (11, 10, 9, 3, 2, 1, 0)
-COPY_ROWS = (8, 7, 6, 5, 4)
+S_ROW0 = S_ROW - 6
+S_BASE = 5 * CH
 HZP = W + 2 * PAD
-RING_A = 12
-RING_B = 16
-KB = 6
-LAG = 1
-R0 = 13
+MUL_ROWS = (6, 5, 4, 3)
+VEC_TOO = {3: (4, 3, 2), 6: (0,)}
+ROUNDS = ((4, 3), (2, 1), (0,))
+AHEAD = 0.12
+DIST_PART = 0.9
+CONV_LATE = 8
+RINGS = (12, 8, 16)
+KB = 3
+ROWMATS = 2
+FIRST = 4
+PRE = 1
+RIGHT = ((12, 17, (2, 3)), (17, 21, (0, 1)))
 
 FLOPS = 2 * 2 * C * C * H * W + 2 * KW * KW * C * H * W
 
@@ -62,12 +73,51 @@ def spread(*lists):
     for n, items in enumerate(lists):
         for k, f in enumerate(items):
             order.append(((k + 0.5) / len(items), n, k, f))
-    order.sort(key=lambda e: e[0:3])
-    return [e[3] for e in order]
+    return [e[3] for e in sorted(order, key=lambda e: e[0:3])]
 
 
-def run(items):
-    for f in items:
+def late(positions):
+    jobs = []
+    for n in range(len(positions) + 2):
+        terms = positions[n][0] if n < len(positions) else []
+        if n >= 2:
+            jobs.append(positions[n - 2][2])
+        jobs += terms[0 : len(terms) // 2]
+        if 1 <= n <= len(positions):
+            jobs.append(positions[n - 1][1])
+        jobs += terms[len(terms) // 2 :]
+    return jobs
+
+
+def interleave(streams, lead=None):
+    total = [max(0.001, sum([e[0] for e in jobs])) for jobs in streams]
+    done = [0 for jobs in streams]
+    at = [0 for jobs in streams]
+
+    def emit(s):
+        size, need, job = streams[s][at[s]]
+        at[s] += 1
+        while at[0] < need:
+            emit(0)
+        job()
+        done[s] += size
+
+    def place(s):
+        return ((done[s] + streams[s][at[s]][0] / 2) / total[s] - (lead[s] if lead else 0), s)
+
+    while True:
+        rest = [s for s in range(len(streams)) if at[s] < len(streams[s])]
+        if not rest:
+            return
+        emit(min(rest, key=place))
+
+
+def plain(jobs):
+    return [(1, 0, f) for f in jobs]
+
+
+def run(jobs):
+    for f in jobs:
         f()
 
 
@@ -78,14 +128,13 @@ def tile_dcblock_t_kernel(
     with ExitStack() as ctx:
         const = ctx.enter_context(tc.tile_pool(name="const", bufs=1))
         ps_msg = ctx.enter_context(tc.psum_pool(name="ps_msg", bufs=3))
-        ps_pos = ctx.enter_context(tc.psum_pool(name="ps_pos", bufs=2))
-        ps_misc = ctx.enter_context(tc.psum_pool(name="ps_misc", bufs=3))
+        ps_pos = ctx.enter_context(tc.psum_pool(name="ps_pos", bufs=3))
+        ps_misc = ctx.enter_context(tc.psum_pool(name="ps_misc", bufs=2))
 
         ident_b = const.tile([P, P], BF16, name="ident_b")
         make_identity(nc, ident_b[:])
         ident_f = const.tile([P, P], F32, name="ident_f")
         make_identity(nc, ident_f[:])
-        aff_f = const.tile([P, KW, KW, BR, BC], F32, name="aff_f")
         aff_e = const.tile([P, KW, KW, HALF, TW], F32, name="aff_e")
         w1q = const.tile([P, C], I32, name="w1q", align_bytes=64)
         w1s = const.tile([P, C], U8, name="w1s", align_bytes=64)
@@ -94,6 +143,7 @@ def tile_dcblock_t_kernel(
         bsc = const.tile([P, T], F32, name="bsc")
         bbi = const.tile([P, T], F32, name="bbi")
         neginv = const.tile([P, 1], F32, name="neginv")
+        twoinv = const.tile([P, 1], F32, name="twoinv")
         negone = const.tile([P, 1], F32, name="negone")
         nc.vector.memset(negone[:], -1.0)
 
@@ -101,12 +151,12 @@ def tile_dcblock_t_kernel(
         x_k = x[0].rearrange("(p t) h w -> p t h w", t=T)
         x_r = x[0].rearrange("(t p) h w -> p t h w", p=P)
         out_v = out[0].rearrange("(m p) h w -> m p h w", p=P)
-        out_s = out[0].rearrange("c h w -> c (h w)")[:, 0 : HE * W].rearrange(
-            "(e b v) (k f) -> e b v k f", e=2, b=2, f=256
-        )
+        out_c = out[0].rearrange("c h w -> c (h w)")
+        park = out_c[:, 0 : HE * W].rearrange("(e v) (n f) -> e v n f", v=P, f=P)
+        park_s = out_c[:, S_ROW * W : H * W].rearrange("(e v) (n f) -> e v n f", v=P, f=P)
 
-        def mx_message(words, scales):
-            msg = ps_msg.tile([P, C], F32, name="msg")
+        def mx_message(words, scales, pool, tag):
+            msg = pool.tile([P, C], F32, name="msg", tag=tag)
             nc.tensor.matmul_mx(
                 out=msg[:],
                 lhsT=words.bitcast(FP8X4),
@@ -129,45 +179,37 @@ def tile_dcblock_t_kernel(
                     stop=(last and t == T - 1),
                 )
 
-        def vector_term(pool, accs, key, msg, wgt):
-            if key not in accs:
-                accs[key] = pool.tile([P, C], F32, name="acc")
-                nc.vector.tensor_scalar(out=accs[key][:], in0=msg[:], scalar1=wgt, scalar2=None, op0=ALU.mult)
+        def vector_term(dst, first, msg, wgt):
+            if first:
+                nc.vector.tensor_scalar(out=dst[:], in0=msg[:], scalar1=wgt, scalar2=None, op0=ALU.mult)
             else:
-                dst = accs[key]
                 nc.vector.scalar_tensor_tensor(
                     out=dst[:], in0=msg[:], scalar=wgt, in1=dst[:], op0=ALU.mult, op1=ALU.add
                 )
 
-        count = [0]
-
         def product(pool, src, wgt):
             prod = pool.tile([P, C], F32, name="prod")
-            count[0] += 1
-            if count[0] % 5 in (2, 4):
-                nc.gpsimd.tensor_scalar(out=prod[:], in0=src[:], scalar1=wgt, scalar2=0.0, op0=ALU.mult, op1=ALU.add)
-            else:
-                nc.scalar.activation(out=prod[:], in_=src[:], func=ACT.Copy, scale=wgt)
+            nc.scalar.activation(out=prod[:], in_=src[:], func=ACT.Copy, scale=wgt)
             return prod
 
-        def pack_steps(pool, stage, row0, xq, xs, base, r_hi):
+        def pack_steps(pool, stage, row0, r_hi, xq, xs, base, by_blocks, clear):
             v0 = max(0, row0)
             v1 = min(r_hi, row0 + CH)
-            n = (v1 - v0) * W
+            n = v1 - v0
+            rows = stage[:].rearrange("p (r z) t -> p r z t", z=PITCH)
             st = {}
 
             def load():
-                st["x"] = pool.tile([P, T, CH * W], BF16, name="x_in")
+                st["x"] = pool.tile([P, T, CH * W], BF16, name="x_in", bufs=2)
                 nc.sync.dma_start(
-                    out=st["x"][:, :, 0:n].rearrange("p t (h w) -> p t h w", w=W), in_=x_k[:, :, v0:v1, :]
+                    out=st["x"][:, :, 0 : n * W].rearrange("p t (h w) -> p t h w", w=W), in_=x_k[:, :, v0:v1, :]
                 )
 
             def norm():
-                st["n"] = pool.tile([P, T, CH * W], BF16, name="x_n")
                 for t in range(T):
                     nc.vector.tensor_scalar(
-                        out=st["n"][:, t, 0:n],
-                        in0=st["x"][:, t, 0:n],
+                        out=st["x"][:, t, 0 : n * W],
+                        in0=st["x"][:, t, 0 : n * W],
                         scalar1=bsc[:, t : t + 1],
                         scalar2=bbi[:, t : t + 1],
                         op0=ALU.mult,
@@ -175,17 +217,20 @@ def tile_dcblock_t_kernel(
                     )
 
             def group(half):
-                rows = stage[:].rearrange("p (r z) t -> p r z t", z=PITCH)
-                a = (v1 - v0) // 2 * half
-                b = (v1 - v0) // 2 if half == 0 else v1 - v0
-                src = st["n"][:, :, a * W : b * W].rearrange("p t (r w) -> p r w t", w=W)
-                dst = rows[:, v0 - row0 + a : v0 - row0 + b, PAD : PAD + W, :]
-                if half == 0:
-                    nc.scalar.copy(out=dst, in_=src)
-                else:
-                    nc.vector.tensor_copy(out=dst, in_=src)
+                a = n // 2 * half
+                b = n // 2 if half == 0 else n
+                src = st["x"][:, :, a * W : b * W].rearrange("p t (r w) -> p r w t", w=W)
+                dst = rows[:, v0 - row0 + a : v0 - row0 + b]
+                if not by_blocks:
+                    nc.vector.tensor_copy(out=dst[:, :, PAD : PAD + W, :], in_=src)
+                    return
+                for k in range(BC):
+                    eng_copy = nc.vector.tensor_copy if k == 0 else nc.scalar.copy
+                    eng_copy(out=dst[:, :, BI * k + 1 : BI * k + 1 + BW, :], in_=src[:, :, k:W:BC, :])
 
             def quant():
+                if clear:
+                    nc.vector.memset(rows[:, n:CH, :, :], 0.0)
                 flat = stage[:].rearrange("p u t -> p (u t)")
                 for c0, c1 in ((0, 1024), (1024, 1536), (1536, CHPX)):
                     nc.vector.quantize_mx(
@@ -196,9 +241,19 @@ def tile_dcblock_t_kernel(
 
             return [load, norm, partial(group, 0), partial(group, 1), quant]
 
+        def second_conv(aq, asc, c0, c1, m, o_ps):
+            nc.tensor.matmul_mx(
+                out=o_ps,
+                lhsT=w2q[:, m * P : (m + 1) * P].bitcast(FP8X4),
+                lhsT_scale=w2s[:, m * P : (m + 1) * P],
+                rhs=aq[:, c0:c1].bitcast(FP8X4),
+                rhs_scale=asc[:, c0:c1],
+                start=True,
+                stop=True,
+            )
+
         def finish_affinity(pool, aff, nq):
             flat = aff[:].rearrange("p a b i j -> p (a b i j)")
-            nc.scalar.activation(out=flat, in_=flat, func=ACT.Exp, scale=neginv[:, 0:1])
             nc.scalar.activation(out=flat, in_=flat, func=ACT.Exp, bias=negone[:, 0:1])
             ssum = pool.tile([P, nq], F32, name="ssum")
             nc.vector.tensor_reduce(
@@ -210,430 +265,715 @@ def tile_dcblock_t_kernel(
                 out=by_off, in0=by_off, in1=ssum[:].unsqueeze(1).to_broadcast([P, KW * KW, nq]), op=ALU.mult
             )
 
-        with ExitStack() as fpool:
-            xqp = fpool.enter_context(tc.tile_pool(name="xqp", bufs=1))
-            xqf = xqp.tile([P, 2 * CHPX], I32, name="xqf", align_bytes=64)
-            xsf = xqp.tile([P, 2 * CHPX], U8, name="xsf", align_bytes=64)
-            p_e = xqp.tile([P, VR, VX, CP], BF16, name="p_e")
-
-            with tc.tile_pool(name="head", bufs=1) as head:
-                nat_f = head.tile([P, 30, HZP], BF16, name="nat_f")
-                nat_e = head.tile([P, 78, HZP], BF16, name="nat_e")
+        with ExitStack() as lower:
+            affp = lower.enter_context(tc.tile_pool(name="affp", bufs=1))
+            aff_f = affp.tile([P, KW, KW, BR, BC], F32, name="aff_f")
+            with ExitStack() as start:
+                xqp = start.enter_context(tc.tile_pool(name="xqp", bufs=1, side="right"))
+                dpool = start.enter_context(tc.tile_pool(name="dpool", bufs=2, side="right"))
+                xqf = xqp.tile([P, 2 * CHPX], I32, name="xqf", align_bytes=64)
+                xsf = xqp.tile([P, 2 * CHPX], U8, name="xsf", align_bytes=64)
+                p_e = xqp.tile([P, CP, VR, VX], BF16, name="p_e")
+                nh = xqp.tile([P, VR, VX], F32, name="nh")
+                nv = xqp.tile([P, 2, NQ], F32, name="nv")
+                natp = start.enter_context(tc.tile_pool(name="natp", bufs=1, side="right"))
+                nat_f = natp.tile([P, 30, HZP], BF16, name="nat_f")
+                nat_e = natp.tile([P, 78, HZP], BF16, name="nat_e")
                 nc.vector.memset(nat_f[:], 0.0)
-                nc.gpsimd.memset(nat_e[:], 0.0)
-                for nat, lo, hi, y0 in ((nat_f, F_ROW0, H, 0), (nat_e, 0, HE + PAD, PAD)):
-                    for s in range(2):
-                        for j in range(BC):
-                            g = s * BC + j
-                            skip = max(0, s - y0)
-                            for c0, c1 in ((0, 16), (16, CP)):
-                                nc.sync.dma_start(
-                                    out=nat[
-                                        CP * g + c0 : CP * g + c1,
-                                        y0 - s + skip : y0 - s + hi - lo,
-                                        PAD - j : PAD - j + W,
-                                    ],
-                                    in_=probs[c0:c1, lo + skip : hi, :],
-                                )
+                nc.vector.memset(nat_e[:], 0.0)
 
-                prm = []
-                for k, vec in enumerate((bn_gamma, bn_beta, bn_mean, bn_var)):
-                    prm.append(head.tile([P, T], BF16, name="prm%d" % k))
-                    nc.sync.dma_start(out=prm[k][:], in_=vec.rearrange("(p t) -> p t", t=T))
-                sd = head.tile([P, T], F32, name="sd")
-                nc.vector.tensor_scalar(out=sd[:], in0=prm[3][:], scalar1=1e-5, scalar2=None, op0=ALU.add)
-                nc.scalar.activation(out=sd[:], in_=sd[:], func=ACT.Sqrt)
-                nc.vector.reciprocal(out=sd[:], in_=sd[:])
-                nc.vector.tensor_tensor(out=bsc[:], in0=prm[0][:], in1=sd[:], op=ALU.mult)
-                ms = head.tile([P, T], F32, name="ms")
-                nc.vector.tensor_tensor(out=ms[:], in0=prm[2][:], in1=bsc[:], op=ALU.mult)
-                nc.vector.tensor_tensor(out=bbi[:], in0=prm[1][:], in1=ms[:], op=ALU.subtract)
+                with tc.tile_pool(name="head", bufs=1, side="right", reuse_waits="tile") as head:
+                    stages = [head.tile([P, CHPX, T], BF16, name="stage%d" % k, align_bytes=64) for k in range(2)]
+                    for k in range(2):
+                        nc.gpsimd.memset(stages[k][:], 0.0)
 
-                sg = head.tile([P, 1], BF16, name="sg")
-                nc.sync.dma_start(out=sg[:], in_=sigma.partition_broadcast(P))
-                sf = head.tile([P, 1], F32, name="sf")
-                nc.vector.tensor_scalar(out=sf[:], in0=sg[:], scalar1=0.0, scalar2=None, op0=ALU.max)
-                nc.vector.tensor_tensor(out=sf[:], in0=sf[:], in1=sf[:], op=ALU.mult)
-                nc.vector.tensor_scalar(out=sf[:], in0=sf[:], scalar1=2.0, scalar2=1e-8, op0=ALU.mult, op1=ALU.add)
-                nc.vector.reciprocal(out=sf[:], in_=sf[:])
-                nc.vector.tensor_scalar(out=neginv[:], in0=sf[:], scalar1=-1.0, scalar2=None, op0=ALU.mult)
-
-                p_f = head.tile([P, IR, JC, CP], BF16, name="p_f")
-                gat_f = head.tile([P, IR // 2, BC, P], BF16, name="gat_f")
-                for y2 in range(IR // 2):
-                    for x3 in range(BC):
-                        src = nat_f[:, 2 * y2 : 2 * y2 + BR * (BA - 1) + 1 : BR, BC * x3 : BC * x3 + BC * (BW - 1) + 1 : BC]
-                        dst = gat_f[:, y2, x3, :].rearrange("p (a w) -> p a w", a=BA)
-                        if (y2 + x3) % 2 == 0:
-                            nc.vector.tensor_copy(out=dst, in_=src)
-                        else:
-                            nc.scalar.copy(out=dst, in_=src)
-                for y2 in range(IR // 2):
-                    ps = ps_misc.tile([P, BC, P], BF16, name="ps_p", tag="misc")
-                    for x3 in range(BC):
-                        nc.tensor.transpose(ps[:, x3, :], gat_f[:, y2, x3, :], ident_b[:])
-                    nc.vector.tensor_copy(
-                        out=p_f[:, 2 * y2 : 2 * y2 + 2].rearrange("p s (x j) c -> p s x (j c)", j=BC),
-                        in_=ps[:, :, 0 : 6 * CP].rearrange("p x (s k) -> p s x k", s=2),
-                    )
-
-                stages = [head.tile([P, CHPX, T], BF16, name="stage%d" % k, align_bytes=64) for k in range(2)]
-                for k in range(2):
-                    nc.gpsimd.memset(stages[k][:], 0.0)
-                for k in range(2):
-                    run(pack_steps(head, stages[k], F_ROW0 + k * CH, xqf, xsf, k * CHPX, H))
-
-                for dh in range(KW):
-                    diff = head.tile([P, KW, NPOS * CP + 2], F32, name="diff", bufs=2)
-                    for dw in range(KW):
-                        eng = nc.gpsimd if dw in (1, 3, 5) else nc.vector
-                        eng.tensor_tensor(
-                            out=diff[:, dw, 0 : NPOS * CP].rearrange("p (i k) -> p i k", i=BR),
-                            in0=p_f[:, dh : dh + BR, dw : dw + BC, :].rearrange("p i j c -> p i (j c)"),
-                            in1=p_f[:, PAD : PAD + BR, PAD : PAD + BC, :].rearrange("p i j c -> p i (j c)"),
-                            op=ALU.subtract,
-                        )
-                    flat = diff[:, :, 0 : NPOS * CP]
-                    nc.scalar.activation(out=flat, in_=flat, func=ACT.Square)
-                    nc.vector.tensor_reduce(
-                        out=aff_f[:, dh].rearrange("p d i j -> p d (i j)"),
-                        in_=flat.rearrange("p d (q c) -> p d q c", c=CP),
-                        axis=AX.X,
-                        op=ALU.add,
-                    )
-                finish_affinity(head, aff_f, NPOS)
-
-                for wi, (rows, wq, wsc) in enumerate(
-                    (
-                        (w_feat.rearrange("(p a) c -> p a c", a=T), w1q, w1s),
-                        (w_fuse.rearrange("(a p) c -> p a c", a=T), w2q, w2s),
-                    )
-                ):
-                    w_sb = head.tile([P, T, C], BF16, name="w_sb", bufs=2)
-                    nc.sync.dma_start(out=w_sb[:], in_=rows)
-                    w_gr = head.tile([P, C, T], BF16, name="w_gr", bufs=2, align_bytes=64)
-                    for a in range(T):
-                        w_t = ps_misc.tile([P, T, P], BF16, name="w_t", tag="misc")
-                        for t in range(T):
-                            nc.tensor.transpose(w_t[:, t, :], w_sb[:, a, t : C : T], ident_b[:])
-                        nc.scalar.copy(out=w_gr[:, a * P : (a + 1) * P, :], in_=w_t[:].rearrange("p t o -> p o t"))
-                    nc.vector.quantize_mx(
-                        out=wq[:].bitcast(FP8X4), scales=wsc[:], in_=w_gr[:].rearrange("p o t -> p (o t)")
-                    )
-
-                gat_e = head.tile([P, VR // 2, 8, P], BF16, name="gat_e")
-                nc.gpsimd.memset(gat_e[:], 0.0)
-                for u in range(VR // 2):
-                    for x3 in range(8):
-                        for half in range(2):
-                            y0 = 2 * u + HALF * half
-                            src = nat_e[:, y0 : y0 + TH * (TR - 1) + 1 : TH, BC * x3 : BC * x3 + TW * (TC - 1) + 1 : TW]
-                            dst = gat_e[:, u, x3, LOW * half : LOW * half + NT].rearrange("p (r c) -> p r c", c=TC)
-                            nc.scalar.copy(out=dst, in_=src)
-                for u in range(VR // 2):
-                    for g in range(2):
-                        ps = ps_misc.tile([P, 4, P], BF16, name="ps_p", tag="misc")
-                        for k in range(4):
-                            nc.tensor.transpose(ps[:, k, :], gat_e[:, u, 4 * g + k, :], ident_b[:])
-                        cols = slice(12 * g, 12 * g + 12)
-                        nc.vector.tensor_copy(
-                            out=p_e[0:LOW, 2 * u : 2 * u + 2, cols, :].rearrange("p s (x j) c -> p s x (j c)", j=BC),
-                            in_=ps[0:LOW, :, 0 : 6 * CP].rearrange("p x (s k) -> p s x k", s=2),
-                        )
+                    def load_probs(nat, lo, hi, y0):
                         for s in range(2):
-                            nc.scalar.copy(
-                                out=p_e[LOW:P, 2 * (4 - u) + 1 - s, cols, :].rearrange("p (x j) c -> p x (j c)", j=BC),
-                                in_=ps[LOW:P, :, 3 * CP * s : 3 * CP * (s + 1)],
+                            for j in range(BC):
+                                g = s * BC + j
+                                skip = max(0, s - y0)
+                                for c0, c1 in ((0, 16), (16, CP)):
+                                    nc.sync.dma_start(
+                                        out=nat[
+                                            CP * g + c0 : CP * g + c1,
+                                            y0 - s + skip : y0 - s + hi - lo,
+                                            PAD - j : PAD - j + W,
+                                        ],
+                                        in_=probs[c0:c1, lo + skip : hi, :],
+                                    )
+
+                    sg = head.tile([P, 1], BF16, name="sg")
+                    nc.sync.dma_start(out=sg[:], in_=sigma.partition_broadcast(P))
+                    load_probs(nat_f, F_ROW0, H, 0)
+                    prm = []
+                    for k, vec in enumerate((bn_gamma, bn_beta, bn_mean, bn_var)):
+                        prm.append(head.tile([P, T], BF16, name="prm%d" % k))
+                        nc.sync.dma_start(out=prm[k][:], in_=vec.rearrange("(p t) -> p t", t=T))
+                    w_sb = [head.tile([P, T, C], BF16, name="w_sb%d" % k) for k in range(2)]
+                    nc.sync.dma_start(out=w_sb[0][:], in_=w_feat.rearrange("(p a) c -> p a c", a=T))
+                    packs = [
+                        pack_steps(head, stages[n], F_ROW0 + n * CH, H, xqf, xsf, n * CHPX, True, False) for n in range(2)
+                    ]
+                    packs[0][0]()
+                    packs[1][0]()
+                    load_probs(nat_e, 0, HE + PAD, PAD)
+                    nc.sync.dma_start(out=w_sb[1][:], in_=w_fuse.rearrange("(a p) c -> p a c", a=T))
+
+                    sf = head.tile([P, 1], F32, name="sf")
+                    nc.vector.tensor_scalar(out=sf[:], in0=sg[:], scalar1=0.0, scalar2=None, op0=ALU.max)
+                    nc.vector.tensor_tensor(out=sf[:], in0=sf[:], in1=sf[:], op=ALU.mult)
+                    nc.vector.tensor_scalar(out=sf[:], in0=sf[:], scalar1=2.0, scalar2=1e-8, op0=ALU.mult, op1=ALU.add)
+                    nc.vector.reciprocal(out=sf[:], in_=sf[:])
+                    nc.vector.tensor_scalar(out=neginv[:], in0=sf[:], scalar1=-1.0, scalar2=None, op0=ALU.mult)
+                    nc.vector.tensor_scalar(out=twoinv[:], in0=sf[:], scalar1=2.0, scalar2=None, op0=ALU.mult)
+
+                    n_y2 = (IR + 1) // 2
+                    p_f = head.tile([P, 2 * n_y2, JC, CP], BF16, name="p_f")
+                    gat_f = head.tile([P, n_y2, BC, P], BF16, name="gat_f")
+                    for y2 in range(n_y2):
+                        for x3 in range(BC):
+                            src = nat_f[
+                                :, 2 * y2 : 2 * y2 + BR * (BA - 1) + 1 : BR, BC * x3 : BC * x3 + BC * (BW - 1) + 1 : BC
+                            ]
+                            dst = gat_f[:, y2, x3, :].rearrange("p (a w) -> p a w", a=BA)
+                            if (y2 + x3) % 2 == 0:
+                                nc.vector.tensor_copy(out=dst, in_=src)
+                            else:
+                                nc.scalar.copy(out=dst, in_=src)
+                    for y2 in range(n_y2):
+                        ps = ps_misc.tile([P, BC, P], BF16, name="ps_p", tag="misc")
+                        for x3 in range(BC):
+                            nc.tensor.transpose(ps[:, x3, :], gat_f[:, y2, x3, :], ident_b[:])
+                        nc.vector.tensor_copy(
+                            out=p_f[:, 2 * y2 : 2 * y2 + 2].rearrange("p s (x j) c -> p s x (j c)", j=BC),
+                            in_=ps[:, :, 0 : 6 * CP].rearrange("p x (s k) -> p s x k", s=2),
+                        )
+
+                    NF = NPOS * CP
+                    diffs = {}
+
+                    def f_diff(dh):
+                        diffs[dh] = head.tile([P, KW, -(-NF // 8) * 8], F32, name="diff", bufs=3)
+                        for dw in range(KW):
+                            eng = nc.vector if dw in (1, 4) else nc.gpsimd
+                            eng.tensor_tensor(
+                                out=diffs[dh][:, dw, 0:NF].rearrange("p (i k) -> p i k", i=BR),
+                                in0=p_f[:, dh : dh + BR, dw : dw + BC, :].rearrange("p i j c -> p i (j c)"),
+                                in1=p_f[:, PAD : PAD + BR, PAD : PAD + BC, :].rearrange("p i j c -> p i (j c)"),
+                                op=ALU.subtract,
                             )
 
-            with ExitStack() as fx:
-                cpool = fx.enter_context(tc.tile_pool(name="cpool", bufs=1))
-                setp = fx.enter_context(tc.tile_pool(name="setp", bufs=3))
-                accp = fx.enter_context(tc.tile_pool(name="accp", bufs=13))
-                prodp = fx.enter_context(tc.tile_pool(name="prodp", bufs=6))
-                dpool = fx.enter_context(tc.tile_pool(name="dpool", bufs=2))
-                st2 = fx.enter_context(tc.tile_pool(name="st2", bufs=2))
+                    def f_square(dh):
+                        flat = diffs[dh][:, :, 0:NF]
+                        nc.scalar.activation(out=flat, in_=flat, func=ACT.Square)
+
+                    def f_reduce(dh):
+                        nc.vector.tensor_reduce(
+                            out=aff_f[:, dh].rearrange("p d i j -> p d (i j)"),
+                            in_=diffs.pop(dh)[:, :, 0:NF].rearrange("p d (q c) -> p d q c", c=CP),
+                            axis=AX.X,
+                            op=ALU.add,
+                        )
+
+                    def f_softmax():
+                        flat = aff_f[:].rearrange("p a b i j -> p (a b i j)")
+                        nc.scalar.activation(out=flat, in_=flat, func=ACT.Exp, scale=neginv[:, 0:1])
+                        finish_affinity(head, aff_f, NPOS)
+
+                    block_jobs = []
+                    for dh in range(KW + 2):
+                        for step, f in enumerate((f_diff, f_square, f_reduce)):
+                            if 0 <= dh - step < KW:
+                                block_jobs.append(partial(f, dh - step))
+                    block_jobs.append(f_softmax)
+
+                    sd = head.tile([P, T], F32, name="sd")
+                    nc.vector.tensor_scalar(out=sd[:], in0=prm[3][:], scalar1=1e-5, scalar2=None, op0=ALU.add)
+                    nc.scalar.activation(out=sd[:], in_=sd[:], func=ACT.Sqrt)
+                    nc.vector.reciprocal(out=sd[:], in_=sd[:])
+                    nc.vector.tensor_tensor(out=bsc[:], in0=prm[0][:], in1=sd[:], op=ALU.mult)
+                    ms = head.tile([P, T], F32, name="ms")
+                    nc.vector.tensor_tensor(out=ms[:], in0=prm[2][:], in1=bsc[:], op=ALU.mult)
+                    nc.vector.tensor_tensor(out=bbi[:], in0=prm[1][:], in1=ms[:], op=ALU.subtract)
+
+                    w_gr = [head.tile([P, C, T], BF16, name="w_gr%d" % k, align_bytes=64) for k in range(2)]
+
+                    def w_turn(k, a):
+                        w_t = ps_misc.tile([P, T, P], BF16, name="w_t", tag="misc")
+                        for t in range(T):
+                            nc.tensor.transpose(w_t[:, t, :], w_sb[k][:, a, t : C : T], ident_b[:])
+                        nc.scalar.copy(out=w_gr[k][:, a * P : (a + 1) * P, :], in_=w_t[:].rearrange("p t o -> p o t"))
+
+                    def w_quant(k):
+                        wq, wsc = ((w1q, w1s), (w2q, w2s))[k]
+                        nc.vector.quantize_mx(
+                            out=wq[:].bitcast(FP8X4), scales=wsc[:], in_=w_gr[k][:].rearrange("p o t -> p (o t)")
+                        )
+
+                    w_jobs = [partial(w_turn, k, a) for k in range(2) for a in range(T)]
+
+                    run(
+                        spread(
+                            block_jobs,
+                            w_jobs[0:T] + [partial(w_quant, 0)] + packs[0][1:] + packs[1][1:] + w_jobs[T:] + [partial(w_quant, 1)],
+                        )
+                    )
+
+                gathered = {}
+                turned = {}
+
+                def e_gather(u):
+                    gathered[u] = natp.tile([P, 8, P], BF16, name="gat_e", bufs=2)
+                    nc.gpsimd.memset(gathered[u][:], 0.0)
+                    for x3 in range(8):
+                        z0 = BC * x3
+                        z1 = z0 + TW * (TC - 1) + 1
+                        for half in range(2):
+                            y0 = 2 * u + HALF * half
+                            nc.scalar.copy(
+                                out=gathered[u][:, x3, LOW * half : LOW * half + NT].rearrange("p (r c) -> p r c", c=TC),
+                                in_=nat_e[:, y0 : y0 + TH * (TR - 1) + 1 : TH, z0:z1:TW],
+                            )
+                        nc.scalar.copy(
+                            out=gathered[u][:, x3, NT : NT + 2 * NS].rearrange("p (h a) -> p h a", h=2),
+                            in_=nat_f[:, S_ROW - PAD - F_ROW0 + 2 * u, z0:z1:TW].rearrange("p (a h) -> p h a", h=2),
+                        )
+
+                def e_turn(u, g):
+                    turned[(u, g)] = ps_misc.tile([P, 4, P], BF16, name="ps_p", tag="misc")
+                    for k in range(4):
+                        nc.tensor.transpose(turned[(u, g)][:, k, :], gathered[u][:, 4 * g + k, :], ident_b[:])
+
+                def e_unload(u, g):
+                    ps = turned.pop((u, g))
+                    for half in range(2):
+                        for s in range(2):
+                            row = 2 * u + s if half == 0 else VR - 1 - 2 * u - s
+                            dst = p_e[LOW * half : LOW * half + LOW, :, row, 12 * g : 12 * g + 12]
+                            src = ps[LOW * half : LOW * half + LOW, :, 3 * CP * s : 3 * CP * (s + 1)]
+                            dst = dst.rearrange("p c (x j) -> p c x j", j=BC)
+                            src = src.rearrange("p x (j c) -> p c x j", j=BC)
+                            if s == 0:
+                                nc.vector.tensor_copy(out=dst, in_=src)
+                            else:
+                                nc.scalar.copy(out=dst, in_=src)
+
+                def e_lengths():
+                    for rows in (slice(0, VR // 2), slice(VR // 2, VR)):
+                        sq = dpool.tile([P, CP, VR // 2 * VX], F32, name="sq", tag="pr")
+                        nc.scalar.activation(
+                            out=sq[:], in_=p_e[:, :, rows, :].rearrange("p c y x -> p c (y x)"), func=ACT.Square
+                        )
+                        nc.vector.tensor_reduce(
+                            out=nh[:, rows, :].rearrange("p y x -> p (y x)"),
+                            in_=sq[:].rearrange("p c z -> p z c"),
+                            axis=AX.X,
+                            op=ALU.add,
+                        )
+                    nc.vector.tensor_scalar(out=nh[:], in0=nh[:], scalar1=-0.5, scalar2=None, op0=ALU.mult)
+                    for n in range(2):
+                        nc.scalar.copy(
+                            out=nv[:, n].rearrange("p (y x) -> p y x", x=TW),
+                            in_=nh[:, PAD : PAD + HALF, PAD : PAD + TW],
+                        )
+
+                tile_jobs = [partial(e_gather, 0)]
+                turns = [(u, g) for u in range(VR // 2) for g in range(2)]
+                for n in range(len(turns) + 1):
+                    if n < len(turns):
+                        if n % 2 == 0 and n + 2 < len(turns):
+                            tile_jobs.append(partial(e_gather, n // 2 + 1))
+                        tile_jobs.append(partial(e_turn, *turns[n]))
+                    if n > 0:
+                        tile_jobs.append(partial(e_unload, *turns[n - 1]))
+                cpool = lower.enter_context(tc.tile_pool(name="cpool", bufs=1, reuse_waits="tile"))
+                accp = lower.enter_context(tc.tile_pool(name="accp", bufs=len(ROUNDS[2]) * BC))
+                prodp = lower.enter_context(tc.tile_pool(name="prodp", bufs=6))
+                st2 = lower.enter_context(tc.tile_pool(name="st2", bufs=2))
+                cpool_1 = start.enter_context(tc.tile_pool(name="cpool_1", bufs=1, side="right", reuse_waits="tile"))
+                accp_1 = start.enter_context(tc.tile_pool(name="accp_1", bufs=NPOS - len(ROUNDS[2]) * BC, side="right"))
+                setp = start.enter_context(tc.tile_pool(name="setp", bufs=2, side="right", reuse_waits="tile"))
                 sets = {}
-                accs = {}
                 copies = {}
+                sums = {}
+                groups = {}
+                conv = {}
+                todo = []
+                clock = [0]
                 xqf_v = xqf[:].rearrange("p (r z) -> p r z", z=PITCH)
                 xsf_v = xsf[:].rearrange("p (r z) -> p r z", z=PITCH)
 
-                def f_set(ip):
-                    words = setp.tile([P, JC * P], I32, name="words", align_bytes=64)
-                    scales = setp.tile([P, JC * P], U8, name="scales", align_bytes=64)
+                def f_set(ip, kind, bufs):
+                    words = setp.tile([P, JC * P], I32, name=kind + "_words", bufs=bufs, align_bytes=64)
+                    scales = setp.tile([P, JC * P], U8, name=kind + "_scales", bufs=bufs, align_bytes=64)
                     for u in range(JC // BC):
                         for dst, src in ((words, xqf_v), (scales, xsf_v)):
                             nc.vector.tensor_copy(
                                 out=dst[:, BC * P * u : BC * P * (u + 1)].rearrange("p (b a w) -> p b a w", b=BC, a=BA),
-                                in_=src[:, ip : ip + BR * (BA - 1) + 1 : BR, BC * u : BC * u + W].rearrange(
-                                    "p a (w b) -> p b a w", b=BC
-                                ),
+                                in_=src[:, ip : ip + BR * (BA - 1) + 1 : BR, 0 : BC * BI].rearrange(
+                                    "p a (b i) -> p b a i", b=BC
+                                )[:, :, :, u : u + BW],
                             )
-                    sets[ip] = (words, scales)
+                    sets[(kind, ip)] = (words, scales)
 
-                def f_message(ip, jp):
-                    words, scales = sets[ip]
-                    return mx_message(words[:, jp * P : (jp + 1) * P], scales[:, jp * P : (jp + 1) * P])
+                def f_message(kind, ip, jp, pool, tag):
+                    words, scales = sets[(kind, ip)]
+                    return mx_message(words[:, jp * P : (jp + 1) * P], scales[:, jp * P : (jp + 1) * P], pool, tag)
 
                 def f_weight(i, j, ip, jp):
                     return aff_f[:, ip - i, jp - j, i, j : j + 1]
 
-                def f_vector(ip, jp):
-                    msg = f_message(ip, jp)
-                    for i in range(max(0, ip - 2 * PAD), min(BR - 1, ip) + 1):
-                        for j in range(max(0, jp - 2 * PAD), min(BC - 1, jp) + 1):
-                            vector_term(accp, accs, (i, j), msg, f_weight(i, j, ip, jp))
+                def f_mul(i, ip):
+                    return i <= ip <= i + 2 * PAD and ip in MUL_ROWS and i not in VEC_TOO.get(ip, ())
+
+                def f_columns(jp):
+                    return range(max(0, jp - 2 * PAD), min(BC - 1, jp) + 1)
+
+                def f_vector(mine, ip, jp):
+                    msg = f_message("vec", ip, jp, ps_msg, "msg")
+                    for i in mine:
+                        for j in f_columns(jp):
+                            first = (i, j) not in sums
+                            if first:
+                                sums[(i, j)] = (accp if i in ROUNDS[2] else accp_1).tile([P, C], F32, name="acc")
+                            vector_term(sums[(i, j)], first, msg, f_weight(i, j, ip, jp))
 
                 def f_copy(ip, jp):
-                    msg = f_message(ip, jp)
-                    copies[(ip, jp)] = cpool.tile([P, C], F32, name="cp%d_%d" % (ip, jp))
+                    msg = f_message("mul", ip, jp, ps_pos, "pos")
+                    pool = cpool if any([f_mul(i, ip) for i in ROUNDS[2]]) else cpool_1
+                    copies[(ip, jp)] = pool.tile([P, C], F32, name="cp%d_%d" % (ip, jp))
                     nc.scalar.copy(out=copies[(ip, jp)][:], in_=msg[:])
 
                 def f_position(i, j):
+                    terms = [(ip, j + dw) for ip in MUL_ROWS if f_mul(i, ip) for dw in range(KW)]
                     st = {}
-                    jobs = []
-                    terms = [(ip, j + dw) for ip in COPY_ROWS if i <= ip <= i + 2 * PAD for dw in range(KW)]
 
                     def term(k, ip, jp):
+                        clock[0] += 1
+                        if todo and todo[0][0] <= clock[0] and k % 2 == 1:
+                            todo.pop(0)[1]()
                         if k == 0:
                             st["pos"] = ps_pos.tile([P, T, P], F32, name="pos")
-                        prod = product(prodp, copies[(ip, jp)], f_weight(i, j, ip, jp))
-                        add_transposed(st["pos"], prod, k == 0, False)
+                        add_transposed(st["pos"], product(prodp, copies[(ip, jp)], f_weight(i, j, ip, jp)), k == 0, False)
 
                     def close():
-                        add_transposed(st["pos"], accs.pop((i, j)), False, True)
+                        add_transposed(st["pos"], sums.pop((i, j)), False, True)
+
+                    def unload():
                         if j == 0:
-                            grp[i] = st2.tile([P, ROWPX, T], BF16, name="grp", align_bytes=64)
+                            groups[i] = st2.tile([P, ROWPX, T], BF16, name="grp", align_bytes=64)
                         nc.scalar.copy(
-                            out=grp[i][:].rearrange("p (k b) t -> p b k t", b=BC)[:, j],
+                            out=groups[i][:].rearrange("p (k b) t -> p b k t", b=BC)[:, j],
                             in_=st["pos"][:].rearrange("p t k -> p k t"),
                         )
+                        if j == BC - 1:
+                            todo.extend([(clock[0] + CONV_LATE, f) for f in f_conv(i)])
 
-                    for k, (ip, jp) in enumerate(terms):
-                        jobs.append(partial(term, k, ip, jp))
-                    jobs.append(close)
-                    return jobs
+                    return [partial(term, k, ip, jp) for k, (ip, jp) in enumerate(terms)], close, unload
 
-                grp = {}
-                f_st = {}
+                def f_image(i):
+                    return slice(HE + i, HE + i + BR * (BA - 1) + 1, BR)
 
                 def f_conv_in(i):
-                    x_res = st2.tile([P, T, ROWPX], BF16, name="x_res")
+                    x_res = st2.tile([P, T, ROWPX], BF16, name="x_res", bufs=1)
                     for t in range(T):
                         nc.sync.dma_start(
-                            out=x_res[:, t, :].rearrange("p (a w) -> p a w", w=W),
-                            in_=x_r[:, t, HE + i : HE + i + BR * (BA - 1) + 1 : BR, :],
+                            out=x_res[:, t, :].rearrange("p (a w) -> p a w", w=W), in_=x_r[:, t, f_image(i), :]
                         )
-                    aq = st2.tile([P, ROWPX], I32, name="aq", align_bytes=64)
-                    asc = st2.tile([P, ROWPX], U8, name="asc", align_bytes=64)
-                    grp_f = grp.pop(i)[:].rearrange("p k t -> p (k t)")
-                    for c0, c1 in ((0, 256), (256, 384)):
+                    aq = st2.tile([P, ROWPX], I32, name="aq", bufs=1, align_bytes=64)
+                    asc = st2.tile([P, ROWPX], U8, name="asc", bufs=1, align_bytes=64)
+                    flat = groups.pop(i)[:].rearrange("p k t -> p (k t)")
+                    for c0, c1 in ((0, 256), (256, ROWPX)):
                         nc.vector.quantize_mx(
-                            out=aq[:, c0:c1].bitcast(FP8X4), scales=asc[:, c0:c1], in_=grp_f[:, T * c0 : T * c1]
+                            out=aq[:, c0:c1].bitcast(FP8X4), scales=asc[:, c0:c1], in_=flat[:, T * c0 : T * c1]
                         )
-                    f_st[i] = (x_res, aq, asc)
+                    conv[i] = (x_res, aq, asc)
 
                 def f_conv_out(i, m):
-                    x_res, aq, asc = f_st[i]
-                    o_ps = ps_misc.tile([P, ROWPX], F32, name="o_ps", tag="misc")
-                    for c0, c1 in ((0, 256), (256, 384)):
-                        nc.tensor.matmul_mx(
-                            out=o_ps[:, c0:c1],
-                            lhsT=w2q[:, m * P : (m + 1) * P].bitcast(FP8X4),
-                            lhsT_scale=w2s[:, m * P : (m + 1) * P],
-                            rhs=aq[:, c0:c1].bitcast(FP8X4),
-                            rhs_scale=asc[:, c0:c1],
-                            start=True,
-                            stop=True,
-                        )
-                    o_sb = st2.tile([P, ROWPX], F32, name="o_sb")
+                    x_res, aq, asc = conv[i]
+                    o_ps = ps_msg.tile([P, ROWPX], F32, name="o_ps", tag="msg")
+                    for c0, c1 in ((0, 256), (256, ROWPX)):
+                        second_conv(aq, asc, c0, c1, m, o_ps[:, c0:c1])
+                    o_sb = st2.tile([P, ROWPX], F32, name="o_sb", bufs=1)
                     nc.vector.tensor_tensor(out=o_sb[:], in0=o_ps[:], in1=x_res[:, m, :], op=ALU.add)
                     nc.sync.dma_start(
-                        out=out_v[m, :, HE + i : HE + i + BR * (BA - 1) + 1 : BR, :],
-                        in_=o_sb[:].rearrange("p (a w) -> p a w", w=W),
+                        out=out_v[m, :, f_image(i), :], in_=o_sb[:].rearrange("p (a w) -> p a w", w=W)
                     )
 
                 def f_conv(i):
                     return [partial(f_conv_in, i)] + [partial(f_conv_out, i, m) for m in range(T)]
 
-                def e_distance(dh, dw):
-                    diff = dpool.tile([P, NQ, CP], F32, name="diff")
-                    nc.gpsimd.tensor_tensor(
-                        out=diff[:].rearrange("p (y x) c -> p y (x c)", y=HALF),
-                        in0=p_e[:, dh : dh + HALF, dw : dw + TW, :].rearrange("p y x c -> p y (x c)"),
-                        in1=p_e[:, PAD : PAD + HALF, PAD : PAD + TW, :].rearrange("p y x c -> p y (x c)"),
-                        op=ALU.subtract,
+                pairs = {}
+
+                def e_products(o):
+                    pr = dpool.tile([P, CP, 2, NQ], F32, name="pr")
+                    nu = dpool.tile([P, 2, NQ], F32, name="nu")
+                    for n in range(2):
+                        dh, dw = divmod(min(o + n, KW * KW - 1), KW)
+                        nc.gpsimd.tensor_tensor(
+                            out=pr[:, :, n].rearrange("p c (y x) -> p c y x", x=TW),
+                            in0=p_e[:, :, dh : dh + HALF, dw : dw + TW],
+                            in1=p_e[:, :, PAD : PAD + HALF, PAD : PAD + TW],
+                            op=ALU.mult,
+                        )
+                        nc.scalar.copy(
+                            out=nu[:, n].rearrange("p (y x) -> p y x", x=TW), in_=nh[:, dh : dh + HALF, dw : dw + TW]
+                        )
+                    pairs[o] = (pr, nu)
+
+                def e_sum(o):
+                    pr, nu = pairs.pop(o)
+                    pairs[o] = ps_misc.tile([P, P], F32, name="ps_d", tag="misc")
+                    for c in range(CP + 2):
+                        src = pr[:, c] if c < CP else (nu if c == CP else nv)[:]
+                        nc.tensor.matmul(
+                            out=pairs[o][:],
+                            lhsT=src.rearrange("p n q -> p (n q)"),
+                            rhs=ident_f[:],
+                            is_transpose=True,
+                            start=(c == 0),
+                            stop=(c == CP + 1),
+                        )
+
+                def e_out(o):
+                    ps = pairs.pop(o)
+                    pairs[o] = dpool.tile([P, P], F32, name="turned")
+                    nc.scalar.copy(out=pairs[o][:], in_=ps[:])
+
+                def e_back(o):
+                    src = pairs.pop(o)
+                    pairs[o] = ps_misc.tile([P, P], F32, name="ps_d", tag="misc")
+                    nc.tensor.transpose(pairs[o][:], src[:], ident_f[:])
+
+                def e_exp(o):
+                    n = min(2, KW * KW - o)
+                    nc.scalar.activation(
+                        out=aff_e[:].rearrange("p a b y x -> p (a b y x)")[:, NQ * o : NQ * (o + n)],
+                        in_=pairs.pop(o)[:, 0 : NQ * n],
+                        func=ACT.Exp,
+                        scale=twoinv[:, 0:1],
                     )
-                    flat = diff[:].rearrange("p q c -> p (q c)")
-                    nc.scalar.activation(out=flat, in_=flat, func=ACT.Square)
-                    nc.vector.tensor_reduce(
-                        out=aff_e[:, dh, dw].rearrange("p y x -> p (y x)"), in_=diff[:], axis=AX.X, op=ALU.add
-                    )
 
-                distances = [partial(e_distance, dh, dw) for dh in range(KW) for dw in range(KW)]
+                distances = []
+                for o in range(0, KW * KW + 8, 2):
+                    for step, f in ((4, e_exp), (2, e_out), (1, e_sum), (3, e_back), (0, e_products)):
+                        if 0 <= o - 2 * step < KW * KW:
+                            distances.append(partial(f, o - 2 * step))
+                distances.append(partial(finish_affinity, st2, aff_e, NQ))
 
-                v_jobs = []
-                for ip in V_ROWS:
-                    v_jobs.append([partial(f_set, ip)] + [partial(f_vector, ip, jp) for jp in range(JC)])
-                c_jobs = []
-                for ip in COPY_ROWS:
-                    c_jobs += [partial(f_set, ip)] + [partial(f_copy, ip, jp) for jp in range(JC)]
+                v_rows = []
+                for rnd in ROUNDS:
+                    for ip in range(IR - 1, -1, -1):
+                        mine = [i for i in rnd if i <= ip <= i + 2 * PAD and not f_mul(i, ip)]
+                        if mine:
+                            v_rows.append((rnd, ip, mine))
+                vec = [(3, 0, partial(f_set, v_rows[0][1], "vec", 2)), (1, 0, partial(f_set, MUL_ROWS[0], "mul", 1))]
+                vec_ends = {}
+                for n, (rnd, ip, mine) in enumerate(v_rows):
+                    if n + 1 < len(v_rows):
+                        vec.append((3, 0, partial(f_set, v_rows[n + 1][1], "vec", 2)))
+                    for jp in range(JC):
+                        vec.append((len(mine) * len(f_columns(jp)), 0, partial(f_vector, mine, ip, jp)))
+                    vec_ends[rnd] = len(vec)
+                mul = []
+                for n, ip in enumerate(MUL_ROWS):
+                    mul += [(1, 2, partial(f_copy, ip, jp)) for jp in range(JC)]
+                    if n + 1 < len(MUL_ROWS):
+                        mul.append((1, 0, partial(f_set, MUL_ROWS[n + 1], "mul", 1)))
 
-                def f_row(i):
-                    return sum([f_position(i, j) for j in range(BC)], [])
+                def f_round(rnd):
+                    spots = []
+                    for i in rnd:
+                        for j in range(BC):
+                            terms, close, unload = f_position(i, j)
+                            spots.append((plain(terms), (1, vec_ends[rnd], close), (0, 0, unload)))
+                    return spots
 
-                run(spread(sum(v_jobs[0:3], []), c_jobs, distances[0:20]))
-                run(spread(v_jobs[3], f_row(5) + f_row(4), distances[20:30]))
-                run(spread(v_jobs[4], f_row(3), f_conv(5) + f_conv(4), distances[30:37]))
-                run(spread(v_jobs[5], f_row(2), f_conv(3), distances[37:43]))
-                run(spread(v_jobs[6], f_row(1), f_conv(2), distances[43:49]))
-                run(spread(f_row(0), f_conv(1), [partial(finish_affinity, dpool, aff_e, NQ)]))
-                run(f_conv(0))
+                mul += late(f_round(ROUNDS[0]) + f_round(ROUNDS[1]))
+                dis = [(0.3, 0, f) for f in tile_jobs + [e_lengths]] + plain(distances)
+                dis.append((len(distances) * (1 / DIST_PART - 1), 0, lambda: None))
+                interleave([vec, mul, dis], (AHEAD, 0, 0))
 
-        with ExitStack() as ex:
-            xep = ex.enter_context(tc.tile_pool(name="xep", bufs=1))
-            vset = ex.enter_context(tc.tile_pool(name="vset", bufs=4))
-            xqe = xep.tile([P, 5 * CHPX], I32, name="xqe", align_bytes=64)
-            xse = xep.tile([P, 5 * CHPX], U8, name="xse", align_bytes=64)
+            own_pixels = ctx.enter_context(ExitStack())
+            xep = ctx.enter_context(tc.tile_pool(name="xep", bufs=1, side="right", reuse_waits="tile"))
+            xqe = xep.tile([P, 6 * CHPX], I32, name="xqe", align_bytes=64)
+            xse = xep.tile([P, 6 * CHPX], U8, name="xse", align_bytes=64)
             xqe_v = xqe[:].rearrange("p (r z) -> p r z", z=PITCH)
             xse_v = xse[:].rearrange("p (r z) -> p r z", z=PITCH)
+            matp = own_pixels.enter_context(tc.tile_pool(name="matp", bufs=1, side="right", reuse_waits="tile"))
+            mat = matp.tile([P, NTS, 2, NQ], F32, name="mat")
+            nc.gpsimd.memset(mat[LOW:P, NT:NTS, 0, :], 0.0)
+            nc.gpsimd.memset(mat[0:LOW, NT:NTS, 1, :], 0.0)
+            mat_rows = {}
+
+            def spread_row(y, kind):
+                m = matp.tile([P, 64 + TW * P + 160], F32, name="rowmat", bufs=ROWMATS)
+                nc.gpsimd.memset(m[:], 0.0)
+                for dh in range(PAD - y, KW):
+                    r = y + dh - PAD
+                    if kind == 0:
+                        parts = ((0, LOW, TW * r), (LOW, P, TW * (TH - 1 - r)))
+                    else:
+                        parts = ((LOW // 2, LOW, NQ + TW * r),) if r < HALF else ()
+                    for lo, hi, u in parts:
+                        s = 64 + u - PAD
+                        dst = m[lo:hi, s : s + TW * (P + 1)].rearrange("p (x e) -> p x e", e=P + 1)[:, :, 0:KW]
+                        nc.scalar.copy(out=dst, in_=aff_e[lo:hi, dh, :, y, :].rearrange("p d x -> p x d"))
+                for x in range(PAD):
+                    left_px = m[:, 64 + x * P : 64 + (x + 1) * P].rearrange("p (r z) -> p r z", z=TW)
+                    nc.gpsimd.memset(left_px[:, :, TW - PAD + x : TW], 0.0)
+                    right_px = m[:, 64 + (TW - 1 - x) * P : 64 + (TW - x) * P].rearrange("p (r z) -> p r z", z=TW)
+                    nc.gpsimd.memset(right_px[:, :, 0 : PAD - x], 0.0)
+                mat_rows[(y, kind)] = m
+
+            def turn(y, kind, g):
+                ps = ps_misc.tile([P, 4, P], F32, name="ps_m", tag="misc")
+                for k in range(4):
+                    a = 64 + (4 * g + k) * P
+                    nc.tensor.transpose(ps[:, k, :], mat_rows[(y, kind)][:, a : a + P], ident_f[:])
+                q = slice(TW * y + 4 * g, TW * y + 4 * g + 4)
+                src = ps[:].rearrange("p q h -> p h q")
+                if kind == 0:
+                    for half in range(2):
+                        nc.scalar.copy(out=mat[:, 0:NT, half, q], in_=src[:, LOW * half : LOW * half + NT])
+                    nc.scalar.copy(out=mat[0:LOW, NT:NTS, 0, q], in_=src[0:LOW, NT : NT + NS])
+                else:
+                    nc.scalar.copy(out=mat[LOW:P, NT:NTS, 1, q], in_=src[LOW:P, NT + NS : NT + 2 * NS])
+
+            mats = []
+            for y in range(HALF):
+                for kind in range(2):
+                    mats += [partial(spread_row, y, kind)] + [partial(turn, y, kind, g) for g in range(TW // 4)]
+            with tc.tile_pool(name="pack", bufs=1, side="right", reuse_waits="tile") as pack:
+                stage = pack.tile([P, CHPX, T], BF16, name="stage", align_bytes=64)
+                rows = stage[:].rearrange("p (r z) t -> p r z t", z=PITCH)
+                nc.vector.memset(rows[:, :, 0:PAD, :], 0.0)
+                nc.vector.memset(rows[:, :, PAD + W : PITCH, :], 0.0)
+                nc.vector.memset(rows[:, 0:PAD, :, :], 0.0)
+                packs = []
+                for k in range(5):
+                    packs += pack_steps(pack, stage, k * CH - PAD, HE + PAD, xqe, xse, k * CHPX, False, False)
+                packs += pack_steps(pack, stage, S_ROW0, H, xqe, xse, 5 * CHPX, False, True)
+                last = [(size, 0, f) for size, need, f in late(f_round(ROUNDS[2]))]
+                interleave([plain(packs), last, plain(mats)])
+            run([f for n, f in todo])
+
+        with ExitStack() as upper:
+            evp = upper.enter_context(tc.tile_pool(name="evp", bufs=1, reuse_waits="tile"))
+            vset = upper.enter_context(tc.tile_pool(name="vset", bufs=1, reuse_waits="tile"))
             ring = []
             free = []
-
-            def add_ring(pool, n):
-                for k in range(len(ring), len(ring) + n):
-                    ring.append(pool.tile([P, C], F32, name="ring%d" % k))
-                    nc.gpsimd.memset(ring[k][:], 0.0)
-                    free.append(k)
-
-            add_ring(xep, RING_A)
             ready = []
             e_acc = {}
-            e_dn = {}
+            e_own = {}
+            loaded = []
+            row_sets = {}
+            side_sets = {}
+            e_copies = {}
 
-            def take():
-                return free.pop(0)
+            def add_ring(pool, n, eng):
+                for k in range(len(ring), len(ring) + n):
+                    ring.append(pool.tile([P, C], F32, name="ring%d" % k))
+                    eng.memset(ring[k][:], 0.0)
+                    free.append(k)
 
-            def e_set(r, k0, k1):
+            add_ring(evp, RINGS[0], nc.gpsimd)
+
+            places = {}
+            for kind, width, n in (("row", KB, 5), ("side", PAD, 2)):
+                places[kind] = []
+                for k in range(n):
+                    words = vset.tile([P, width, P], I32, name="%s_words%d" % (kind, k), align_bytes=64)
+                    scales = vset.tile([P, width, P], U8, name="%s_scales%d" % (kind, k), align_bytes=64)
+                    nc.gpsimd.memset(words[:], 0)
+                    nc.gpsimd.memset(scales[:], 0)
+                    places[kind].append((words, scales))
+
+            def e_set(r, k0, k1, kind):
                 n = k1 - k0
-                words = vset.tile([P, KB, P], I32, name="words", align_bytes=64)
-                scales = vset.tile([P, KB, P], U8, name="scales", align_bytes=64)
+                words, scales = places[kind].pop(0)
+                places[kind].append((words, scales))
                 base = 0 if k1 <= TW else 8
+                cols = slice(k0 - base, k1 - base)
                 for dst, src in ((words, xqe_v), (scales, xse_v)):
-                    nc.vector.memset(dst[:, 0:n].rearrange("p k (h x) -> p k h x", h=2)[:, :, :, NT:LOW], 0)
                     for half in range(2):
                         s0 = r + PAD if half == 0 else TH - 1 - r + PAD
                         nc.vector.tensor_copy(
                             out=dst[:, 0:n, LOW * half : LOW * half + NT].rearrange("p k (r c) -> p k r c", c=TC),
                             in_=src[:, s0 : s0 + TH * (TR - 1) + 1 : TH, base : base + W].rearrange(
                                 "p r (c x) -> p x r c", x=TW
-                            )[:, k0 - base : k1 - base],
+                            )[:, cols],
                         )
+                    nc.vector.tensor_copy(
+                        out=dst[:, 0:n, NT : NT + 2 * NS].rearrange("p k (h a) -> p k h a", h=2),
+                        in_=src[:, S_BASE + S_ROW - S_ROW0 + r, base : base + W].rearrange(
+                            "p (a h x) -> p x h a", h=2, x=TW
+                        )[:, cols],
+                    )
                 return [(words[:, k], scales[:, k]) for k in range(n)]
 
             def e_weight(y, x, r, k):
                 return aff_e[:, r - y + PAD, k - x, y, x : x + 1]
 
+            def e_columns(k):
+                return range(max(0, k - 2 * PAD), min(TW - 1, k) + 1)
+
             def e_vector_term(y, x, r, k, msg):
-                wgt = e_weight(y, x, r, k)
                 if (y, x) not in e_acc and ready:
                     load_own(y, x)
-                if (y, x) not in e_acc:
-                    e_acc[(y, x)] = take()
-                    dst = ring[e_acc[(y, x)]]
-                    nc.vector.tensor_scalar(out=dst[:], in0=msg[:], scalar1=wgt, scalar2=None, op0=ALU.mult)
-                else:
-                    dst = ring[e_acc[(y, x)]]
-                    nc.vector.scalar_tensor_tensor(
-                        out=dst[:], in0=msg[:], scalar=wgt, in1=dst[:], op0=ALU.mult, op1=ALU.add
-                    )
+                first = (y, x) not in e_acc
+                if first:
+                    e_acc[(y, x)] = free.pop(0)
+                vector_term(ring[e_acc[(y, x)]], first, msg, e_weight(y, x, r, k))
 
-            side_sets = {}
+            def load_own(y, x):
+                if not 0 <= x < TW or (y, x) in loaded or not ready:
+                    return
+                loaded.append((y, x))
+                where = e_own if (y, x) in e_acc else e_acc
+                where[(y, x)] = free.pop(0)
+                dst = ring[where[(y, x)]]
+                for half in range(2):
+                    v = NQ * half + TW * y + x
+                    for p0, n, src in ((LOW * half, NT, park), (NT + NS * half, NS, park_s)):
+                        nc.sync.dma_start(
+                            out=dst[p0 : p0 + n, :].rearrange("p (e f) -> p e f", e=T),
+                            in_=src[:, v, :, :].rearrange("e n f -> n e f"),
+                        )
 
             def side_set(r, k0):
-                side_sets[(r, k0)] = e_set(r, k0, k0 + PAD)
+                side_sets[(r, k0)] = e_set(r, k0, k0 + PAD, "side")
 
-            def side_message(r, k0, k):
-                msg = mx_message(*side_sets[(r, k0)][k - k0])
-                for y in range(max(0, r - PAD), min(HALF - 1, r + PAD) + 1):
-                    for x in range(max(0, k - 2 * PAD), min(TW - 1, k) + 1):
+            def side_message(ys, r, k0, k):
+                msg = mx_message(*side_sets[(r, k0)][k - k0], ps_msg, "msg")
+                for y in range(max(ys[0], r - PAD), min(ys[-1], r + PAD) + 1):
+                    for x in e_columns(k):
                         e_vector_term(y, x, r, k, msg)
 
-            def side_jobs(k0):
+            def side_jobs(ys, k0):
                 jobs = []
-                for r in range(HALF + PAD):
-                    jobs.append(partial(side_set, r, k0))
-                    jobs += [partial(side_message, r, k0, k) for k in range(k0, k0 + PAD)]
+                rows = range(max(0, ys[0] - PAD), ys[-1] + PAD + 1)
+                for r in rows:
+                    if r == rows[0]:
+                        jobs.append((2, 0, partial(side_set, r, k0)))
+                    if r + 1 in rows:
+                        jobs.append((2, 0, partial(side_set, r + 1, k0)))
+                    for k in range(k0, k0 + PAD):
+                        n = (min(ys[-1], r + PAD) - max(ys[0], r - PAD) + 1) * len(e_columns(k))
+                        jobs.append((n, 0, partial(side_message, ys, r, k0, k)))
                 return jobs
 
-            with tc.tile_pool(name="dense", bufs=1) as dense:
-                stages = [dense.tile([P, CHPX, T], BF16, name="stage%d" % k, align_bytes=64) for k in range(2)]
-                for k in range(2):
-                    nc.gpsimd.memset(stages[k][:], 0.0)
-                packs = []
-                for k in range(5):
-                    packs += pack_steps(dense, stages[k % 2], k * CH - PAD, xqe, xse, k * CHPX, HE + PAD)
+            def row_set(r, k0):
+                for k, ws in enumerate(e_set(r, k0, min(k0 + KB, VC), "row")):
+                    row_sets[(r, k0 + k)] = ws
 
-                aff_t = dense.tile([P, KW, KW, HALF, TW], F32, name="aff_t")
-                mat = dense.tile([P, NT, 2, NQ], F32, name="mat")
+            def far_message(r, k):
+                msg = mx_message(*row_sets.pop((r, k)), ps_msg, "msg")
+                for y in range(r + PAD + 1):
+                    for x in e_columns(k):
+                        e_vector_term(y, x, r, k, msg)
 
-                def mask_columns():
-                    nc.vector.tensor_copy(
-                        out=aff_t[:].rearrange("p a b y x -> p (a b y x)"),
-                        in_=aff_e[:].rearrange("p a b y x -> p (a b y x)"),
-                    )
-                    for dw in range(KW):
-                        if dw < PAD:
-                            nc.vector.memset(aff_t[:, :, dw, :, 0 : PAD - dw], 0.0)
-                        if dw > PAD:
-                            nc.vector.memset(aff_t[:, :, dw, :, TW + PAD - dw : TW], 0.0)
+            def near_message(k):
+                e_copies[(-1, k)] = mx_message(*row_sets.pop((-1, k)), ps_misc, "misc")
+                if not ready:
+                    near_copy(k)
+                    copied.append(k)
 
-                rows = {}
+            copied = []
 
-                def spread_row(y):
-                    m = dense.tile([P, 64 + TW * P + 160], F32, name="rowmat", bufs=2)
-                    nc.gpsimd.memset(m[:], 0.0)
-                    for dh in range(PAD - y, KW):
-                        r = y + dh - PAD
-                        for half in range(2):
-                            lo, hi = LOW * half, LOW * half + LOW
-                            s = 64 + TW * (r if half == 0 else TH - 1 - r) - PAD
-                            dst = m[lo:hi, s : s + TW * (P + 1)].rearrange("p (x e) -> p x e", e=P + 1)[:, :, 0:KW]
-                            nc.vector.tensor_copy(out=dst, in_=aff_t[lo:hi, dh, :, y, :].rearrange("p d x -> p x d"))
-                    rows[y] = m
+            def near_copy(k):
+                if k in copied:
+                    return
+                msg = e_copies[(-1, k)]
+                e_copies[(-1, k)] = cpe.tile([P, C], F32, name="cp", bufs=8)
+                nc.scalar.copy(out=e_copies[(-1, k)][:], in_=msg[:])
 
-                def turn(y, g):
-                    ps = ps_misc.tile([P, 4, P], F32, name="ps_m", tag="misc")
-                    for k in range(4):
-                        a = 64 + (4 * g + k) * P
-                        nc.tensor.transpose(ps[:, k, :], rows[y][:, a : a + P], ident_f[:])
-                    q0 = TW * y + 4 * g
-                    src = ps[:].rearrange("p q (h n) -> p h n q", h=2)
+            def column(k):
+                jobs = []
+                if k == 0:
+                    jobs += [(2, 0, partial(row_set, r, 0)) for r in (-3, -2, -1)]
+                nxt = k // KB * KB + KB
+                if nxt < VC and k % KB == KB - 2:
+                    jobs += [(2, 0, partial(row_set, r, nxt)) for r in (-3, -2)]
+                jobs += [(0, 0, partial(load_own, y, k + PRE)) for y in range(2)]
+                jobs += [(0, 0, partial(load_own, y, k - 2 * PAD)) for y in range(2, HALF)]
+                n = len(e_columns(k))
+                jobs += [
+                    (2 * n, 0, partial(far_message, -2, k)),
+                    (1, 0, partial(near_message, k)),
+                    (n, 0, partial(far_message, -3, k)),
+                    (1, 0, partial(near_copy, k)),
+                ]
+                if nxt < VC and k % KB == KB - 1:
+                    jobs.append((2, 0, partial(row_set, -1, nxt)))
+                return jobs
+
+            def e_position(y, x):
+                terms = [x + dw for dw in range(KW)] if y < PAD else []
+                st = {}
+
+                def start():
+                    load_own(y, x)
+                    st["pos"] = ps_pos.tile([P, T, P], F32, name="pos")
+
+                def term(n, k):
+                    add_transposed(st["pos"], product(e_prodp, e_copies[(-1, k)], e_weight(y, x, -1, k)), n == 0, False)
+
+                def close():
+                    rest = [d.pop((y, x)) for d in (e_own, e_acc) if (y, x) in d]
+                    for n, k in enumerate(rest):
+                        add_transposed(st["pos"], ring[k], not terms and n == 0, n == len(rest) - 1)
+                        free.append(k)
+
+                def unload():
                     for half in range(2):
-                        dst = mat[:, :, half, q0 : q0 + 4]
-                        if half == 0:
-                            nc.scalar.copy(out=dst, in_=src[:, half, 0:NT])
-                        else:
-                            nc.vector.tensor_copy(out=dst, in_=src[:, half, 0:NT])
+                        r = y if half == 0 else TH - 1 - y
+                        nc.scalar.copy(
+                            out=groups_t[:, :, r, :, x, :],
+                            in_=st["pos"][:, :, LOW * half : LOW * half + NT].rearrange("p t (a c) -> p a c t", c=TC),
+                        )
+                    nc.scalar.copy(
+                        out=groups_s[:, y, :, :, x, :].rearrange("p a h t -> p h a t"),
+                        in_=st["pos"][:, :, NT : NT + 2 * NS].rearrange("p t (h a) -> p h a t", h=2),
+                    )
 
+                return [start] + [partial(term, n, k) for n, k in enumerate(terms)], close, unload
+
+            e_prodp = upper.enter_context(tc.tile_pool(name="e_prodp", bufs=6, reuse_waits="tile"))
+            cpe = upper.enter_context(tc.tile_pool(name="cpe", bufs=1, reuse_waits="tile"))
+            add_ring(cpe, RINGS[1], nc.gpsimd)
+
+            with own_pixels:
+                dense = own_pixels.enter_context(tc.tile_pool(name="dense", bufs=1, side="right", reuse_waits="tile"))
                 own = {}
+                own_m = {}
+                own_o = {}
 
-                def own_set(tr):
+                def own_set(g):
                     words = dense.tile([P, TC, P], I32, name="own_w", bufs=2, align_bytes=64)
                     scales = dense.tile([P, TC, P], U8, name="own_s", bufs=2, align_bytes=64)
                     for dst, src in ((words, xqe_v), (scales, xse_v)):
-                        nc.vector.tensor_copy(
-                            out=dst[:].rearrange("p c (r x) -> p c r x", x=TW),
-                            in_=src[:, TH * tr + PAD : TH * tr + PAD + TH, PAD : PAD + W].rearrange(
-                                "p r (c x) -> p c r x", x=TW
-                            ),
-                        )
-                    own[tr] = (words, scales)
+                        if g < TR:
+                            nc.vector.tensor_copy(
+                                out=dst[:].rearrange("p c (r x) -> p c r x", x=TW),
+                                in_=src[:, TH * g + PAD : TH * g + PAD + TH, PAD : PAD + W].rearrange(
+                                    "p r (c x) -> p c r x", x=TW
+                                ),
+                            )
+                            continue
+                        for h in range(2):
+                            s0 = S_BASE + S_ROW - S_ROW0
+                            nc.vector.tensor_copy(
+                                out=dst[:, 0:NS, NQ * h : NQ * (h + 1)].rearrange("p a (r x) -> p a r x", x=TW),
+                                in_=src[:, s0 : s0 + HALF, PAD : PAD + W].rearrange(
+                                    "p r (a h x) -> p h a r x", h=2, x=TW
+                                )[:, h],
+                            )
+                    own[g] = (words, scales)
 
                 def own_message(n):
                     words, scales = own[n // TC]
-                    msg = mx_message(words[:, n % TC], scales[:, n % TC])
+                    msg = mx_message(words[:, n % TC], scales[:, n % TC], ps_pos, "pos")
                     own_m[n] = dense.tile([P, C], F32, name="own_m", bufs=3)
                     nc.scalar.copy(out=own_m[n][:], in_=msg[:])
 
@@ -646,152 +986,107 @@ def tile_dcblock_t_kernel(
                         start=True,
                         stop=True,
                     )
-                    res = dense.tile([P, C], F32, name="own_o", bufs=3)
-                    nc.scalar.copy(out=res[:], in_=ps[:])
-                    nc.sync.dma_start(
-                        out=out_s[:, n // 27, :, n % 27, :].rearrange("e v f -> v e f"),
-                        in_=res[:].rearrange("p (e f) -> p e f", e=2),
-                    )
+                    if n % 3 == 0:
+                        own_o[0] = dense.tile([P, T, 3, P], F32, name="own_o", bufs=2)
+                    nc.scalar.copy(out=own_o[0][:, :, n % 3, :], in_=ps[:].rearrange("p (e f) -> p e f", e=T))
+                    if n % 3 == 2:
+                        dst = park[:, :, n - 2 : n + 1, :] if n < NT else park_s
+                        nc.sync.dma_start(out=dst.rearrange("e v n f -> v e n f"), in_=own_o[0][:])
 
-                own_m = {}
-                mats = [mask_columns]
-                for y in range(HALF):
-                    mats += [partial(spread_row, y)] + [partial(turn, y, g) for g in range(TW // 4)]
-                owns = []
-                for tr in range(TR):
-                    owns.append(partial(own_set, tr))
-                    for n in range(tr * TC, tr * TC + TC):
+                owns = [partial(own_set, 0)]
+                for n in range(NTS + 2):
+                    if n < NT and n % TC == 0:
+                        owns.append(partial(own_set, n // TC + 1))
+                    if n < NTS:
                         owns.append(partial(own_message, n))
-                        if n > 0:
-                            owns.append(partial(own_sum, n - 1))
-                owns.append(partial(own_sum, NT - 1))
-                left = side_jobs(0)
-                run(spread(packs, mats))
-                run(spread(owns, left))
+                    if n >= 2:
+                        owns.append(partial(own_sum, n - 2))
+                vec = side_jobs(range(HALF), 0)
+                for k in range(FIRST):
+                    vec += column(k)
+                interleave([vec, plain(owns)])
 
-            gpool = ex.enter_context(tc.tile_pool(name="gpool", bufs=1))
-            grp_e = gpool.tile([P, HE * W, T], BF16, name="grp_e", align_bytes=64)
-            add_ring(gpool, RING_B)
-            with ExitStack() as e2:
-                prodp = e2.enter_context(tc.tile_pool(name="prode", bufs=6))
-                cpe = e2.enter_context(tc.tile_pool(name="cpe", bufs=8))
-                row_sets = {}
-                copies = {}
+            gpool = ctx.enter_context(tc.tile_pool(name="gpool", bufs=1, side="right", reuse_waits="tile"))
+            grp = gpool.tile([P, (HE + HALF) * W, T], BF16, name="grp", align_bytes=64)
+            groups_t = grp[:, 0 : HE * W].rearrange("p (a r c x) t -> p a r c x t", r=TH, c=TC, x=TW)
+            groups_s = grp[:, HE * W : (HE + HALF) * W].rearrange("p (r a h x) t -> p r a h x t", a=NS, h=2, x=TW)
+            add_ring(gpool, RINGS[2], nc.gpsimd)
+            ready.append(True)
+            right = [(k0, k1, ys, side_jobs(ys, VC - PAD)) for k0, k1, ys in RIGHT]
+            spots = []
+            ends = [0]
+            resting = []
+            for x in range(TW + 1):
+                spots_x = [e_position(y, x) for y in range(HALF)] if x < TW else []
+                spots += [(plain(a), (1, 0, b), (0, 0, f)) for a, b, f in spots_x[0:PAD] + resting]
+                resting = spots_x[PAD:]
+                ends.append(sum([len(e[0]) + 2 for e in spots]) - 3)
+            spots = late(spots)
+            for k in range(FIRST, VC + 2):
+                vec = column(k) if k < VC else []
+                sides = []
+                for k0, k1, ys, jobs in right:
+                    if k0 - PAD <= k < k0:
+                        vec += [(0, 0, partial(load_own, y, TW + k - k0)) for y in ys]
+                    if k0 <= k < k1:
+                        sides += jobs[len(jobs) * (k - k0) // (k1 - k0) : len(jobs) * (k - k0 + 1) // (k1 - k0)]
+                x = k - 2 * PAD - 1
+                mul = spots[ends[x] : ends[x + 1]] if 0 <= x < TW else spots[ends[TW] :] if x == TW else []
+                interleave([vec, sides, mul])
 
-                ready.append(True)
+        with tc.tile_pool(name="tail", bufs=2, side="right", reuse_waits="tile") as tail:
+            NPX = TH * W
+            bands = [(TH * n, TH) for n in range(TR)] + [(S_ROW, HALF)]
+            banks = ((ps_misc, "misc"), (ps_pos, "pos"), (ps_msg, "msg"), (ps_pos, "pos"), (ps_msg, "msg"))
+            turn_no = [0]
+            res = {}
+            args = {}
 
-                def load_own(y, x):
-                    where = e_dn if (y, x) in e_acc else e_acc
-                    where[(y, x)] = take()
-                    dst = ring[where[(y, x)]]
-                    for half in range(2):
-                        v = NQ * half + TW * y + x
-                        for b in range(2):
-                            p0 = LOW * half + 27 * b
-                            nc.sync.dma_start(
-                                out=dst[p0 : p0 + 27, :].rearrange("p (e f) -> p e f", e=2),
-                                in_=out_s[:, b, v, :, :].rearrange("e k f -> k e f"),
-                            )
+            def t_load(n):
+                r0, nr = bands[n]
+                res[n] = tail.tile([P, T, NPX], BF16, name="x_res", bufs=4)
+                nc.sync.dma_start(
+                    out=res[n][:, :, 0 : nr * W].rearrange("p t (h w) -> p t h w", w=W), in_=x_r[:, :, r0 : r0 + nr, :]
+                )
 
-                def row_set(r, k0):
-                    for k, ws in enumerate(e_set(r, k0, min(k0 + KB, VC))):
-                        row_sets[(r, k0 + k)] = ws
+            def t_cuts(n):
+                px = bands[n][1] * W
+                return ((0, px * 2 // 3), (px * 2 // 3, px))
 
-                def far_message(k):
-                    msg = mx_message(*row_sets.pop((-3, k)))
-                    for x in range(max(0, k - 2 * PAD), min(TW - 1, k) + 1):
-                        e_vector_term(0, x, -3, k, msg)
-
-                def mid_message(k):
-                    msg = mx_message(*row_sets.pop((-2, k)))
-                    copies[(-2, k)] = cpe.tile([P, C], F32, name="cp_mid")
-                    nc.scalar.copy(out=copies[(-2, k)][:], in_=msg[:])
-                    for x in range(max(0, k - 2 * PAD), min(TW - 1, k) + 1):
-                        e_vector_term(1, x, -2, k, msg)
-
-                def near_message(k):
-                    msg = mx_message(*row_sets.pop((-1, k)))
-                    copies[(-1, k)] = cpe.tile([P, C], F32, name="cp_near")
-                    nc.scalar.copy(out=copies[(-1, k)][:], in_=msg[:])
-
-                def e_position(y, x):
-                    st = {}
-                    jobs = []
-                    terms = [(r, x + dw) for r in (-1, -2) if r >= y - PAD and not (y == 1 and r == -2) for dw in range(KW)]
-
-                    def term(n, r, k):
-                        if n == 0:
-                            st["pos"] = ps_pos.tile([P, T, P], F32, name="pos")
-                        prod = product(prodp, copies[(r, k)], e_weight(y, x, r, k))
-                        add_transposed(st["pos"], prod, n == 0, False)
-
-                    def close():
-                        if not terms:
-                            st["pos"] = ps_pos.tile([P, T, P], F32, name="pos")
-                        rest = [d.pop((y, x)) for d in (e_dn, e_acc) if (y, x) in d]
-                        for n, k in enumerate(rest):
-                            add_transposed(st["pos"], ring[k], not terms and n == 0, n == len(rest) - 1)
-                            free.append(k)
-                        for half in range(2):
-                            r = y if half == 0 else TH - 1 - y
-                            nc.scalar.copy(
-                                out=grp_e[:].rearrange("p (a r c x) t -> p a r c x t", r=TH, c=TC, x=TW)[:, :, r, :, x, :],
-                                in_=st["pos"][:, :, LOW * half : LOW * half + NT].rearrange("p t (a c) -> p a c t", c=TC),
-                            )
-
-                    for n, (r, k) in enumerate(terms):
-                        jobs.append(partial(term, n, r, k))
-                    jobs.append(close)
-                    return jobs
-
-                right = side_jobs(VC - PAD)
-                for k in range(VC + LAG):
-                    v_list = []
-                    if k < VC:
-                        if k % KB == 0:
-                            v_list += [partial(row_set, r, k) for r in (-3, -2, -1)]
-                        v_list += [partial(far_message, k), partial(mid_message, k), partial(near_message, k)]
-                    if R0 <= k < 19:
-                        v_list += right[len(right) * (k - R0) // (19 - R0) : len(right) * (k - R0 + 1) // (19 - R0)]
-                    x_pos = k - 2 * PAD - LAG
-                    p_list = []
-                    if 0 <= x_pos < TW:
-                        p_list = [partial(load_own, y, x_pos) for y in range(HALF) if x_pos < PAD or (y, x_pos) not in e_acc]
-                        for y in range(HALF):
-                            p_list += e_position(y, x_pos)
-                    lists = [a for a in (v_list, p_list) if a]
-                    run(spread(*lists))
-
-            with tc.tile_pool(name="tail", bufs=2) as tail:
-                npx = TH * W
-                for tr in range(TR):
-                    x_res = tail.tile([P, T, npx], BF16, name="x_res")
-                    nc.sync.dma_start(
-                        out=x_res[:].rearrange("p t (h w) -> p t h w", w=W), in_=x_r[:, :, TH * tr : TH * tr + TH, :]
+            def t_quant(n):
+                aq = tail.tile([P, NPX], I32, name="aq", align_bytes=64)
+                asc = tail.tile([P, NPX], U8, name="asc", align_bytes=64)
+                flat = grp[:, n * NPX : n * NPX + bands[n][1] * W, :].rearrange("p u t -> p (u t)")
+                for c0, c1 in t_cuts(n):
+                    nc.vector.quantize_mx(
+                        out=aq[:, c0:c1].bitcast(FP8X4), scales=asc[:, c0:c1], in_=flat[:, T * c0 : T * c1]
                     )
-                    aq = tail.tile([P, npx], I32, name="aq", align_bytes=64)
-                    asc = tail.tile([P, npx], U8, name="asc", align_bytes=64)
-                    flat = grp_e[:, tr * npx : (tr + 1) * npx, :].rearrange("p u t -> p (u t)")
-                    for c0, c1 in ((0, 512), (512, 768)):
-                        nc.vector.quantize_mx(
-                            out=aq[:, c0:c1].bitcast(FP8X4), scales=asc[:, c0:c1], in_=flat[:, T * c0 : T * c1]
+                args[n] = (aq, asc)
+
+            def t_out(n, m):
+                r0, nr = bands[n]
+                o_sb = tail.tile([P, NPX], F32, name="o_sb", bufs=6)
+                for c0, c1 in t_cuts(n):
+                    pool, tag = banks[turn_no[0] % len(banks)]
+                    turn_no[0] += 1
+                    o_ps = pool.tile([P, c1 - c0], F32, name="o_ps", tag=tag)
+                    second_conv(*args[n], c0, c1, m, o_ps[:])
+                    if m == T - 1:
+                        nc.scalar.copy(out=o_sb[:, c0:c1], in_=o_ps[:])
+                        nc.gpsimd.tensor_tensor(
+                            out=o_sb[:, c0:c1], in0=o_sb[:, c0:c1], in1=res[n][:, m, c0:c1], op=ALU.add
                         )
-                    for m in range(T):
-                        o_sb = tail.tile([P, npx], F32, name="o_sb")
-                        for c0, c1 in ((0, 512), (512, 768)):
-                            o_ps = ps_misc.tile([P, c1 - c0], F32, name="o_ps", tag="misc")
-                            nc.tensor.matmul_mx(
-                                out=o_ps[:],
-                                lhsT=w2q[:, m * P : (m + 1) * P].bitcast(FP8X4),
-                                lhsT_scale=w2s[:, m * P : (m + 1) * P],
-                                rhs=aq[:, c0:c1].bitcast(FP8X4),
-                                rhs_scale=asc[:, c0:c1],
-                                start=True,
-                                stop=True,
-                            )
-                            nc.vector.tensor_tensor(
-                                out=o_sb[:, c0:c1], in0=o_ps[:], in1=x_res[:, m, c0:c1], op=ALU.add
-                            )
-                        nc.sync.dma_start(
-                            out=out_v[m, :, TH * tr : TH * tr + TH, :], in_=o_sb[:].rearrange("p (h w) -> p h w", w=W)
-                        )
+                    else:
+                        nc.vector.tensor_tensor(out=o_sb[:, c0:c1], in0=o_ps[:], in1=res[n][:, m, c0:c1], op=ALU.add)
+                nc.sync.dma_start(
+                    out=out_v[m, :, r0 : r0 + nr, :], in_=o_sb[:, 0 : nr * W].rearrange("p (h w) -> p h w", w=W)
+                )
+
+            run([partial(t_load, n) for n in range(3)] + [partial(t_quant, 0)])
+            for n in range(len(bands)):
+                for m in range(T):
+                    if m == 0 and n + 3 < len(bands):
+                        t_load(n + 3)
+                    if m == 1 and n + 1 < len(bands):
+                        t_quant(n + 1)
+                    t_out(n, m)

from contextlib import ExitStack
from functools import partial

import concourse.mybir as mybir
from concourse.masks import make_identity

F32 = mybir.dt.float32
BF16 = mybir.dt.bfloat16
I32 = mybir.dt.int32
U8 = mybir.dt.uint8
FP8X4 = mybir.dt.float8_e4m3fn_x4
ALU = mybir.AluOpType
ACT = mybir.ActivationFunctionType
AX = mybir.AxisListType

P = 128
C = 512
CP = 19
H = 96
W = 96
KW = 7
PAD = 3
T = 4
TH = 8
TW = 16
TR = 9
TC = W // TW
NT = TR * TC
HE = TR * TH
HALF = TH // 2
NQ = HALF * TW
LOW = 64
NS = 3
S_ROW = H - HALF
NTS = NT + NS
VR = HALF + 2 * PAD
VC = TW + 2 * PAD
VX = 24
BR = 5
BC = 3
BA = 4
BW = W // BC
ROWPX = BA * W
IR = BR + 2 * PAD
JC = BC + 2 * PAD
NPOS = BR * BC
BI = BW + 2 * PAD // BC
PITCH = 104
CH = 16
CHPX = CH * PITCH
F_ROW0 = HE - PAD
S_ROW0 = S_ROW - 6
S_BASE = 5 * CH
HZP = W + 2 * PAD
MUL_ROWS = (6, 5, 4, 3)
VEC_TOO = {3: (4, 3, 2), 6: (0,)}
ROUNDS = ((4, 3), (2, 1), (0,))
AHEAD = 0.12
DIST_PART = 0.9
CONV_LATE = 8
RINGS = (12, 8, 16)
KB = 3
ROWMATS = 2
FIRST = 4
PRE = 1
RIGHT = ((12, 17, (2, 3)), (17, 21, (0, 1)))

FLOPS = 2 * 2 * C * C * H * W + 2 * KW * KW * C * H * W


def spread(*lists):
    order = []
    for n, items in enumerate(lists):
        for k, f in enumerate(items):
            order.append(((k + 0.5) / len(items), n, k, f))
    return [e[3] for e in sorted(order, key=lambda e: e[0:3])]


def late(positions):
    jobs = []
    for n in range(len(positions) + 2):
        terms = positions[n][0] if n < len(positions) else []
        if n >= 2:
            jobs.append(positions[n - 2][2])
        jobs += terms[0 : len(terms) // 2]
        if 1 <= n <= len(positions):
            jobs.append(positions[n - 1][1])
        jobs += terms[len(terms) // 2 :]
    return jobs


def interleave(streams, lead=None):
    total = [max(0.001, sum([e[0] for e in jobs])) for jobs in streams]
    done = [0 for jobs in streams]
    at = [0 for jobs in streams]

    def emit(s):
        size, need, job = streams[s][at[s]]
        at[s] += 1
        while at[0] < need:
            emit(0)
        job()
        done[s] += size

    def place(s):
        return ((done[s] + streams[s][at[s]][0] / 2) / total[s] - (lead[s] if lead else 0), s)

    while True:
        rest = [s for s in range(len(streams)) if at[s] < len(streams[s])]
        if not rest:
            return
        emit(min(rest, key=place))


def plain(jobs):
    return [(1, 0, f) for f in jobs]


def run(jobs):
    for f in jobs:
        f()


def tile_dcblock_t_kernel(
    tc, x, coarse_probs, sigma, w_feat, w_fuse, bn_gamma, bn_beta, bn_mean, bn_var, out
):
    nc = tc.nc
    with ExitStack() as ctx:
        const = ctx.enter_context(tc.tile_pool(name="const", bufs=1))
        ps_msg = ctx.enter_context(tc.psum_pool(name="ps_msg", bufs=3))
        ps_pos = ctx.enter_context(tc.psum_pool(name="ps_pos", bufs=3))
        ps_misc = ctx.enter_context(tc.psum_pool(name="ps_misc", bufs=2))

        ident_b = const.tile([P, P], BF16, name="ident_b")
        make_identity(nc, ident_b[:])
        ident_f = const.tile([P, P], F32, name="ident_f")
        make_identity(nc, ident_f[:])
        aff_e = const.tile([P, KW, KW, HALF, TW], F32, name="aff_e")
        w1q = const.tile([P, C], I32, name="w1q", align_bytes=64)
        w1s = const.tile([P, C], U8, name="w1s", align_bytes=64)
        w2q = const.tile([P, C], I32, name="w2q", align_bytes=64)
        w2s = const.tile([P, C], U8, name="w2s", align_bytes=64)
        bsc = const.tile([P, T], F32, name="bsc")
        bbi = const.tile([P, T], F32, name="bbi")
        neginv = const.tile([P, 1], F32, name="neginv")
        twoinv = const.tile([P, 1], F32, name="twoinv")
        negone = const.tile([P, 1], F32, name="negone")
        nc.vector.memset(negone[:], -1.0)

        probs = coarse_probs[0]
        x_k = x[0].rearrange("(p t) h w -> p t h w", t=T)
        x_r = x[0].rearrange("(t p) h w -> p t h w", p=P)
        out_v = out[0].rearrange("(m p) h w -> m p h w", p=P)
        out_c = out[0].rearrange("c h w -> c (h w)")
        park = out_c[:, 0 : HE * W].rearrange("(e v) (n f) -> e v n f", v=P, f=P)
        park_s = out_c[:, S_ROW * W : H * W].rearrange("(e v) (n f) -> e v n f", v=P, f=P)

        def mx_message(words, scales, pool, tag):
            msg = pool.tile([P, C], F32, name="msg", tag=tag)
            nc.tensor.matmul_mx(
                out=msg[:],
                lhsT=words.bitcast(FP8X4),
                lhsT_scale=scales,
                rhs=w1q[:].bitcast(FP8X4),
                rhs_scale=w1s[:],
                start=True,
                stop=True,
            )
            return msg

        def add_transposed(pos, src, first, last):
            for t in range(T):
                nc.tensor.matmul(
                    out=pos[:, t, :],
                    lhsT=src[:, t * P : (t + 1) * P],
                    rhs=ident_f[:],
                    is_transpose=True,
                    start=(first and t == 0),
                    stop=(last and t == T - 1),
                )

        def vector_term(dst, first, msg, wgt):
            if first:
                nc.vector.tensor_scalar(out=dst[:], in0=msg[:], scalar1=wgt, scalar2=None, op0=ALU.mult)
            else:
                nc.vector.scalar_tensor_tensor(
                    out=dst[:], in0=msg[:], scalar=wgt, in1=dst[:], op0=ALU.mult, op1=ALU.add
                )

        def product(pool, src, wgt):
            prod = pool.tile([P, C], F32, name="prod")
            nc.scalar.activation(out=prod[:], in_=src[:], func=ACT.Copy, scale=wgt)
            return prod

        def pack_steps(pool, stage, row0, r_hi, xq, xs, base, by_blocks, clear):
            v0 = max(0, row0)
            v1 = min(r_hi, row0 + CH)
            n = v1 - v0
            rows = stage[:].rearrange("p (r z) t -> p r z t", z=PITCH)
            st = {}

            def load():
                st["x"] = pool.tile([P, T, CH * W], BF16, name="x_in", bufs=2)
                nc.sync.dma_start(
                    out=st["x"][:, :, 0 : n * W].rearrange("p t (h w) -> p t h w", w=W), in_=x_k[:, :, v0:v1, :]
                )

            def norm():
                for t in range(T):
                    nc.vector.tensor_scalar(
                        out=st["x"][:, t, 0 : n * W],
                        in0=st["x"][:, t, 0 : n * W],
                        scalar1=bsc[:, t : t + 1],
                        scalar2=bbi[:, t : t + 1],
                        op0=ALU.mult,
                        op1=ALU.add,
                    )

            def group(half):
                a = n // 2 * half
                b = n // 2 if half == 0 else n
                src = st["x"][:, :, a * W : b * W].rearrange("p t (r w) -> p r w t", w=W)
                dst = rows[:, v0 - row0 + a : v0 - row0 + b]
                if not by_blocks:
                    nc.vector.tensor_copy(out=dst[:, :, PAD : PAD + W, :], in_=src)
                    return
                for k in range(BC):
                    eng_copy = nc.vector.tensor_copy if k == 0 else nc.scalar.copy
                    eng_copy(out=dst[:, :, BI * k + 1 : BI * k + 1 + BW, :], in_=src[:, :, k:W:BC, :])

            def quant():
                if clear:
                    nc.vector.memset(rows[:, n:CH, :, :], 0.0)
                flat = stage[:].rearrange("p u t -> p (u t)")
                for c0, c1 in ((0, 1024), (1024, 1536), (1536, CHPX)):
                    nc.vector.quantize_mx(
                        out=xq[:, base + c0 : base + c1].bitcast(FP8X4),
                        scales=xs[:, base + c0 : base + c1],
                        in_=flat[:, T * c0 : T * c1],
                    )

            return [load, norm, partial(group, 0), partial(group, 1), quant]

        def second_conv(aq, asc, c0, c1, m, o_ps):
            nc.tensor.matmul_mx(
                out=o_ps,
                lhsT=w2q[:, m * P : (m + 1) * P].bitcast(FP8X4),
                lhsT_scale=w2s[:, m * P : (m + 1) * P],
                rhs=aq[:, c0:c1].bitcast(FP8X4),
                rhs_scale=asc[:, c0:c1],
                start=True,
                stop=True,
            )

        def finish_affinity(pool, aff, nq):
            flat = aff[:].rearrange("p a b i j -> p (a b i j)")
            nc.scalar.activation(out=flat, in_=flat, func=ACT.Exp, bias=negone[:, 0:1])
            ssum = pool.tile([P, nq], F32, name="ssum")
            nc.vector.tensor_reduce(
                out=ssum[:], in_=aff[:].rearrange("p a b i j -> p (i j) (a b)"), axis=AX.X, op=ALU.add
            )
            nc.vector.reciprocal(out=ssum[:], in_=ssum[:])
            by_off = aff[:].rearrange("p a b i j -> p (a b) (i j)")
            nc.vector.tensor_tensor(
                out=by_off, in0=by_off, in1=ssum[:].unsqueeze(1).to_broadcast([P, KW * KW, nq]), op=ALU.mult
            )

        with ExitStack() as lower:
            affp = lower.enter_context(tc.tile_pool(name="affp", bufs=1))
            aff_f = affp.tile([P, KW, KW, BR, BC], F32, name="aff_f")
            with ExitStack() as start:
                xqp = start.enter_context(tc.tile_pool(name="xqp", bufs=1, side="right"))
                dpool = start.enter_context(tc.tile_pool(name="dpool", bufs=2, side="right"))
                xqf = xqp.tile([P, 2 * CHPX], I32, name="xqf", align_bytes=64)
                xsf = xqp.tile([P, 2 * CHPX], U8, name="xsf", align_bytes=64)
                p_e = xqp.tile([P, CP, VR, VX], BF16, name="p_e")
                nh = xqp.tile([P, VR, VX], F32, name="nh")
                nv = xqp.tile([P, 2, NQ], F32, name="nv")
                natp = start.enter_context(tc.tile_pool(name="natp", bufs=1, side="right"))
                nat_f = natp.tile([P, 30, HZP], BF16, name="nat_f")
                nat_e = natp.tile([P, 78, HZP], BF16, name="nat_e")
                nc.vector.memset(nat_f[:], 0.0)
                nc.vector.memset(nat_e[:], 0.0)

                with tc.tile_pool(name="head", bufs=1, side="right", reuse_waits="tile") as head:
                    stages = [head.tile([P, CHPX, T], BF16, name="stage%d" % k, align_bytes=64) for k in range(2)]
                    for k in range(2):
                        nc.gpsimd.memset(stages[k][:], 0.0)

                    def load_probs(nat, lo, hi, y0):
                        for s in range(2):
                            for j in range(BC):
                                g = s * BC + j
                                skip = max(0, s - y0)
                                for c0, c1 in ((0, 16), (16, CP)):
                                    nc.sync.dma_start(
                                        out=nat[
                                            CP * g + c0 : CP * g + c1,
                                            y0 - s + skip : y0 - s + hi - lo,
                                            PAD - j : PAD - j + W,
                                        ],
                                        in_=probs[c0:c1, lo + skip : hi, :],
                                    )

                    sg = head.tile([P, 1], BF16, name="sg")
                    nc.sync.dma_start(out=sg[:], in_=sigma.partition_broadcast(P))
                    load_probs(nat_f, F_ROW0, H, 0)
                    prm = []
                    for k, vec in enumerate((bn_gamma, bn_beta, bn_mean, bn_var)):
                        prm.append(head.tile([P, T], BF16, name="prm%d" % k))
                        nc.sync.dma_start(out=prm[k][:], in_=vec.rearrange("(p t) -> p t", t=T))
                    w_sb = [head.tile([P, T, C], BF16, name="w_sb%d" % k) for k in range(2)]
                    nc.sync.dma_start(out=w_sb[0][:], in_=w_feat.rearrange("(p a) c -> p a c", a=T))
                    packs = [
                        pack_steps(head, stages[n], F_ROW0 + n * CH, H, xqf, xsf, n * CHPX, True, False) for n in range(2)
                    ]
                    packs[0][0]()
                    packs[1][0]()
                    load_probs(nat_e, 0, HE + PAD, PAD)
                    nc.sync.dma_start(out=w_sb[1][:], in_=w_fuse.rearrange("(a p) c -> p a c", a=T))

                    sf = head.tile([P, 1], F32, name="sf")
                    nc.vector.tensor_scalar(out=sf[:], in0=sg[:], scalar1=0.0, scalar2=None, op0=ALU.max)
                    nc.vector.tensor_tensor(out=sf[:], in0=sf[:], in1=sf[:], op=ALU.mult)
                    nc.vector.tensor_scalar(out=sf[:], in0=sf[:], scalar1=2.0, scalar2=1e-8, op0=ALU.mult, op1=ALU.add)
                    nc.vector.reciprocal(out=sf[:], in_=sf[:])
                    nc.vector.tensor_scalar(out=neginv[:], in0=sf[:], scalar1=-1.0, scalar2=None, op0=ALU.mult)
                    nc.vector.tensor_scalar(out=twoinv[:], in0=sf[:], scalar1=2.0, scalar2=None, op0=ALU.mult)

                    n_y2 = (IR + 1) // 2
                    p_f = head.tile([P, 2 * n_y2, JC, CP], BF16, name="p_f")
                    gat_f = head.tile([P, n_y2, BC, P], BF16, name="gat_f")
                    for y2 in range(n_y2):
                        for x3 in range(BC):
                            src = nat_f[
                                :, 2 * y2 : 2 * y2 + BR * (BA - 1) + 1 : BR, BC * x3 : BC * x3 + BC * (BW - 1) + 1 : BC
                            ]
                            dst = gat_f[:, y2, x3, :].rearrange("p (a w) -> p a w", a=BA)
                            if (y2 + x3) % 2 == 0:
                                nc.vector.tensor_copy(out=dst, in_=src)
                            else:
                                nc.scalar.copy(out=dst, in_=src)
                    for y2 in range(n_y2):
                        ps = ps_misc.tile([P, BC, P], BF16, name="ps_p", tag="misc")
                        for x3 in range(BC):
                            nc.tensor.transpose(ps[:, x3, :], gat_f[:, y2, x3, :], ident_b[:])
                        nc.vector.tensor_copy(
                            out=p_f[:, 2 * y2 : 2 * y2 + 2].rearrange("p s (x j) c -> p s x (j c)", j=BC),
                            in_=ps[:, :, 0 : 6 * CP].rearrange("p x (s k) -> p s x k", s=2),
                        )

                    NF = NPOS * CP
                    diffs = {}

                    def f_diff(dh):
                        diffs[dh] = head.tile([P, KW, -(-NF // 8) * 8], F32, name="diff", bufs=3)
                        for dw in range(KW):
                            eng = nc.vector if dw in (1, 4) else nc.gpsimd
                            eng.tensor_tensor(
                                out=diffs[dh][:, dw, 0:NF].rearrange("p (i k) -> p i k", i=BR),
                                in0=p_f[:, dh : dh + BR, dw : dw + BC, :].rearrange("p i j c -> p i (j c)"),
                                in1=p_f[:, PAD : PAD + BR, PAD : PAD + BC, :].rearrange("p i j c -> p i (j c)"),
                                op=ALU.subtract,
                            )

                    def f_square(dh):
                        flat = diffs[dh][:, :, 0:NF]
                        nc.scalar.activation(out=flat, in_=flat, func=ACT.Square)

                    def f_reduce(dh):
                        nc.vector.tensor_reduce(
                            out=aff_f[:, dh].rearrange("p d i j -> p d (i j)"),
                            in_=diffs.pop(dh)[:, :, 0:NF].rearrange("p d (q c) -> p d q c", c=CP),
                            axis=AX.X,
                            op=ALU.add,
                        )

                    def f_softmax():
                        flat = aff_f[:].rearrange("p a b i j -> p (a b i j)")
                        nc.scalar.activation(out=flat, in_=flat, func=ACT.Exp, scale=neginv[:, 0:1])
                        finish_affinity(head, aff_f, NPOS)

                    block_jobs = []
                    for dh in range(KW + 2):
                        for step, f in enumerate((f_diff, f_square, f_reduce)):
                            if 0 <= dh - step < KW:
                                block_jobs.append(partial(f, dh - step))
                    block_jobs.append(f_softmax)

                    sd = head.tile([P, T], F32, name="sd")
                    nc.vector.tensor_scalar(out=sd[:], in0=prm[3][:], scalar1=1e-5, scalar2=None, op0=ALU.add)
                    nc.scalar.activation(out=sd[:], in_=sd[:], func=ACT.Sqrt)
                    nc.vector.reciprocal(out=sd[:], in_=sd[:])
                    nc.vector.tensor_tensor(out=bsc[:], in0=prm[0][:], in1=sd[:], op=ALU.mult)
                    ms = head.tile([P, T], F32, name="ms")
                    nc.vector.tensor_tensor(out=ms[:], in0=prm[2][:], in1=bsc[:], op=ALU.mult)
                    nc.vector.tensor_tensor(out=bbi[:], in0=prm[1][:], in1=ms[:], op=ALU.subtract)

                    w_gr = [head.tile([P, C, T], BF16, name="w_gr%d" % k, align_bytes=64) for k in range(2)]

                    def w_turn(k, a):
                        w_t = ps_misc.tile([P, T, P], BF16, name="w_t", tag="misc")
                        for t in range(T):
                            nc.tensor.transpose(w_t[:, t, :], w_sb[k][:, a, t : C : T], ident_b[:])
                        nc.scalar.copy(out=w_gr[k][:, a * P : (a + 1) * P, :], in_=w_t[:].rearrange("p t o -> p o t"))

                    def w_quant(k):
                        wq, wsc = ((w1q, w1s), (w2q, w2s))[k]
                        nc.vector.quantize_mx(
                            out=wq[:].bitcast(FP8X4), scales=wsc[:], in_=w_gr[k][:].rearrange("p o t -> p (o t)")
                        )

                    w_jobs = [partial(w_turn, k, a) for k in range(2) for a in range(T)]

                    run(
                        spread(
                            block_jobs,
                            w_jobs[0:T] + [partial(w_quant, 0)] + packs[0][1:] + packs[1][1:] + w_jobs[T:] + [partial(w_quant, 1)],
                        )
                    )

                gathered = {}
                turned = {}

                def e_gather(u):
                    gathered[u] = natp.tile([P, 8, P], BF16, name="gat_e", bufs=2)
                    nc.gpsimd.memset(gathered[u][:], 0.0)
                    for x3 in range(8):
                        z0 = BC * x3
                        z1 = z0 + TW * (TC - 1) + 1
                        for half in range(2):
                            y0 = 2 * u + HALF * half
                            nc.scalar.copy(
                                out=gathered[u][:, x3, LOW * half : LOW * half + NT].rearrange("p (r c) -> p r c", c=TC),
                                in_=nat_e[:, y0 : y0 + TH * (TR - 1) + 1 : TH, z0:z1:TW],
                            )
                        nc.scalar.copy(
                            out=gathered[u][:, x3, NT : NT + 2 * NS].rearrange("p (h a) -> p h a", h=2),
                            in_=nat_f[:, S_ROW - PAD - F_ROW0 + 2 * u, z0:z1:TW].rearrange("p (a h) -> p h a", h=2),
                        )

                def e_turn(u, g):
                    turned[(u, g)] = ps_misc.tile([P, 4, P], BF16, name="ps_p", tag="misc")
                    for k in range(4):
                        nc.tensor.transpose(turned[(u, g)][:, k, :], gathered[u][:, 4 * g + k, :], ident_b[:])

                def e_unload(u, g):
                    ps = turned.pop((u, g))
                    for half in range(2):
                        for s in range(2):
                            row = 2 * u + s if half == 0 else VR - 1 - 2 * u - s
                            dst = p_e[LOW * half : LOW * half + LOW, :, row, 12 * g : 12 * g + 12]
                            src = ps[LOW * half : LOW * half + LOW, :, 3 * CP * s : 3 * CP * (s + 1)]
                            dst = dst.rearrange("p c (x j) -> p c x j", j=BC)
                            src = src.rearrange("p x (j c) -> p c x j", j=BC)
                            if s == 0:
                                nc.vector.tensor_copy(out=dst, in_=src)
                            else:
                                nc.scalar.copy(out=dst, in_=src)

                def e_lengths():
                    for rows in (slice(0, VR // 2), slice(VR // 2, VR)):
                        sq = dpool.tile([P, CP, VR // 2 * VX], F32, name="sq", tag="pr")
                        nc.scalar.activation(
                            out=sq[:], in_=p_e[:, :, rows, :].rearrange("p c y x -> p c (y x)"), func=ACT.Square
                        )
                        nc.vector.tensor_reduce(
                            out=nh[:, rows, :].rearrange("p y x -> p (y x)"),
                            in_=sq[:].rearrange("p c z -> p z c"),
                            axis=AX.X,
                            op=ALU.add,
                        )
                    nc.vector.tensor_scalar(out=nh[:], in0=nh[:], scalar1=-0.5, scalar2=None, op0=ALU.mult)
                    for n in range(2):
                        nc.scalar.copy(
                            out=nv[:, n].rearrange("p (y x) -> p y x", x=TW),
                            in_=nh[:, PAD : PAD + HALF, PAD : PAD + TW],
                        )

                tile_jobs = [partial(e_gather, 0)]
                turns = [(u, g) for u in range(VR // 2) for g in range(2)]
                for n in range(len(turns) + 1):
                    if n < len(turns):
                        if n % 2 == 0 and n + 2 < len(turns):
                            tile_jobs.append(partial(e_gather, n // 2 + 1))
                        tile_jobs.append(partial(e_turn, *turns[n]))
                    if n > 0:
                        tile_jobs.append(partial(e_unload, *turns[n - 1]))
                cpool = lower.enter_context(tc.tile_pool(name="cpool", bufs=1, reuse_waits="tile"))
                accp = lower.enter_context(tc.tile_pool(name="accp", bufs=len(ROUNDS[2]) * BC))
                prodp = lower.enter_context(tc.tile_pool(name="prodp", bufs=6))
                st2 = lower.enter_context(tc.tile_pool(name="st2", bufs=2))
                cpool_1 = start.enter_context(tc.tile_pool(name="cpool_1", bufs=1, side="right", reuse_waits="tile"))
                accp_1 = start.enter_context(tc.tile_pool(name="accp_1", bufs=NPOS - len(ROUNDS[2]) * BC, side="right"))
                setp = start.enter_context(tc.tile_pool(name="setp", bufs=2, side="right", reuse_waits="tile"))
                sets = {}
                copies = {}
                sums = {}
                groups = {}
                conv = {}
                todo = []
                clock = [0]
                xqf_v = xqf[:].rearrange("p (r z) -> p r z", z=PITCH)
                xsf_v = xsf[:].rearrange("p (r z) -> p r z", z=PITCH)

                def f_set(ip, kind, bufs):
                    words = setp.tile([P, JC * P], I32, name=kind + "_words", bufs=bufs, align_bytes=64)
                    scales = setp.tile([P, JC * P], U8, name=kind + "_scales", bufs=bufs, align_bytes=64)
                    for u in range(JC // BC):
                        for dst, src in ((words, xqf_v), (scales, xsf_v)):
                            nc.vector.tensor_copy(
                                out=dst[:, BC * P * u : BC * P * (u + 1)].rearrange("p (b a w) -> p b a w", b=BC, a=BA),
                                in_=src[:, ip : ip + BR * (BA - 1) + 1 : BR, 0 : BC * BI].rearrange(
                                    "p a (b i) -> p b a i", b=BC
                                )[:, :, :, u : u + BW],
                            )
                    sets[(kind, ip)] = (words, scales)

                def f_message(kind, ip, jp, pool, tag):
                    words, scales = sets[(kind, ip)]
                    return mx_message(words[:, jp * P : (jp + 1) * P], scales[:, jp * P : (jp + 1) * P], pool, tag)

                def f_weight(i, j, ip, jp):
                    return aff_f[:, ip - i, jp - j, i, j : j + 1]

                def f_mul(i, ip):
                    return i <= ip <= i + 2 * PAD and ip in MUL_ROWS and i not in VEC_TOO.get(ip, ())

                def f_columns(jp):
                    return range(max(0, jp - 2 * PAD), min(BC - 1, jp) + 1)

                def f_vector(mine, ip, jp):
                    msg = f_message("vec", ip, jp, ps_msg, "msg")
                    for i in mine:
                        for j in f_columns(jp):
                            first = (i, j) not in sums
                            if first:
                                sums[(i, j)] = (accp if i in ROUNDS[2] else accp_1).tile([P, C], F32, name="acc")
                            vector_term(sums[(i, j)], first, msg, f_weight(i, j, ip, jp))

                def f_copy(ip, jp):
                    msg = f_message("mul", ip, jp, ps_pos, "pos")
                    pool = cpool if any([f_mul(i, ip) for i in ROUNDS[2]]) else cpool_1
                    copies[(ip, jp)] = pool.tile([P, C], F32, name="cp%d_%d" % (ip, jp))
                    nc.scalar.copy(out=copies[(ip, jp)][:], in_=msg[:])

                def f_position(i, j):
                    terms = [(ip, j + dw) for ip in MUL_ROWS if f_mul(i, ip) for dw in range(KW)]
                    st = {}

                    def term(k, ip, jp):
                        clock[0] += 1
                        if todo and todo[0][0] <= clock[0] and k % 2 == 1:
                            todo.pop(0)[1]()
                        if k == 0:
                            st["pos"] = ps_pos.tile([P, T, P], F32, name="pos")
                        add_transposed(st["pos"], product(prodp, copies[(ip, jp)], f_weight(i, j, ip, jp)), k == 0, False)

                    def close():
                        add_transposed(st["pos"], sums.pop((i, j)), False, True)

                    def unload():
                        if j == 0:
                            groups[i] = st2.tile([P, ROWPX, T], BF16, name="grp", align_bytes=64)
                        nc.scalar.copy(
                            out=groups[i][:].rearrange("p (k b) t -> p b k t", b=BC)[:, j],
                            in_=st["pos"][:].rearrange("p t k -> p k t"),
                        )
                        if j == BC - 1:
                            todo.extend([(clock[0] + CONV_LATE, f) for f in f_conv(i)])

                    return [partial(term, k, ip, jp) for k, (ip, jp) in enumerate(terms)], close, unload

                def f_image(i):
                    return slice(HE + i, HE + i + BR * (BA - 1) + 1, BR)

                def f_conv_in(i):
                    x_res = st2.tile([P, T, ROWPX], BF16, name="x_res", bufs=1)
                    for t in range(T):
                        nc.sync.dma_start(
                            out=x_res[:, t, :].rearrange("p (a w) -> p a w", w=W), in_=x_r[:, t, f_image(i), :]
                        )
                    aq = st2.tile([P, ROWPX], I32, name="aq", bufs=1, align_bytes=64)
                    asc = st2.tile([P, ROWPX], U8, name="asc", bufs=1, align_bytes=64)
                    flat = groups.pop(i)[:].rearrange("p k t -> p (k t)")
                    for c0, c1 in ((0, 256), (256, ROWPX)):
                        nc.vector.quantize_mx(
                            out=aq[:, c0:c1].bitcast(FP8X4), scales=asc[:, c0:c1], in_=flat[:, T * c0 : T * c1]
                        )
                    conv[i] = (x_res, aq, asc)

                def f_conv_out(i, m):
                    x_res, aq, asc = conv[i]
                    o_ps = ps_msg.tile([P, ROWPX], F32, name="o_ps", tag="msg")
                    for c0, c1 in ((0, 256), (256, ROWPX)):
                        second_conv(aq, asc, c0, c1, m, o_ps[:, c0:c1])
                    o_sb = st2.tile([P, ROWPX], F32, name="o_sb", bufs=1)
                    nc.vector.tensor_tensor(out=o_sb[:], in0=o_ps[:], in1=x_res[:, m, :], op=ALU.add)
                    nc.sync.dma_start(
                        out=out_v[m, :, f_image(i), :], in_=o_sb[:].rearrange("p (a w) -> p a w", w=W)
                    )

                def f_conv(i):
                    return [partial(f_conv_in, i)] + [partial(f_conv_out, i, m) for m in range(T)]

                pairs = {}

                def e_products(o):
                    pr = dpool.tile([P, CP, 2, NQ], F32, name="pr")
                    nu = dpool.tile([P, 2, NQ], F32, name="nu")
                    for n in range(2):
                        dh, dw = divmod(min(o + n, KW * KW - 1), KW)
                        nc.gpsimd.tensor_tensor(
                            out=pr[:, :, n].rearrange("p c (y x) -> p c y x", x=TW),
                            in0=p_e[:, :, dh : dh + HALF, dw : dw + TW],
                            in1=p_e[:, :, PAD : PAD + HALF, PAD : PAD + TW],
                            op=ALU.mult,
                        )
                        nc.scalar.copy(
                            out=nu[:, n].rearrange("p (y x) -> p y x", x=TW), in_=nh[:, dh : dh + HALF, dw : dw + TW]
                        )
                    pairs[o] = (pr, nu)

                def e_sum(o):
                    pr, nu = pairs.pop(o)
                    pairs[o] = ps_misc.tile([P, P], F32, name="ps_d", tag="misc")
                    for c in range(CP + 2):
                        src = pr[:, c] if c < CP else (nu if c == CP else nv)[:]
                        nc.tensor.matmul(
                            out=pairs[o][:],
                            lhsT=src.rearrange("p n q -> p (n q)"),
                            rhs=ident_f[:],
                            is_transpose=True,
                            start=(c == 0),
                            stop=(c == CP + 1),
                        )

                def e_out(o):
                    ps = pairs.pop(o)
                    pairs[o] = dpool.tile([P, P], F32, name="turned")
                    nc.scalar.copy(out=pairs[o][:], in_=ps[:])

                def e_back(o):
                    src = pairs.pop(o)
                    pairs[o] = ps_misc.tile([P, P], F32, name="ps_d", tag="misc")
                    nc.tensor.transpose(pairs[o][:], src[:], ident_f[:])

                def e_exp(o):
                    n = min(2, KW * KW - o)
                    nc.scalar.activation(
                        out=aff_e[:].rearrange("p a b y x -> p (a b y x)")[:, NQ * o : NQ * (o + n)],
                        in_=pairs.pop(o)[:, 0 : NQ * n],
                        func=ACT.Exp,
                        scale=twoinv[:, 0:1],
                    )

                distances = []
                for o in range(0, KW * KW + 8, 2):
                    for step, f in ((4, e_exp), (2, e_out), (1, e_sum), (3, e_back), (0, e_products)):
                        if 0 <= o - 2 * step < KW * KW:
                            distances.append(partial(f, o - 2 * step))
                distances.append(partial(finish_affinity, st2, aff_e, NQ))

                v_rows = []
                for rnd in ROUNDS:
                    for ip in range(IR - 1, -1, -1):
                        mine = [i for i in rnd if i <= ip <= i + 2 * PAD and not f_mul(i, ip)]
                        if mine:
                            v_rows.append((rnd, ip, mine))
                vec = [(3, 0, partial(f_set, v_rows[0][1], "vec", 2)), (1, 0, partial(f_set, MUL_ROWS[0], "mul", 1))]
                vec_ends = {}
                for n, (rnd, ip, mine) in enumerate(v_rows):
                    if n + 1 < len(v_rows):
                        vec.append((3, 0, partial(f_set, v_rows[n + 1][1], "vec", 2)))
                    for jp in range(JC):
                        vec.append((len(mine) * len(f_columns(jp)), 0, partial(f_vector, mine, ip, jp)))
                    vec_ends[rnd] = len(vec)
                mul = []
                for n, ip in enumerate(MUL_ROWS):
                    mul += [(1, 2, partial(f_copy, ip, jp)) for jp in range(JC)]
                    if n + 1 < len(MUL_ROWS):
                        mul.append((1, 0, partial(f_set, MUL_ROWS[n + 1], "mul", 1)))

                def f_round(rnd):
                    spots = []
                    for i in rnd:
                        for j in range(BC):
                            terms, close, unload = f_position(i, j)
                            spots.append((plain(terms), (1, vec_ends[rnd], close), (0, 0, unload)))
                    return spots

                mul += late(f_round(ROUNDS[0]) + f_round(ROUNDS[1]))
                dis = [(0.3, 0, f) for f in tile_jobs + [e_lengths]] + plain(distances)
                dis.append((len(distances) * (1 / DIST_PART - 1), 0, lambda: None))
                interleave([vec, mul, dis], (AHEAD, 0, 0))

            own_pixels = ctx.enter_context(ExitStack())
            xep = ctx.enter_context(tc.tile_pool(name="xep", bufs=1, side="right", reuse_waits="tile"))
            xqe = xep.tile([P, 6 * CHPX], I32, name="xqe", align_bytes=64)
            xse = xep.tile([P, 6 * CHPX], U8, name="xse", align_bytes=64)
            xqe_v = xqe[:].rearrange("p (r z) -> p r z", z=PITCH)
            xse_v = xse[:].rearrange("p (r z) -> p r z", z=PITCH)
            matp = own_pixels.enter_context(tc.tile_pool(name="matp", bufs=1, side="right", reuse_waits="tile"))
            mat = matp.tile([P, NTS, 2, NQ], F32, name="mat")
            nc.gpsimd.memset(mat[LOW:P, NT:NTS, 0, :], 0.0)
            nc.gpsimd.memset(mat[0:LOW, NT:NTS, 1, :], 0.0)
            mat_rows = {}

            def spread_row(y, kind):
                m = matp.tile([P, 64 + TW * P + 160], F32, name="rowmat", bufs=ROWMATS)
                nc.gpsimd.memset(m[:], 0.0)
                for dh in range(PAD - y, KW):
                    r = y + dh - PAD
                    if kind == 0:
                        parts = ((0, LOW, TW * r), (LOW, P, TW * (TH - 1 - r)))
                    else:
                        parts = ((LOW // 2, LOW, NQ + TW * r),) if r < HALF else ()
                    for lo, hi, u in parts:
                        s = 64 + u - PAD
                        dst = m[lo:hi, s : s + TW * (P + 1)].rearrange("p (x e) -> p x e", e=P + 1)[:, :, 0:KW]
                        nc.scalar.copy(out=dst, in_=aff_e[lo:hi, dh, :, y, :].rearrange("p d x -> p x d"))
                for x in range(PAD):
                    left_px = m[:, 64 + x * P : 64 + (x + 1) * P].rearrange("p (r z) -> p r z", z=TW)
                    nc.gpsimd.memset(left_px[:, :, TW - PAD + x : TW], 0.0)
                    right_px = m[:, 64 + (TW - 1 - x) * P : 64 + (TW - x) * P].rearrange("p (r z) -> p r z", z=TW)
                    nc.gpsimd.memset(right_px[:, :, 0 : PAD - x], 0.0)
                mat_rows[(y, kind)] = m

            def turn(y, kind, g):
                ps = ps_misc.tile([P, 4, P], F32, name="ps_m", tag="misc")
                for k in range(4):
                    a = 64 + (4 * g + k) * P
                    nc.tensor.transpose(ps[:, k, :], mat_rows[(y, kind)][:, a : a + P], ident_f[:])
                q = slice(TW * y + 4 * g, TW * y + 4 * g + 4)
                src = ps[:].rearrange("p q h -> p h q")
                if kind == 0:
                    for half in range(2):
                        nc.scalar.copy(out=mat[:, 0:NT, half, q], in_=src[:, LOW * half : LOW * half + NT])
                    nc.scalar.copy(out=mat[0:LOW, NT:NTS, 0, q], in_=src[0:LOW, NT : NT + NS])
                else:
                    nc.scalar.copy(out=mat[LOW:P, NT:NTS, 1, q], in_=src[LOW:P, NT + NS : NT + 2 * NS])

            mats = []
            for y in range(HALF):
                for kind in range(2):
                    mats += [partial(spread_row, y, kind)] + [partial(turn, y, kind, g) for g in range(TW // 4)]
            with tc.tile_pool(name="pack", bufs=1, side="right", reuse_waits="tile") as pack:
                stage = pack.tile([P, CHPX, T], BF16, name="stage", align_bytes=64)
                rows = stage[:].rearrange("p (r z) t -> p r z t", z=PITCH)
                nc.vector.memset(rows[:, :, 0:PAD, :], 0.0)
                nc.vector.memset(rows[:, :, PAD + W : PITCH, :], 0.0)
                nc.vector.memset(rows[:, 0:PAD, :, :], 0.0)
                packs = []
                for k in range(5):
                    packs += pack_steps(pack, stage, k * CH - PAD, HE + PAD, xqe, xse, k * CHPX, False, False)
                packs += pack_steps(pack, stage, S_ROW0, H, xqe, xse, 5 * CHPX, False, True)
                last = [(size, 0, f) for size, need, f in late(f_round(ROUNDS[2]))]
                interleave([plain(packs), last, plain(mats)])
            run([f for n, f in todo])

        with ExitStack() as upper:
            evp = upper.enter_context(tc.tile_pool(name="evp", bufs=1, reuse_waits="tile"))
            vset = upper.enter_context(tc.tile_pool(name="vset", bufs=1, reuse_waits="tile"))
            ring = []
            free = []
            ready = []
            e_acc = {}
            e_own = {}
            loaded = []
            row_sets = {}
            side_sets = {}
            e_copies = {}

            def add_ring(pool, n, eng):
                for k in range(len(ring), len(ring) + n):
                    ring.append(pool.tile([P, C], F32, name="ring%d" % k))
                    eng.memset(ring[k][:], 0.0)
                    free.append(k)

            add_ring(evp, RINGS[0], nc.gpsimd)

            places = {}
            for kind, width, n in (("row", KB, 5), ("side", PAD, 2)):
                places[kind] = []
                for k in range(n):
                    words = vset.tile([P, width, P], I32, name="%s_words%d" % (kind, k), align_bytes=64)
                    scales = vset.tile([P, width, P], U8, name="%s_scales%d" % (kind, k), align_bytes=64)
                    nc.gpsimd.memset(words[:], 0)
                    nc.gpsimd.memset(scales[:], 0)
                    places[kind].append((words, scales))

            def e_set(r, k0, k1, kind):
                n = k1 - k0
                words, scales = places[kind].pop(0)
                places[kind].append((words, scales))
                base = 0 if k1 <= TW else 8
                cols = slice(k0 - base, k1 - base)
                for dst, src in ((words, xqe_v), (scales, xse_v)):
                    for half in range(2):
                        s0 = r + PAD if half == 0 else TH - 1 - r + PAD
                        nc.vector.tensor_copy(
                            out=dst[:, 0:n, LOW * half : LOW * half + NT].rearrange("p k (r c) -> p k r c", c=TC),
                            in_=src[:, s0 : s0 + TH * (TR - 1) + 1 : TH, base : base + W].rearrange(
                                "p r (c x) -> p x r c", x=TW
                            )[:, cols],
                        )
                    nc.vector.tensor_copy(
                        out=dst[:, 0:n, NT : NT + 2 * NS].rearrange("p k (h a) -> p k h a", h=2),
                        in_=src[:, S_BASE + S_ROW - S_ROW0 + r, base : base + W].rearrange(
                            "p (a h x) -> p x h a", h=2, x=TW
                        )[:, cols],
                    )
                return [(words[:, k], scales[:, k]) for k in range(n)]

            def e_weight(y, x, r, k):
                return aff_e[:, r - y + PAD, k - x, y, x : x + 1]

            def e_columns(k):
                return range(max(0, k - 2 * PAD), min(TW - 1, k) + 1)

            def e_vector_term(y, x, r, k, msg):
                if (y, x) not in e_acc and ready:
                    load_own(y, x)
                first = (y, x) not in e_acc
                if first:
                    e_acc[(y, x)] = free.pop(0)
                vector_term(ring[e_acc[(y, x)]], first, msg, e_weight(y, x, r, k))

            def load_own(y, x):
                if not 0 <= x < TW or (y, x) in loaded or not ready:
                    return
                loaded.append((y, x))
                where = e_own if (y, x) in e_acc else e_acc
                where[(y, x)] = free.pop(0)
                dst = ring[where[(y, x)]]
                for half in range(2):
                    v = NQ * half + TW * y + x
                    for p0, n, src in ((LOW * half, NT, park), (NT + NS * half, NS, park_s)):
                        nc.sync.dma_start(
                            out=dst[p0 : p0 + n, :].rearrange("p (e f) -> p e f", e=T),
                            in_=src[:, v, :, :].rearrange("e n f -> n e f"),
                        )

            def side_set(r, k0):
                side_sets[(r, k0)] = e_set(r, k0, k0 + PAD, "side")

            def side_message(ys, r, k0, k):
                msg = mx_message(*side_sets[(r, k0)][k - k0], ps_msg, "msg")
                for y in range(max(ys[0], r - PAD), min(ys[-1], r + PAD) + 1):
                    for x in e_columns(k):
                        e_vector_term(y, x, r, k, msg)

            def side_jobs(ys, k0):
                jobs = []
                rows = range(max(0, ys[0] - PAD), ys[-1] + PAD + 1)
                for r in rows:
                    if r == rows[0]:
                        jobs.append((2, 0, partial(side_set, r, k0)))
                    if r + 1 in rows:
                        jobs.append((2, 0, partial(side_set, r + 1, k0)))
                    for k in range(k0, k0 + PAD):
                        n = (min(ys[-1], r + PAD) - max(ys[0], r - PAD) + 1) * len(e_columns(k))
                        jobs.append((n, 0, partial(side_message, ys, r, k0, k)))
                return jobs

            def row_set(r, k0):
                for k, ws in enumerate(e_set(r, k0, min(k0 + KB, VC), "row")):
                    row_sets[(r, k0 + k)] = ws

            def far_message(r, k):
                msg = mx_message(*row_sets.pop((r, k)), ps_msg, "msg")
                for y in range(r + PAD + 1):
                    for x in e_columns(k):
                        e_vector_term(y, x, r, k, msg)

            def near_message(k):
                e_copies[(-1, k)] = mx_message(*row_sets.pop((-1, k)), ps_misc, "misc")
                if not ready:
                    near_copy(k)
                    copied.append(k)

            copied = []

            def near_copy(k):
                if k in copied:
                    return
                msg = e_copies[(-1, k)]
                e_copies[(-1, k)] = cpe.tile([P, C], F32, name="cp", bufs=8)
                nc.scalar.copy(out=e_copies[(-1, k)][:], in_=msg[:])

            def column(k):
                jobs = []
                if k == 0:
                    jobs += [(2, 0, partial(row_set, r, 0)) for r in (-3, -2, -1)]
                nxt = k // KB * KB + KB
                if nxt < VC and k % KB == KB - 2:
                    jobs += [(2, 0, partial(row_set, r, nxt)) for r in (-3, -2)]
                jobs += [(0, 0, partial(load_own, y, k + PRE)) for y in range(2)]
                jobs += [(0, 0, partial(load_own, y, k - 2 * PAD)) for y in range(2, HALF)]
                n = len(e_columns(k))
                jobs += [
                    (2 * n, 0, partial(far_message, -2, k)),
                    (1, 0, partial(near_message, k)),
                    (n, 0, partial(far_message, -3, k)),
                    (1, 0, partial(near_copy, k)),
                ]
                if nxt < VC and k % KB == KB - 1:
                    jobs.append((2, 0, partial(row_set, -1, nxt)))
                return jobs

            def e_position(y, x):
                terms = [x + dw for dw in range(KW)] if y < PAD else []
                st = {}

                def start():
                    load_own(y, x)
                    st["pos"] = ps_pos.tile([P, T, P], F32, name="pos")

                def term(n, k):
                    add_transposed(st["pos"], product(e_prodp, e_copies[(-1, k)], e_weight(y, x, -1, k)), n == 0, False)

                def close():
                    rest = [d.pop((y, x)) for d in (e_own, e_acc) if (y, x) in d]
                    for n, k in enumerate(rest):
                        add_transposed(st["pos"], ring[k], not terms and n == 0, n == len(rest) - 1)
                        free.append(k)

                def unload():
                    for half in range(2):
                        r = y if half == 0 else TH - 1 - y
                        nc.scalar.copy(
                            out=groups_t[:, :, r, :, x, :],
                            in_=st["pos"][:, :, LOW * half : LOW * half + NT].rearrange("p t (a c) -> p a c t", c=TC),
                        )
                    nc.scalar.copy(
                        out=groups_s[:, y, :, :, x, :].rearrange("p a h t -> p h a t"),
                        in_=st["pos"][:, :, NT : NT + 2 * NS].rearrange("p t (h a) -> p h a t", h=2),
                    )

                return [start] + [partial(term, n, k) for n, k in enumerate(terms)], close, unload

            e_prodp = upper.enter_context(tc.tile_pool(name="e_prodp", bufs=6, reuse_waits="tile"))
            cpe = upper.enter_context(tc.tile_pool(name="cpe", bufs=1, reuse_waits="tile"))
            add_ring(cpe, RINGS[1], nc.gpsimd)

            with own_pixels:
                dense = own_pixels.enter_context(tc.tile_pool(name="dense", bufs=1, side="right", reuse_waits="tile"))
                own = {}
                own_m = {}
                own_o = {}

                def own_set(g):
                    words = dense.tile([P, TC, P], I32, name="own_w", bufs=2, align_bytes=64)
                    scales = dense.tile([P, TC, P], U8, name="own_s", bufs=2, align_bytes=64)
                    for dst, src in ((words, xqe_v), (scales, xse_v)):
                        if g < TR:
                            nc.vector.tensor_copy(
                                out=dst[:].rearrange("p c (r x) -> p c r x", x=TW),
                                in_=src[:, TH * g + PAD : TH * g + PAD + TH, PAD : PAD + W].rearrange(
                                    "p r (c x) -> p c r x", x=TW
                                ),
                            )
                            continue
                        for h in range(2):
                            s0 = S_BASE + S_ROW - S_ROW0
                            nc.vector.tensor_copy(
                                out=dst[:, 0:NS, NQ * h : NQ * (h + 1)].rearrange("p a (r x) -> p a r x", x=TW),
                                in_=src[:, s0 : s0 + HALF, PAD : PAD + W].rearrange(
                                    "p r (a h x) -> p h a r x", h=2, x=TW
                                )[:, h],
                            )
                    own[g] = (words, scales)

                def own_message(n):
                    words, scales = own[n // TC]
                    msg = mx_message(words[:, n % TC], scales[:, n % TC], ps_pos, "pos")
                    own_m[n] = dense.tile([P, C], F32, name="own_m", bufs=3)
                    nc.scalar.copy(out=own_m[n][:], in_=msg[:])

                def own_sum(n):
                    ps = ps_misc.tile([P, C], F32, name="own_ps", tag="misc")
                    nc.tensor.matmul(
                        out=ps[:],
                        lhsT=mat[:, n].rearrange("p h q -> p (h q)"),
                        rhs=own_m.pop(n)[:],
                        start=True,
                        stop=True,
                    )
                    if n % 3 == 0:
                        own_o[0] = dense.tile([P, T, 3, P], F32, name="own_o", bufs=2)
                    nc.scalar.copy(out=own_o[0][:, :, n % 3, :], in_=ps[:].rearrange("p (e f) -> p e f", e=T))
                    if n % 3 == 2:
                        dst = park[:, :, n - 2 : n + 1, :] if n < NT else park_s
                        nc.sync.dma_start(out=dst.rearrange("e v n f -> v e n f"), in_=own_o[0][:])

                owns = [partial(own_set, 0)]
                for n in range(NTS + 2):
                    if n < NT and n % TC == 0:
                        owns.append(partial(own_set, n // TC + 1))
                    if n < NTS:
                        owns.append(partial(own_message, n))
                    if n >= 2:
                        owns.append(partial(own_sum, n - 2))
                vec = side_jobs(range(HALF), 0)
                for k in range(FIRST):
                    vec += column(k)
                interleave([vec, plain(owns)])

            gpool = ctx.enter_context(tc.tile_pool(name="gpool", bufs=1, side="right", reuse_waits="tile"))
            grp = gpool.tile([P, (HE + HALF) * W, T], BF16, name="grp", align_bytes=64)
            groups_t = grp[:, 0 : HE * W].rearrange("p (a r c x) t -> p a r c x t", r=TH, c=TC, x=TW)
            groups_s = grp[:, HE * W : (HE + HALF) * W].rearrange("p (r a h x) t -> p r a h x t", a=NS, h=2, x=TW)
            add_ring(gpool, RINGS[2], nc.gpsimd)
            ready.append(True)
            right = [(k0, k1, ys, side_jobs(ys, VC - PAD)) for k0, k1, ys in RIGHT]
            spots = []
            ends = [0]
            resting = []
            for x in range(TW + 1):
                spots_x = [e_position(y, x) for y in range(HALF)] if x < TW else []
                spots += [(plain(a), (1, 0, b), (0, 0, f)) for a, b, f in spots_x[0:PAD] + resting]
                resting = spots_x[PAD:]
                ends.append(sum([len(e[0]) + 2 for e in spots]) - 3)
            spots = late(spots)
            for k in range(FIRST, VC + 2):
                vec = column(k) if k < VC else []
                sides = []
                for k0, k1, ys, jobs in right:
                    if k0 - PAD <= k < k0:
                        vec += [(0, 0, partial(load_own, y, TW + k - k0)) for y in ys]
                    if k0 <= k < k1:
                        sides += jobs[len(jobs) * (k - k0) // (k1 - k0) : len(jobs) * (k - k0 + 1) // (k1 - k0)]
                x = k - 2 * PAD - 1
                mul = spots[ends[x] : ends[x + 1]] if 0 <= x < TW else spots[ends[TW] :] if x == TW else []
                interleave([vec, sides, mul])

        with tc.tile_pool(name="tail", bufs=2, side="right", reuse_waits="tile") as tail:
            NPX = TH * W
            bands = [(TH * n, TH) for n in range(TR)] + [(S_ROW, HALF)]
            banks = ((ps_misc, "misc"), (ps_pos, "pos"), (ps_msg, "msg"), (ps_pos, "pos"), (ps_msg, "msg"))
            turn_no = [0]
            res = {}
            args = {}

            def t_load(n):
                r0, nr = bands[n]
                res[n] = tail.tile([P, T, NPX], BF16, name="x_res", bufs=4)
                nc.sync.dma_start(
                    out=res[n][:, :, 0 : nr * W].rearrange("p t (h w) -> p t h w", w=W), in_=x_r[:, :, r0 : r0 + nr, :]
                )

            def t_cuts(n):
                px = bands[n][1] * W
                return ((0, px * 2 // 3), (px * 2 // 3, px))

            def t_quant(n):
                aq = tail.tile([P, NPX], I32, name="aq", align_bytes=64)
                asc = tail.tile([P, NPX], U8, name="asc", align_bytes=64)
                flat = grp[:, n * NPX : n * NPX + bands[n][1] * W, :].rearrange("p u t -> p (u t)")
                for c0, c1 in t_cuts(n):
                    nc.vector.quantize_mx(
                        out=aq[:, c0:c1].bitcast(FP8X4), scales=asc[:, c0:c1], in_=flat[:, T * c0 : T * c1]
                    )
                args[n] = (aq, asc)

            def t_out(n, m):
                r0, nr = bands[n]
                o_sb = tail.tile([P, NPX], F32, name="o_sb", bufs=6)
                for c0, c1 in t_cuts(n):
                    pool, tag = banks[turn_no[0] % len(banks)]
                    turn_no[0] += 1
                    o_ps = pool.tile([P, c1 - c0], F32, name="o_ps", tag=tag)
                    second_conv(*args[n], c0, c1, m, o_ps[:])
                    if m == T - 1:
                        nc.scalar.copy(out=o_sb[:, c0:c1], in_=o_ps[:])
                        nc.gpsimd.tensor_tensor(
                            out=o_sb[:, c0:c1], in0=o_sb[:, c0:c1], in1=res[n][:, m, c0:c1], op=ALU.add
                        )
                    else:
                        nc.vector.tensor_tensor(out=o_sb[:, c0:c1], in0=o_ps[:], in1=res[n][:, m, c0:c1], op=ALU.add)
                nc.sync.dma_start(
                    out=out_v[m, :, r0 : r0 + nr, :], in_=o_sb[:, 0 : nr * W].rearrange("p (h w) -> p h w", w=W)
                )

            run([partial(t_load, n) for n in range(3)] + [partial(t_quant, 0)])
            for n in range(len(bands)):
                for m in range(T):
                    if m == 0 and n + 3 < len(bands):
                        t_load(n + 3)
                    if m == 1 and n + 1 < len(bands):
                        t_quant(n + 1)
                    t_out(n, m)
